import numpy as np
import ml_dtypes


def mxq(x, axis, fmt="e4m3"):
    dtype, down = {"e4m3": (ml_dtypes.float8_e4m3fn, 7), "e5m2": (ml_dtypes.float8_e5m2, 14)}[fmt]
    v = np.moveaxis(np.asarray(x, np.float32).astype(ml_dtypes.bfloat16).astype(np.float64), axis, -1)
    blocks = v.reshape(v.shape[:-1] + (-1, 32))
    amax = np.abs(blocks).max(-1, keepdims=True)
    byte = np.maximum(np.where(amax > 0, np.frexp(amax)[1] - 1 + 127, 0) - down, 1)
    scale = np.exp2(byte - 127.0)
    codes = (blocks / scale).astype(np.float32).astype(dtype).astype(np.float64)
    return np.moveaxis((codes * scale).reshape(v.shape), -1, axis)


WIDE = False


def mx_kscale(k):
    if not WIDE:
        return np.ones(k)
    levels = np.array([10, -10, 5, -5, 0])
    if k % 512:
        return np.exp2(np.random.permutation(np.resize(levels, k // 32))).repeat(32)
    a = np.empty((k // 512, 16))
    for p in range(k // 512):
        a[p, :8] = np.random.permutation(np.resize(levels, 8))
        for g in range(8):
            far = levels[np.abs(levels - a[p, g]) >= 10]
            a[p, g + 8] = far[np.random.randint(len(far))]
    return np.exp2(a.ravel()).repeat(32)


BF16 = ml_dtypes.bfloat16


def bf(x):
    return np.asarray(x, np.float32).astype(BF16)


def f64(x):
    return np.asarray(x).astype(np.float64)


B, S, D, QC, KVC, FF = 1, 512, 1024, 8, 2, 4096
EPS = 1e-5


def rmsnorm(u, w):
    return u / np.sqrt(np.square(u).mean(-1, keepdims=True) + EPS) * w


def draw0():
    s = mx_kscale(D)
    t = np.exp2(np.round(np.log2(mx_kscale(FF)) / 2))
    return {"h_attn": bf(np.random.standard_normal((B, S, D)) * 1.3),
            "norm2_w": bf((1.0 + 0.1 * np.random.standard_normal(D)) * s),
            "ffn_wk": bf(np.random.standard_normal((D, FF)) / np.sqrt(D) / s[:, None] * t),
            "ffn_wv": bf(np.random.standard_normal((FF, D)) / np.sqrt(FF) / (t * t)[:, None])}


def core(h_attn, norm2_w, ffn_wk, ffn_wv):
    h = f64(h_attn)
    hn = rmsnorm(h, f64(norm2_w))
    k = np.square(np.maximum(mxq(hn, 2, "e4m3") @ mxq(f64(ffn_wk), 0, "e4m3"), 0.0))
    return h + (mxq(k, 2, "e4m3") @ mxq(f64(ffn_wv), 0, "e4m3"))


def e4m3fn_bytes(y):
    return np.clip(np.asarray(y, np.float64), -448.0, 448.0).astype(np.float32).astype(ml_dtypes.float8_e4m3fn).view(np.uint8)


def e4m3fn_values(b):
    return np.asarray(b, np.uint8).view(ml_dtypes.float8_e4m3fn).astype(np.float64)


def setup_inputs():
    d = draw0()
    x0 = np.asarray(d['ffn_wv']).astype(np.float64)
    s = (np.max(np.abs(x0), axis=(1,), keepdims=True) / 448.0).astype(np.float32)
    out = {}
    for k, v in d.items():
        if k == 'ffn_wv':
            out['ffn_wv_bytes'] = e4m3fn_bytes(x0 / s.astype(np.float64))
            out['ffn_wv_scale'] = s
        else:
            out[k] = v
    return out


def reference(h_attn, norm2_w, ffn_wk, ffn_wv_bytes, ffn_wv_scale):
    return core(h_attn, norm2_w, ffn_wk, e4m3fn_values(ffn_wv_bytes) * ffn_wv_scale.astype(np.float64))

@@ -1,0 +1,336 @@
+from contextlib import ExitStack
+
+import concourse.mybir as mybir
+from concourse.masks import make_identity
+
+S, D, FF = 512, 1024, 4096
+EPS = 1e-5
+FLOPS = 2 * 2 * S * D * FF
+
+F32 = mybir.dt.float32
+BF16 = mybir.dt.bfloat16
+U32 = mybir.dt.uint32
+U8 = mybir.dt.uint8
+FP8 = mybir.dt.float8_e4m3fn
+FP8X4 = mybir.dt.float8_e4m3fn_x4
+ALU = mybir.AluOpType
+ACT = mybir.ActivationFunctionType
+
+P = 128
+PACK = 4
+K_PASS = P * PACK
+NT = S // P
+G = FF // K_PASS
+Q = D // K_PASS
+
+SLICES = ((0, 512), (512, 256), (768, 256))
+UNITS = [(g, 0, 512) for g in range(G)] + [(g, 512, 512) for g in range(G - 1)] + [(G - 1, 512, 256), (G - 1, 768, 256)]
+V_WIDENS = range(4, 11)
+PE_GROUPS = range(1, G)
+EARLY = 3
+
+
+def tile_block_pc_kernel(tc, h_attn, norm2_w, ffn_wk, ffn_wv_bytes, ffn_wv_scale, out):
+    nc = tc.nc
+    h_v = h_attn.rearrange("b (i p) d -> (b i) p d", p=P)
+    out_v = out.rearrange("b (i p) d -> (b i) p d", p=P)
+    wk_v = ffn_wk.rearrange("(q p j) (g c) -> g q p j c", q=Q, p=P, j=PACK, c=K_PASS)
+    wv_v = ffn_wv_bytes.rearrange("(g p t) n -> g p t n", p=P, t=PACK)
+    scale_v = ffn_wv_scale.rearrange("(g p t) o -> p g (t o)", p=P, t=PACK)
+
+    with ExitStack() as ctx:
+        keep = ctx.enter_context(tc.tile_pool(name="keep", bufs=1))
+        stage2 = ctx.enter_context(tc.tile_pool(name="stage2", bufs=2))
+        stage3 = ctx.enter_context(tc.tile_pool(name="stage3", bufs=3))
+        stage4 = ctx.enter_context(tc.tile_pool(name="stage4", bufs=4))
+        stage8 = ctx.enter_context(tc.tile_pool(name="stage8", bufs=8))
+        psum4 = ctx.enter_context(tc.psum_pool(name="psum4", bufs=4))
+        psum2 = ctx.enter_context(tc.psum_pool(name="psum2", bufs=2))
+
+        h_sb = keep.tile([P, NT, D], BF16, align_bytes=64, name="h_sb")
+        h_codes = keep.tile([P, NT, Q, P], U32, align_bytes=64, name="h_codes")
+        h_scales = keep.tile([P, NT, Q, P], U8, align_bytes=64, name="h_scales")
+        wv_bytes = keep.tile([P, G, PACK, D], U8, align_bytes=64, name="wv_bytes")
+        wv_scale = keep.tile([P, G, PACK], F32, align_bytes=64, name="wv_scale")
+        wv_codes = keep.tile([P, G, D], U32, align_bytes=64, name="wv_codes")
+        wv_scales = keep.tile([P, G, D], U8, align_bytes=64, name="wv_scales")
+        k_codes = keep.tile([P, G, S], U32, align_bytes=64, name="k_codes")
+        k_scales = keep.tile([P, G, S], U8, align_bytes=64, name="k_scales")
+        gain_row = keep.tile([P, D], BF16, align_bytes=64, name="gain_row")
+        ones = keep.tile([P, P], BF16, align_bytes=64, name="ones")
+        ident_bf16 = keep.tile([P, P], BF16, align_bytes=64, name="ident_bf16")
+        ident_f32 = keep.tile([P, P], F32, align_bytes=64, name="ident_f32")
+        unused = keep.tile([P, D], BF16, align_bytes=64, name="unused")
+        sumsq = keep.tile([P, NT], F32, align_bytes=64, name="sumsq")
+        rms = keep.tile([P, NT], F32, align_bytes=64, name="rms")
+        rstd = keep.tile([P, NT], F32, align_bytes=64, name="rstd")
+
+        nc.vector.memset(gain_row[:], 0.0)
+        nc.vector.memset(ones[:], 1.0)
+        make_identity(nc, ident_f32[:])
+        make_identity(nc, ident_bf16[:])
+
+        wk_raw = {}
+
+        def load_wk(g, q, parts=1):
+            if q == 0:
+                wk_raw[g] = stage3.tile([P, Q, PACK, K_PASS], BF16, align_bytes=64, name="wk_raw")
+            w = K_PASS // parts
+            for a in range(parts):
+                cols = slice(a * w, (a + 1) * w)
+                nc.sync.dma_start(out=wk_raw[g][:, q, :, cols], in_=wk_v[g, q][:, :, cols])
+
+        def load_wv(g):
+            nc.sync.dma_start(out=wv_bytes[:, g, :, :], in_=wv_v[g])
+
+        def load_h(i):
+            nc.sync.dma_start(out=h_sb[:, i, :], in_=h_v[i])
+
+        load_h(0)
+        load_wk(0, 0, 2)
+        load_h(1)
+        nc.sync.dma_start(out=gain_row[0:1, :], in_=norm2_w.rearrange("(o d) -> o d", o=1))
+        load_h(2)
+        load_h(3)
+        load_wk(0, 1)
+        nc.sync.dma_start(out=wv_scale[:], in_=scale_v)
+        load_wv(0)
+        for g in (1, 2):
+            load_wk(g, 0)
+            load_wk(g, 1)
+            load_wv(g)
+        load_wv(3)
+        load_wv(4)
+
+        wk_grouped, wk_codes, wk_scales = {}, {}, {}
+
+        def new_wk(g):
+            if g not in wk_grouped:
+                wk_grouped[g] = stage2.tile([P, Q, K_PASS * PACK], BF16, align_bytes=64, name="wk_grouped")
+                wk_codes[g] = stage3.tile([P, Q, K_PASS], U32, align_bytes=64, name="wk_codes")
+                wk_scales[g] = stage3.tile([P, Q, K_PASS], U8, align_bytes=64, name="wk_scales")
+
+        def interleave_wk_on_tensor(g, q):
+            new_wk(g)
+            for b in range(2):
+                bank = psum2.tile([P, PACK, 64, PACK], BF16, name="interleave")
+                for a in range(2):
+                    c0 = 256 * b + 128 * a
+                    nc.tensor.matmul(
+                        bank[:, :, 32 * a:32 * a + 32, :].rearrange("p t m j -> p j m t"),
+                        lhsT=ident_bf16[:],
+                        rhs=wk_raw[g][:, q, :, c0:c0 + 128].rearrange("p j (m t) -> p j m t", t=PACK),
+                        start=True,
+                        stop=True,
+                    )
+                nc.scalar.copy(
+                    out=wk_grouped[g][:, q, :].bitcast(F32).rearrange("p (t w) -> p t w", t=PACK)[:, :, 128 * b:128 * b + 128],
+                    in_=bank[:].rearrange("p t m j -> p t (m j)").bitcast(F32),
+                )
+
+        def interleave_wk_on_vector(g, q, parts=1):
+            new_wk(g)
+            w = P // parts
+            for a in range(parts):
+                ms = slice(a * w, (a + 1) * w)
+                nc.vector.tensor_copy(
+                    out=wk_grouped[g][:, q, :].rearrange("p (t m j) -> p m j t", t=PACK, j=PACK)[:, ms, :, :],
+                    in_=wk_raw[g][:, q, :, :].rearrange("p j (m t) -> p m j t", t=PACK)[:, ms, :, :],
+                )
+
+        def interleave_wk(g):
+            for q in range(Q):
+                if q == 0 and g in PE_GROUPS:
+                    interleave_wk_on_tensor(g, q)
+                else:
+                    interleave_wk_on_vector(g, q)
+
+        def quantize_wk(g, q):
+            nc.vector.quantize_mx(
+                out=wk_codes[g][:, q, :].bitcast(FP8X4), scales=wk_scales[g][:, q, :], in_=wk_grouped[g][:, q, :])
+
+        wv_planes, wv_grouped = {}, {}
+
+        def widen_wv(u):
+            g, c0, w = UNITS[u]
+            wv_planes[u] = stage4.tile([P, PACK, w], BF16, align_bytes=64, name="wv_planes")
+            for t in range(PACK):
+                values = wv_bytes[:, g, t, c0:c0 + w].bitcast(FP8)
+                scale = wv_scale[:, g, t:t + 1]
+                if u in V_WIDENS:
+                    nc.vector.tensor_scalar(
+                        out=wv_planes[u][:, t, :], in0=values, scalar1=scale, scalar2=None, op0=ALU.mult)
+                else:
+                    nc.scalar.activation(out=wv_planes[u][:, t, :], in_=values, func=ACT.Copy, scale=scale)
+
+        def interleave_wv(u):
+            w = UNITS[u][2]
+            wv_grouped[u] = stage2.tile([P, w * PACK], BF16, align_bytes=64, name="wv_grouped")
+            nc.vector.tensor_copy(
+                out=wv_grouped[u][:].rearrange("p (c i t) -> p c t i", i=4, t=PACK),
+                in_=wv_planes[u][:].rearrange("p t (c i) -> p c t i", i=4),
+            )
+
+        ready = [0] * len(SLICES)
+
+        def quantize_wv(u):
+            g, c0, w = UNITS[u]
+            nc.vector.quantize_mx(
+                out=wv_codes[:, g, c0:c0 + w].bitcast(FP8X4), scales=wv_scales[:, g, c0:c0 + w], in_=wv_grouped[u][:])
+            for sl in range(len(SLICES)):
+                if c0 <= SLICES[sl][0] < c0 + w:
+                    ready[sl] += 1
+
+        next_unit = {widen_wv: 0, interleave_wv: 0, quantize_wv: 0}
+
+        def advance(*jobs):
+            for job in jobs:
+                if next_unit[job] < len(UNITS):
+                    job(next_unit[job])
+                    next_unit[job] += 1
+
+        relu, k_grouped = {}, {}
+
+        def first_product(g, i):
+            bank = psum2.tile([P, PACK, P], F32, name="hidden")
+            for t in range(PACK):
+                for q in range(Q):
+                    nc.tensor.matmul_mx(
+                        out=bank[:, t, :],
+                        lhsT=wk_codes[g][:, q, t * P:(t + 1) * P].bitcast(FP8X4),
+                        lhsT_scale=wk_scales[g][:, q, t * P:(t + 1) * P],
+                        rhs=h_codes[:, i, q, :].bitcast(FP8X4),
+                        rhs_scale=h_scales[:, i, q, :],
+                        start=(q == 0),
+                        stop=(q == Q - 1),
+                    )
+            if i == 0:
+                relu[g] = stage2.tile([P, NT, P, PACK], F32, align_bytes=64, name="relu")
+                k_grouped[g] = stage2.tile([P, NT, P, PACK], BF16, align_bytes=64, name="k_grouped")
+            nc.scalar.activation(out=relu[g][:, i, :, :], in_=bank[:].rearrange("p t n -> p n t"), func=ACT.Relu)
+
+        def square(g, first, last):
+            nc.scalar.activation(
+                out=k_grouped[g][:, first:last, :, :], in_=relu[g][:, first:last, :, :], func=ACT.Square)
+
+        def quantize_k(g):
+            nc.vector.quantize_mx(
+                out=k_codes[:, g, :].bitcast(FP8X4),
+                scales=k_scales[:, g, :],
+                in_=k_grouped[g][:].rearrange("p i n t -> p (i n t)"),
+            )
+
+        acc = {}
+
+        def second_product(sl, g, i):
+            c0, w = SLICES[sl]
+            if g == 0:
+                if sl == 1:
+                    acc[sl, i] = psum2.tile([P, w], F32, name="interleave" if i < 2 else "hidden")
+                else:
+                    acc[sl, i] = psum4.tile([P, w], F32, name="acc")
+            nc.tensor.matmul_mx(
+                out=acc[sl, i][:],
+                lhsT=k_codes[:, g, i * P:(i + 1) * P].bitcast(FP8X4),
+                lhsT_scale=k_scales[:, g, i * P:(i + 1) * P],
+                rhs=wv_codes[:, g, c0:c0 + w].bitcast(FP8X4),
+                rhs_scale=wv_scales[:, g, c0:c0 + w],
+                start=(g == 0),
+                stop=(g == G - 1),
+            )
+            if g == G - 1:
+                result = (stage4 if sl == 0 else stage8).tile([P, w], F32, align_bytes=64, name="result")
+                nc.vector.tensor_tensor(out=result[:], in0=acc[sl, i][:], in1=h_sb[:, i, c0:c0 + w], op=ALU.add)
+                nc.sync.dma_start(out=out_v[i][:, c0:c0 + w], in_=result[:])
+
+        done = {(sl, i): 0 for sl in range(len(SLICES)) for i in range(NT)}
+
+        def second_products(k_ready):
+            for sl in range(len(SLICES)):
+                for i in range(NT):
+                    if sl == 1 and k_ready < (G - 2 if i < 2 else G):
+                        continue
+                    if sl == 2 and done[0, i] < G:
+                        continue
+                    while done[sl, i] < min(ready[sl], k_ready):
+                        second_product(sl, done[sl, i], i)
+                        done[sl, i] += 1
+
+        gain_all = []
+        for c in range(2):
+            bank = psum4.tile([P, 512], F32, name="acc")
+            nc.tensor.matmul(bank[:], lhsT=ones[:], rhs=gain_row[:, c * 512:(c + 1) * 512], start=True, stop=True)
+            gain_all.append(bank)
+
+        def sum_squares(i):
+            nc.scalar.activation(out=unused[:], in_=h_sb[:, i, :], func=ACT.Square, accum_out=sumsq[:, i:i + 1])
+
+        def root(i0):
+            two = slice(i0, i0 + 2)
+            nc.vector.tensor_scalar(
+                out=rms[:, two], in0=sumsq[:, two], scalar1=1.0 / D, scalar2=EPS, op0=ALU.mult, op1=ALU.add)
+            nc.scalar.activation(out=rms[:, two], in_=rms[:, two], func=ACT.Sqrt)
+            nc.vector.reciprocal(out=rstd[:, two], in_=rms[:, two])
+
+        def normalize(i):
+            hn = stage2.tile([P, D], BF16, align_bytes=64, name="hn")
+            for c in range(2):
+                cols = slice(c * 512, (c + 1) * 512)
+                nc.vector.scalar_tensor_tensor(
+                    out=hn[:, cols], in0=h_sb[:, i, cols], scalar=rstd[:, i:i + 1], in1=gain_all[c][:],
+                    op0=ALU.mult, op1=ALU.mult)
+            turned = psum2.tile([P, Q, 2, P], F32, name="hidden")
+            words = hn[:].bitcast(F32)
+            for q in range(Q):
+                for v in range(2):
+                    nc.tensor.transpose(turned[:, q, v, :], words[:, 256 * q + v:256 * (q + 1):2], ident_f32[:])
+            hn_grouped = stage2.tile([P, Q * P * PACK], BF16, align_bytes=64, name="hn_grouped")
+            nc.scalar.copy(
+                out=hn_grouped[:].bitcast(F32).rearrange("p (q n v) -> p q n v", q=Q, v=2),
+                in_=turned[:].rearrange("p q v n -> p q n v"),
+            )
+            nc.vector.quantize_mx(
+                out=h_codes[:, i, :, :].rearrange("p q n -> p (q n)").bitcast(FP8X4),
+                scales=h_scales[:, i, :, :].rearrange("p q n -> p (q n)"),
+                in_=hn_grouped[:],
+            )
+
+        for a in range(2):
+            sum_squares(2 * a)
+            sum_squares(2 * a + 1)
+            root(2 * a)
+            normalize(2 * a)
+            normalize(2 * a + 1)
+            interleave_wk_on_vector(0, a, 2 - a)
+            quantize_wk(0, a)
+        interleave_wk(1)
+        for q in range(Q):
+            quantize_wk(1, q)
+        for u in range(EARLY):
+            advance(widen_wv)
+        for u in range(EARLY - 1):
+            advance(interleave_wv)
+
+        for g in range(G):
+            if g + 3 < G:
+                load_wk(g + 3, 0)
+                load_wk(g + 3, 1)
+            for later in (2 * g + 5, 2 * g + 6):
+                if later < G:
+                    load_wv(later)
+            for i in range(NT):
+                first_product(g, i)
+                if i % 2 == 1:
+                    square(g, i - 1, i + 1)
+            if g + 2 < G:
+                interleave_wk(g + 2)
+            quantize_k(g)
+            second_products(g + 1)
+            advance(quantize_wv, interleave_wv, widen_wv)
+            if g + 2 < G:
+                for q in range(Q):
+                    quantize_wk(g + 2, q)
+
+        while next_unit[quantize_wv] < len(UNITS):
+            advance(quantize_wv, interleave_wv, widen_wv)
+            second_products(G)

@@ -22,30 +22,34 @@ K_PASS = P * PACK
 NT = S // P
 G = FF // K_PASS
 Q = D // K_PASS
+HALF = D // 2
 
 SLICES = ((0, 512), (512, 256), (768, 256))
-UNITS = [(g, 0, 512) for g in range(G)] + [(g, 512, 512) for g in range(G - 1)] + [(G - 1, 512, 256), (G - 1, 768, 256)]
-V_WIDENS = range(4, 11)
-PE_GROUPS = range(1, G)
-EARLY = 3
+WHOLE = 5
+V_UPPER = 2
+PACE = 3
 
 
 def tile_block_pc_kernel(tc, h_attn, norm2_w, ffn_wk, ffn_wv_bytes, ffn_wv_scale, out):
     nc = tc.nc
     h_v = h_attn.rearrange("b (i p) d -> (b i) p d", p=P)
-    out_v = out.rearrange("b (i p) d -> (b i) p d", p=P)
+    out_v = out.rearrange("b (i p) d -> p (b i) d", p=P)
     wk_v = ffn_wk.rearrange("(q p j) (g c) -> g q p j c", q=Q, p=P, j=PACK, c=K_PASS)
     wv_v = ffn_wv_bytes.rearrange("(g p t) n -> g p t n", p=P, t=PACK)
     scale_v = ffn_wv_scale.rearrange("(g p t) o -> p g (t o)", p=P, t=PACK)
+
+    lower = [(g, 0, HALF) for g in range(G)]
+    upper = [(g, HALF, HALF) for g in range(WHOLE)]
+    upper += [(g, 512, 256) for g in range(WHOLE, G)] + [(g, 768, 256) for g in range(WHOLE, G)]
 
     with ExitStack() as ctx:
         keep = ctx.enter_context(tc.tile_pool(name="keep", bufs=1))
         stage2 = ctx.enter_context(tc.tile_pool(name="stage2", bufs=2))
         stage3 = ctx.enter_context(tc.tile_pool(name="stage3", bufs=3))
         stage4 = ctx.enter_context(tc.tile_pool(name="stage4", bufs=4))
-        stage8 = ctx.enter_context(tc.tile_pool(name="stage8", bufs=8))
-        psum4 = ctx.enter_context(tc.psum_pool(name="psum4", bufs=4))
-        psum2 = ctx.enter_context(tc.psum_pool(name="psum2", bufs=2))
+        stage6 = ctx.enter_context(tc.tile_pool(name="stage6", bufs=6))
+        psum = ctx.enter_context(tc.psum_pool(name="psum", bufs=1))
+        ctx.enter_context(tc.manual_schedule())
 
         h_sb = keep.tile([P, NT, D], BF16, align_bytes=64, name="h_sb")
         h_codes = keep.tile([P, NT, Q, P], U32, align_bytes=64, name="h_codes")
@@ -60,158 +64,144 @@ def tile_block_pc_kernel(tc, h_attn, norm2_w, ffn_wk, ffn_wv_bytes, ffn_wv_scale
         ones = keep.tile([P, P], BF16, align_bytes=64, name="ones")
         ident_bf16 = keep.tile([P, P], BF16, align_bytes=64, name="ident_bf16")
         ident_f32 = keep.tile([P, P], F32, align_bytes=64, name="ident_f32")
-        unused = keep.tile([P, D], BF16, align_bytes=64, name="unused")
         sumsq = keep.tile([P, NT], F32, align_bytes=64, name="sumsq")
-        rms = keep.tile([P, NT], F32, align_bytes=64, name="rms")
         rstd = keep.tile([P, NT], F32, align_bytes=64, name="rstd")
 
-        nc.vector.memset(gain_row[:], 0.0)
-        nc.vector.memset(ones[:], 1.0)
-        make_identity(nc, ident_f32[:])
-        make_identity(nc, ident_bf16[:])
+        turn = [0]
+
+        def work_bank(shape, dtype):
+            return psum.tile(shape, dtype, name="work%d" % turn[0])
 
         wk_raw = {}
 
-        def load_wk(g, q, parts=1):
-            if q == 0:
-                wk_raw[g] = stage3.tile([P, Q, PACK, K_PASS], BF16, align_bytes=64, name="wk_raw")
-            w = K_PASS // parts
-            for a in range(parts):
-                cols = slice(a * w, (a + 1) * w)
-                nc.sync.dma_start(out=wk_raw[g][:, q, :, cols], in_=wk_v[g, q][:, :, cols])
+        def load_wk(g, q):
+            wk_raw[g, q] = stage6.tile([P, PACK, K_PASS], BF16, align_bytes=64, name="wk_raw")
+            nc.sync.dma_start(out=wk_raw[g, q][:], in_=wk_v[g, q])
 
-        def load_wv(g):
-            nc.sync.dma_start(out=wv_bytes[:, g, :, :], in_=wv_v[g])
+        def load_wv(g, first, last):
+            nc.sync.dma_start(out=wv_bytes[:, g, :, first:last], in_=wv_v[g][:, :, first:last])
+
+        def load_scale():
+            nc.sync.dma_start(out=wv_scale[:], in_=scale_v)
+
+        def load_gain():
+            nc.sync.dma_start(out=gain_row[0:1, :], in_=norm2_w.rearrange("(o d) -> o d", o=1))
 
         def load_h(i):
             nc.sync.dma_start(out=h_sb[:, i, :], in_=h_v[i])
 
-        load_h(0)
-        load_wk(0, 0, 2)
-        load_h(1)
-        nc.sync.dma_start(out=gain_row[0:1, :], in_=norm2_w.rearrange("(o d) -> o d", o=1))
-        load_h(2)
-        load_h(3)
-        load_wk(0, 1)
-        nc.sync.dma_start(out=wv_scale[:], in_=scale_v)
-        load_wv(0)
-        for g in (1, 2):
-            load_wk(g, 0)
-            load_wk(g, 1)
-            load_wv(g)
-        load_wv(3)
-        load_wv(4)
+        wk_grouped, wk_codes, wk_scales, banks = {}, {}, {}, {}
 
-        wk_grouped, wk_codes, wk_scales = {}, {}, {}
-
-        def new_wk(g):
-            if g not in wk_grouped:
-                wk_grouped[g] = stage2.tile([P, Q, K_PASS * PACK], BF16, align_bytes=64, name="wk_grouped")
-                wk_codes[g] = stage3.tile([P, Q, K_PASS], U32, align_bytes=64, name="wk_codes")
-                wk_scales[g] = stage3.tile([P, Q, K_PASS], U8, align_bytes=64, name="wk_scales")
-
-        def interleave_wk_on_tensor(g, q):
-            new_wk(g)
-            for b in range(2):
-                bank = psum2.tile([P, PACK, 64, PACK], BF16, name="interleave")
-                for a in range(2):
-                    c0 = 256 * b + 128 * a
-                    nc.tensor.matmul(
-                        bank[:, :, 32 * a:32 * a + 32, :].rearrange("p t m j -> p j m t"),
-                        lhsT=ident_bf16[:],
-                        rhs=wk_raw[g][:, q, :, c0:c0 + 128].rearrange("p j (m t) -> p j m t", t=PACK),
-                        start=True,
-                        stop=True,
-                    )
-                nc.scalar.copy(
-                    out=wk_grouped[g][:, q, :].bitcast(F32).rearrange("p (t w) -> p t w", t=PACK)[:, :, 128 * b:128 * b + 128],
-                    in_=bank[:].rearrange("p t m j -> p t (m j)").bitcast(F32),
+        def wk_on_tensor(g, q, b):
+            bank = work_bank([P, PACK, 64, PACK], BF16)
+            for a in range(2):
+                c0 = 256 * b + 128 * a
+                nc.tensor.matmul(
+                    bank[:, :, 32 * a:32 * a + 32, :].rearrange("p t m j -> p j m t"),
+                    lhsT=ident_bf16[:],
+                    rhs=wk_raw[g, q][:, :, c0:c0 + 128].rearrange("p j (m t) -> p j m t", t=PACK),
+                    start=True,
+                    stop=True,
                 )
+            banks["wk", g, q, b] = bank
 
-        def interleave_wk_on_vector(g, q, parts=1):
-            new_wk(g)
-            w = P // parts
-            for a in range(parts):
-                ms = slice(a * w, (a + 1) * w)
-                nc.vector.tensor_copy(
-                    out=wk_grouped[g][:, q, :].rearrange("p (t m j) -> p m j t", t=PACK, j=PACK)[:, ms, :, :],
-                    in_=wk_raw[g][:, q, :, :].rearrange("p j (m t) -> p m j t", t=PACK)[:, ms, :, :],
-                )
+        def wk_out(g, q, b):
+            if b == 0:
+                wk_grouped[g, q] = stage3.tile([P, K_PASS * PACK], BF16, align_bytes=64, name="wk_grouped")
+            nc.scalar.copy(
+                out=wk_grouped[g, q][:].bitcast(F32).rearrange("p (t w) -> p t w", t=PACK)[:, :, 128 * b:128 * b + 128],
+                in_=banks["wk", g, q, b][:].rearrange("p t m j -> p t (m j)").bitcast(F32),
+            )
 
-        def interleave_wk(g):
-            for q in range(Q):
-                if q == 0 and g in PE_GROUPS:
-                    interleave_wk_on_tensor(g, q)
-                else:
-                    interleave_wk_on_vector(g, q)
+        def wk_on_vector(g, q):
+            wk_grouped[g, q] = stage3.tile([P, K_PASS * PACK], BF16, align_bytes=64, name="wk_grouped")
+            nc.vector.tensor_copy(
+                out=wk_grouped[g, q][:].rearrange("p (t m j) -> p m j t", t=PACK, j=PACK),
+                in_=wk_raw[g, q][:].rearrange("p j (m t) -> p m j t", t=PACK),
+            )
 
         def quantize_wk(g, q):
+            wk_codes[g, q] = stage6.tile([P, K_PASS], U32, align_bytes=64, name="wk_codes")
+            wk_scales[g, q] = stage6.tile([P, K_PASS], U8, align_bytes=64, name="wk_scales")
             nc.vector.quantize_mx(
-                out=wk_codes[g][:, q, :].bitcast(FP8X4), scales=wk_scales[g][:, q, :], in_=wk_grouped[g][:, q, :])
+                out=wk_codes[g, q][:].bitcast(FP8X4), scales=wk_scales[g, q][:], in_=wk_grouped[g, q][:])
 
         wv_planes, wv_grouped = {}, {}
+        planes_pool = {True: stage2, False: stage4}
 
-        def widen_wv(u):
-            g, c0, w = UNITS[u]
-            wv_planes[u] = stage4.tile([P, PACK, w], BF16, align_bytes=64, name="wv_planes")
-            for t in range(PACK):
+        def widen(u, on_vector, first, last):
+            g, c0, w = u
+            if first == 0:
+                wv_planes[u] = planes_pool[on_vector].tile([P, PACK, w], BF16, align_bytes=64, name="wv_planes")
+            for t in range(first, last):
                 values = wv_bytes[:, g, t, c0:c0 + w].bitcast(FP8)
                 scale = wv_scale[:, g, t:t + 1]
-                if u in V_WIDENS:
+                if on_vector:
                     nc.vector.tensor_scalar(
                         out=wv_planes[u][:, t, :], in0=values, scalar1=scale, scalar2=None, op0=ALU.mult)
                 else:
                     nc.scalar.activation(out=wv_planes[u][:, t, :], in_=values, func=ACT.Copy, scale=scale)
 
-        def interleave_wv(u):
-            w = UNITS[u][2]
-            wv_grouped[u] = stage2.tile([P, w * PACK], BF16, align_bytes=64, name="wv_grouped")
+        def wv_on_vector(u):
+            wv_grouped[u] = stage3.tile([P, u[2] * PACK], BF16, align_bytes=64, name="wv_grouped")
             nc.vector.tensor_copy(
                 out=wv_grouped[u][:].rearrange("p (c i t) -> p c t i", i=4, t=PACK),
                 in_=wv_planes[u][:].rearrange("p t (c i) -> p c t i", i=4),
             )
 
-        ready = [0] * len(SLICES)
+        def wv_on_tensor(u, b):
+            bank = work_bank([P, 256, PACK], BF16)
+            for a in range(2):
+                c0 = 256 * b + 128 * a
+                nc.tensor.matmul(
+                    bank[:, 128 * a:128 * a + 128, :].rearrange("p n t -> p t n"),
+                    lhsT=ident_bf16[:],
+                    rhs=wv_planes[u][:, :, c0:c0 + 128],
+                    start=True,
+                    stop=True,
+                )
+            banks["wv", u, b] = bank
+
+        def wv_out(u, b):
+            if b == 0:
+                wv_grouped[u] = stage3.tile([P, u[2] * PACK], BF16, align_bytes=64, name="wv_grouped")
+            nc.scalar.copy(
+                out=wv_grouped[u][:].bitcast(F32)[:, 512 * b:512 * b + 512],
+                in_=banks["wv", u, b][:].rearrange("p n t -> p (n t)").bitcast(F32),
+            )
 
         def quantize_wv(u):
-            g, c0, w = UNITS[u]
+            g, c0, w = u
             nc.vector.quantize_mx(
                 out=wv_codes[:, g, c0:c0 + w].bitcast(FP8X4), scales=wv_scales[:, g, c0:c0 + w], in_=wv_grouped[u][:])
-            for sl in range(len(SLICES)):
-                if c0 <= SLICES[sl][0] < c0 + w:
-                    ready[sl] += 1
-
-        next_unit = {widen_wv: 0, interleave_wv: 0, quantize_wv: 0}
-
-        def advance(*jobs):
-            for job in jobs:
-                if next_unit[job] < len(UNITS):
-                    job(next_unit[job])
-                    next_unit[job] += 1
 
         relu, k_grouped = {}, {}
 
         def first_product(g, i):
-            bank = psum2.tile([P, PACK, P], F32, name="hidden")
+            bank = work_bank([P, PACK, P], F32)
             for t in range(PACK):
                 for q in range(Q):
                     nc.tensor.matmul_mx(
                         out=bank[:, t, :],
-                        lhsT=wk_codes[g][:, q, t * P:(t + 1) * P].bitcast(FP8X4),
-                        lhsT_scale=wk_scales[g][:, q, t * P:(t + 1) * P],
+                        lhsT=wk_codes[g, q][:, t * P:(t + 1) * P].bitcast(FP8X4),
+                        lhsT_scale=wk_scales[g, q][:, t * P:(t + 1) * P],
                         rhs=h_codes[:, i, q, :].bitcast(FP8X4),
                         rhs_scale=h_scales[:, i, q, :],
                         start=(q == 0),
                         stop=(q == Q - 1),
                     )
-            if i == 0:
-                relu[g] = stage2.tile([P, NT, P, PACK], F32, align_bytes=64, name="relu")
-                k_grouped[g] = stage2.tile([P, NT, P, PACK], BF16, align_bytes=64, name="k_grouped")
-            nc.scalar.activation(out=relu[g][:, i, :, :], in_=bank[:].rearrange("p t n -> p n t"), func=ACT.Relu)
+            banks["hidden", g, i] = bank
 
-        def square(g, first, last):
+        def rectify(g, i):
+            if i % 2 == 0:
+                relu[g, i // 2] = stage2.tile([P, 2, P, PACK], F32, align_bytes=64, name="relu")
             nc.scalar.activation(
-                out=k_grouped[g][:, first:last, :, :], in_=relu[g][:, first:last, :, :], func=ACT.Square)
+                out=relu[g, i // 2][:, i % 2, :, :], in_=banks["hidden", g, i][:].rearrange("p t n -> p n t"), func=ACT.Relu)
+
+        def square(g, a):
+            if a == 0:
+                k_grouped[g] = stage3.tile([P, NT, P, PACK], BF16, align_bytes=64, name="k_grouped")
+            nc.scalar.activation(out=k_grouped[g][:, 2 * a:2 * a + 2, :, :], in_=relu[g, a][:], func=ACT.Square)
 
         def quantize_k(g):
             nc.vector.quantize_mx(
@@ -220,117 +210,267 @@ def tile_block_pc_kernel(tc, h_attn, norm2_w, ffn_wk, ffn_wv_bytes, ffn_wv_scale
                 in_=k_grouped[g][:].rearrange("p i n t -> p (i n t)"),
             )
 
-        acc = {}
+        acc, result = {}, {}
+        bank_of = {(0, 0): "acc0", (0, 1): "acc1", (0, 2): "acc2", (0, 3): "acc3",
+                   (1, 0): "work2", (1, 1): "work3", (2, 0): "acc0", (2, 1): "acc1"}
 
-        def second_product(sl, g, i):
+        def second_product(sl, g, first, last):
             c0, w = SLICES[sl]
-            if g == 0:
-                if sl == 1:
-                    acc[sl, i] = psum2.tile([P, w], F32, name="interleave" if i < 2 else "hidden")
-                else:
-                    acc[sl, i] = psum4.tile([P, w], F32, name="acc")
-            nc.tensor.matmul_mx(
-                out=acc[sl, i][:],
-                lhsT=k_codes[:, g, i * P:(i + 1) * P].bitcast(FP8X4),
-                lhsT_scale=k_scales[:, g, i * P:(i + 1) * P],
-                rhs=wv_codes[:, g, c0:c0 + w].bitcast(FP8X4),
-                rhs_scale=wv_scales[:, g, c0:c0 + w],
-                start=(g == 0),
-                stop=(g == G - 1),
-            )
-            if g == G - 1:
-                result = (stage4 if sl == 0 else stage8).tile([P, w], F32, align_bytes=64, name="result")
-                nc.vector.tensor_tensor(out=result[:], in0=acc[sl, i][:], in1=h_sb[:, i, c0:c0 + w], op=ALU.add)
-                nc.sync.dma_start(out=out_v[i][:, c0:c0 + w], in_=result[:])
+            share = HALF // w
+            for i in range(first, last):
+                b, r = divmod(i, share)
+                if g == 0 and r == 0:
+                    acc[sl, b] = psum.tile([P, share, w], F32, name=bank_of[sl, b])
+                nc.tensor.matmul_mx(
+                    out=acc[sl, b][:, r, :],
+                    lhsT=k_codes[:, g, i * P:(i + 1) * P].bitcast(FP8X4),
+                    lhsT_scale=k_scales[:, g, i * P:(i + 1) * P],
+                    rhs=wv_codes[:, g, c0:c0 + w].bitcast(FP8X4),
+                    rhs_scale=wv_scales[:, g, c0:c0 + w],
+                    start=(g == 0 and r == 0),
+                    stop=(g == G - 1 and r == share - 1),
+                )
 
-        done = {(sl, i): 0 for sl in range(len(SLICES)) for i in range(NT)}
+        def finish(sl, b):
+            c0, w = SLICES[sl]
+            share = HALF // w
+            tiles = slice(b * share, (b + 1) * share)
+            result[sl, b] = stage4.tile([P, share, w], F32, align_bytes=64, name="result")
+            nc.vector.tensor_tensor(out=result[sl, b][:], in0=acc[sl, b][:], in1=h_sb[:, tiles, c0:c0 + w], op=ALU.add)
 
-        def second_products(k_ready):
-            for sl in range(len(SLICES)):
-                for i in range(NT):
-                    if sl == 1 and k_ready < (G - 2 if i < 2 else G):
-                        continue
-                    if sl == 2 and done[0, i] < G:
-                        continue
-                    while done[sl, i] < min(ready[sl], k_ready):
-                        second_product(sl, done[sl, i], i)
-                        done[sl, i] += 1
+        def store(sl, b):
+            c0, w = SLICES[sl]
+            share = HALF // w
+            nc.sync.dma_start(out=out_v[:, b * share:(b + 1) * share, c0:c0 + w], in_=result[sl, b][:])
 
-        gain_all = []
-        for c in range(2):
-            bank = psum4.tile([P, 512], F32, name="acc")
-            nc.tensor.matmul(bank[:], lhsT=ones[:], rhs=gain_row[:, c * 512:(c + 1) * 512], start=True, stop=True)
-            gain_all.append(bank)
+        gain_all, hn, hn_grouped = [], {}, {}
+
+        def spread_gain():
+            for c in range(2):
+                bank = psum.tile([P, 512], F32, name="acc%d" % c)
+                nc.tensor.matmul(bank[:], lhsT=ones[:], rhs=gain_row[:, c * 512:(c + 1) * 512], start=True, stop=True)
+                gain_all.append(bank)
 
         def sum_squares(i):
-            nc.scalar.activation(out=unused[:], in_=h_sb[:, i, :], func=ACT.Square, accum_out=sumsq[:, i:i + 1])
+            squares = stage2.tile([P, D], BF16, align_bytes=64, name="squares")
+            nc.scalar.activation(out=squares[:], in_=h_sb[:, i, :], func=ACT.Square, accum_out=sumsq[:, i:i + 1])
 
-        def root(i0):
-            two = slice(i0, i0 + 2)
-            nc.vector.tensor_scalar(
-                out=rms[:, two], in0=sumsq[:, two], scalar1=1.0 / D, scalar2=EPS, op0=ALU.mult, op1=ALU.add)
-            nc.scalar.activation(out=rms[:, two], in_=rms[:, two], func=ACT.Sqrt)
-            nc.vector.reciprocal(out=rstd[:, two], in_=rms[:, two])
+        def root(i):
+            nc.scalar.activation(
+                out=rstd[:, i:i + 1], in_=sumsq[:, i:i + 1], func=ACT.Abs_reciprocal_sqrt, scale=1.0 / D, bias=EPS)
 
         def normalize(i):
-            hn = stage2.tile([P, D], BF16, align_bytes=64, name="hn")
+            hn[i] = stage2.tile([P, D], BF16, align_bytes=64, name="hn")
             for c in range(2):
                 cols = slice(c * 512, (c + 1) * 512)
                 nc.vector.scalar_tensor_tensor(
-                    out=hn[:, cols], in0=h_sb[:, i, cols], scalar=rstd[:, i:i + 1], in1=gain_all[c][:],
+                    out=hn[i][:, cols], in0=h_sb[:, i, cols], scalar=rstd[:, i:i + 1], in1=gain_all[c][:],
                     op0=ALU.mult, op1=ALU.mult)
-            turned = psum2.tile([P, Q, 2, P], F32, name="hidden")
-            words = hn[:].bitcast(F32)
+
+        def turn_hn(i):
+            bank = work_bank([P, Q, 2, P], F32)
+            words = hn[i][:].bitcast(F32)
             for q in range(Q):
                 for v in range(2):
-                    nc.tensor.transpose(turned[:, q, v, :], words[:, 256 * q + v:256 * (q + 1):2], ident_f32[:])
-            hn_grouped = stage2.tile([P, Q * P * PACK], BF16, align_bytes=64, name="hn_grouped")
+                    nc.tensor.transpose(bank[:, q, v, :], words[:, 256 * q + v:256 * (q + 1):2], ident_f32[:])
+            banks["hn", i] = bank
+
+        def hn_out(i):
+            hn_grouped[i] = stage2.tile([P, Q * P * PACK], BF16, align_bytes=64, name="hn_grouped")
             nc.scalar.copy(
-                out=hn_grouped[:].bitcast(F32).rearrange("p (q n v) -> p q n v", q=Q, v=2),
-                in_=turned[:].rearrange("p q v n -> p q n v"),
+                out=hn_grouped[i][:].bitcast(F32).rearrange("p (q n v) -> p q n v", q=Q, v=2),
+                in_=banks["hn", i][:].rearrange("p q v n -> p q n v"),
             )
+
+        def quantize_hn(i):
             nc.vector.quantize_mx(
                 out=h_codes[:, i, :, :].rearrange("p q n -> p (q n)").bitcast(FP8X4),
                 scales=h_scales[:, i, :, :].rearrange("p q n -> p (q n)"),
-                in_=hn_grouped[:],
+                in_=hn_grouped[i][:],
             )
 
-        for a in range(2):
-            sum_squares(2 * a)
-            sum_squares(2 * a + 1)
-            root(2 * a)
-            normalize(2 * a)
-            normalize(2 * a + 1)
-            interleave_wk_on_vector(0, a, 2 - a)
-            quantize_wk(0, a)
-        interleave_wk(1)
-        for q in range(Q):
-            quantize_wk(1, q)
-        for u in range(EARLY):
-            advance(widen_wv)
-        for u in range(EARLY - 1):
-            advance(interleave_wv)
+        nc.vector.memset(ones[:], 1.0)
+        nc.vector.memset(gain_row[:], 0.0)
+        make_identity(nc, ident_bf16[:])
+        make_identity(nc, ident_f32[:])
 
+        sync = [(load_h, 0), (load_scale,), (load_wv, 0, 0, HALF), (load_h, 1), (load_gain,), (load_h, 2),
+                (load_wk, 0, 1), (load_h, 3), (load_wv, 0, HALF, D), (load_wk, 0, 0), (load_wk, 1, 0), (load_wk, 1, 1)]
+        for g in range(2, G):
+            sync += [(load_wk, g, 0), (load_wk, g, 1), (load_wv, g - 1, 0, D)]
+        sync += [(load_wv, G - 1, 0, D)]
+        sync += [(store, 0, b) for b in range(4)] + [(store, 1, 0), (store, 1, 1), (store, 2, 0), (store, 2, 1)]
+
+        def planes(u):
+            return [(widen, u, False, t, t + 1) for t in range(PACK)]
+
+        early = planes(upper[0])
+        tensor = [(spread_gain,), (wk_on_tensor, 0, 1, 0), (turn_hn, 0), (wk_on_tensor, 0, 1, 1), (turn_hn, 1),
+                  (wk_on_tensor, 1, 0, 0), (turn_hn, 2), (wk_on_tensor, 1, 0, 1)]
+        scalar = [(sum_squares, 0), (sum_squares, 1), (root, 0), (sum_squares, 2), (root, 1), (sum_squares, 3), (root, 2),
+                  early[0], (root, 3), early[1], (wk_out, 0, 1, 0), (hn_out, 0), early[2], (wk_out, 0, 1, 1), (hn_out, 1), early[3],
+                  (wk_out, 1, 0, 0), (hn_out, 2), (wk_out, 1, 0, 1)]
+        vector = [(widen, lower[0], True, 0, 4), (wv_on_vector, lower[0]), (normalize, 0), (normalize, 1), (quantize_wv, lower[0]),
+                  (wk_on_vector, 0, 0), (quantize_hn, 0), (normalize, 2), (quantize_wk, 0, 0), (quantize_wk, 0, 1), (quantize_hn, 1),
+                  (normalize, 3), (wk_on_vector, 1, 1), (quantize_hn, 2), (quantize_wk, 1, 0), (quantize_wk, 1, 1), (quantize_hn, 3)]
+        lower_products = [(second_product, 0, g, i, i + 1) for g in range(G) for i in range(NT)]
+        a, b, c = upper[2], upper[3], upper[4]
+        taken = 0
         for g in range(G):
-            if g + 3 < G:
-                load_wk(g + 3, 0)
-                load_wk(g + 3, 1)
-            for later in (2 * g + 5, 2 * g + 6):
-                if later < G:
-                    load_wv(later)
-            for i in range(NT):
-                first_product(g, i)
-                if i % 2 == 1:
-                    square(g, i - 1, i + 1)
             if g + 2 < G:
-                interleave_wk(g + 2)
-            quantize_k(g)
-            second_products(g + 1)
-            advance(quantize_wv, interleave_wv, widen_wv)
+                mm = [[(wk_on_tensor, g + 2, 0, half)] for half in range(2)]
+                fill = [[(wk_out, g + 2, 0, half)] for half in range(2)]
+            elif g == G - 2:
+                mm = [[], []]
+                fill = [planes(a)[:2], planes(a)[2:]]
+            else:
+                mm = [[(wv_on_tensor, a, half)] for half in range(2)]
+                fill = [[(wv_out, a, half), planes(b)[half]] for half in range(2)]
+            tensor += [(first_product, g, 0), (first_product, g, 1)]
+            scalar += [(rectify, g, 0), (rectify, g, 1)]
+            if g == 0:
+                tensor += [(turn_hn, 3)]
+                scalar += [(hn_out, 3)]
+            tensor += mm[0] + [(first_product, g, 2), (first_product, g, 3)] + mm[1]
+            scalar += fill[0] + [(square, g, 0), (rectify, g, 2), (rectify, g, 3)] + fill[1] + [(square, g, 1)]
+            upto = max(0, min(NT * (g - 1), taken + PACE))
+            tensor += lower_products[taken:upto]
+            taken = upto
             if g + 2 < G:
-                for q in range(Q):
-                    quantize_wk(g + 2, q)
+                u = lower[g + 1]
+                vector += [(wk_on_vector, g + 2, 1), (widen, u, True, 0, 4), (quantize_wk, g + 2, 1), (quantize_wk, g + 2, 0),
+                           (wv_on_vector, u), (quantize_k, g), (quantize_wv, u)]
+            elif g == G - 2:
+                vector += [(widen, lower[G - 1], True, 0, 4), (wv_on_vector, upper[0]), (wv_on_vector, lower[G - 1]), (quantize_k, g),
+                           (quantize_wv, upper[0]), (widen, upper[1], True, 0, 4), (quantize_wv, lower[G - 1])]
+            else:
+                vector += [(wv_on_vector, upper[1]), (quantize_wv, a), (quantize_k, g), (quantize_wv, upper[1])]
+        done = [G, 0, 0]
 
-        while next_unit[quantize_wv] < len(UNITS):
-            advance(quantize_wv, interleave_wv, widen_wv)
-            second_products(G)
+        def products(upto, slices):
+            jobs = []
+            for sl in slices:
+                jobs += [(second_product, sl, g, 0, NT) for g in range(done[sl], upto[sl])]
+                done[sl] = max(done[sl], upto[sl])
+            return jobs
+
+        todo = upper[5:]
+        scalar += planes(b)[2:] + planes(c) + planes(todo[0]) + [(wv_out, b, 0), (wv_out, b, 1)]
+        for u in todo[1:]:
+            scalar += planes(u)
+        tensor += lower_products[taken:] + [(wv_on_tensor, b, 0), (wv_on_tensor, b, 1)]
+        tensor += products([G, 3, 3], (1, 2)) + products([G, 5, 5], (1, 2))
+        vector += [(finish, 0, 0), (finish, 0, 1), (finish, 0, 2), (wv_on_vector, c), (finish, 0, 3), (wv_on_vector, todo[0]),
+                   (quantize_wv, c), (quantize_wv, b)]
+        for n in range(1, len(todo) - 1):
+            vector += [(wv_on_vector, todo[n]), (quantize_wv, todo[n - 1])]
+        vector += [(quantize_wv, todo[-2]), (wv_on_vector, todo[-1]), (finish, 1, 0), (quantize_wv, todo[-1]),
+                   (finish, 1, 1), (finish, 2, 0), (finish, 2, 1)]
+        for g, c0, w in todo:
+            tensor += products([g + 1 if c0 == SLICES[sl][0] else 0 for sl in range(3)], (1, 2))
+
+        def widened(u):
+            return [job for job in vector + scalar if job[0] is widen and job[1] == u]
+
+        def grouped_by(u):
+            return [job for job in vector + scalar if job[0] in (wv_on_vector, wv_out) and job[1] == u]
+
+        def needs(job):
+            f, a = job[0], job[1:]
+            if f is spread_gain:
+                return [(load_gain,)]
+            if f is sum_squares:
+                return [(load_h, a[0])]
+            if f is normalize:
+                return [(root, a[0]), (spread_gain,)]
+            if f is turn_hn:
+                return [(normalize, a[0])]
+            if f is hn_out:
+                return [(turn_hn, a[0])]
+            if f is quantize_hn:
+                return [(hn_out, a[0])]
+            if f in (wk_on_tensor, wk_on_vector):
+                return [(load_wk, a[0], a[1])]
+            if f is wk_out:
+                return [(wk_on_tensor,) + a]
+            if f is quantize_wk:
+                return [(wk_out,) + a + (1,)] if (wk_out,) + a + (1,) in scalar else [(wk_on_vector,) + a]
+            if f is widen:
+                return [(load_scale,)] + [j for j in sync if j[0] is load_wv and j[1] == a[0][0] and j[2] <= a[0][1] < j[3]]
+            if f in (wv_on_vector, wv_on_tensor):
+                return widened(a[0])
+            if f is wv_out:
+                return [(wv_on_tensor,) + a]
+            if f is quantize_wv:
+                return grouped_by(a[0])
+            if f is first_product:
+                return [(quantize_wk, a[0], q) for q in range(Q)] + [(quantize_hn, a[1])]
+            if f is rectify:
+                return [(first_product,) + a]
+            if f is quantize_k:
+                return [(square, a[0], 1)]
+            if f is second_product:
+                c0 = SLICES[a[0]][0]
+                unit = [u for u in lower + upper if u[0] == a[1] and u[1] <= c0 < u[1] + u[2]][0]
+                return [(quantize_k, a[1]), (quantize_wv, unit)] + freed.get(a[:2], [])
+            if f is finish:
+                return [j for j in tensor if j[:3] == (second_product, a[0], G - 1)]
+            if f is store:
+                return [(finish,) + a]
+            return []
+
+        def last_readers(job):
+            f, a = job[0], job[1:]
+            if f is load_wk:
+                return "wk_raw", 6, [j for j in tensor + vector if j[0] in (wk_on_tensor, wk_on_vector) and j[1:3] == a]
+            if f is wk_on_vector or (f is wk_out and a[2] == 0):
+                return "wk_grouped", 3, [(quantize_wk,) + a[:2]]
+            if f is quantize_wk:
+                return "wk_codes", 6, [(first_product, a[0], NT - 1)]
+            if f is widen and a[2] == 0:
+                return ("planes", a[1]), 2 if a[1] else 4, [
+                    j for j in tensor + vector if j[0] in (wv_on_tensor, wv_on_vector) and j[1] == a[0]]
+            if f is wv_on_vector or (f is wv_out and a[1] == 0):
+                return "wv_grouped", 3, [(quantize_wv, a[0])]
+            if f is square and a[1] == 0:
+                return "k_grouped", 3, [(quantize_k, a[0])]
+            if f is normalize:
+                return "hn", 2, [(turn_hn, a[0])]
+            if f is hn_out:
+                return "hn_grouped", 2, [(quantize_hn, a[0])]
+            if f is finish:
+                return "result", 4, [(store,) + a]
+            return None, 0, []
+
+        emptied_by = {wk_on_tensor: wk_out, wv_on_tensor: wv_out, first_product: rectify, turn_hn: hn_out}
+        bank_user = {}
+        freed = {(0, 0): [(normalize, NT - 1)], (1, 0): [(rectify, G - 1, NT - 1)], (2, 0): [(finish, 0, 0), (finish, 0, 1)]}
+        written, rings = set(), {}
+        queues = [sync, tensor, scalar, vector]
+        at = [0] * len(queues)
+        count = 0
+        while any(at[e] < len(queues[e]) for e in range(len(queues))):
+            moved = False
+            for e in range(len(queues)):
+                if at[e] == len(queues[e]):
+                    continue
+                job = queues[e][at[e]]
+                wanted = list(needs(job))
+                ring, depth, readers = last_readers(job)
+                if ring is not None and len(rings.setdefault(ring, [])) >= depth:
+                    wanted += rings[ring][-depth]
+                if job[0] in emptied_by:
+                    bank = count % (2 if (rectify, G - 1, NT - 1) in written else 4)
+                    wanted += bank_user.get(bank, [])
+                if all(w in written for w in wanted):
+                    if ring is not None:
+                        rings[ring].append(readers)
+                    if job[0] in emptied_by:
+                        turn[0] = bank
+                        bank_user[bank] = [(emptied_by[job[0]],) + job[1:]]
+                        count += 1
+                    job[0](*job[1:])
+                    written.add(job)
+                    at[e] += 1
+                    moved = True
+            assert moved, [queues[e][at[e]:at[e] + 1] for e in range(len(queues))]

@@ -52,10 +52,10 @@ def tile_block_pc_kernel(tc, h_attn, norm2_w, ffn_wk, ffn_wv_bytes, ffn_wv_scale
         ctx.enter_context(tc.manual_schedule())
 
         h_sb = keep.tile([P, NT, D], BF16, align_bytes=64, name="h_sb")
-        h_codes = keep.tile([P, NT, Q, P], U32, align_bytes=64, name="h_codes")
-        h_scales = keep.tile([P, NT, Q, P], U8, align_bytes=64, name="h_scales")
+        h_codes = keep.tile([P, Q, S], U32, align_bytes=64, name="h_codes")
+        h_scales = keep.tile([P, Q, S], U8, align_bytes=64, name="h_scales")
         wv_bytes = keep.tile([P, G, PACK, D], U8, align_bytes=64, name="wv_bytes")
-        wv_scale = keep.tile([P, G, PACK], F32, align_bytes=64, name="wv_scale")
+        wv_scale = keep.tile([P, G, 2 * PACK], F32, align_bytes=64, name="wv_scale")
         wv_codes = keep.tile([P, G, D], U32, align_bytes=64, name="wv_codes")
         wv_scales = keep.tile([P, G, D], U8, align_bytes=64, name="wv_scales")
         k_codes = keep.tile([P, G, S], U32, align_bytes=64, name="k_codes")
@@ -75,14 +75,14 @@ def tile_block_pc_kernel(tc, h_attn, norm2_w, ffn_wk, ffn_wv_bytes, ffn_wv_scale
         wk_raw = {}
 
         def load_wk(g, q):
-            wk_raw[g, q] = stage6.tile([P, PACK, K_PASS], BF16, align_bytes=64, name="wk_raw")
+            wk_raw[g, q] = stage6.tile([P, PACK, K_PASS], BF16, align_bytes=64, name="wk_raw", bufs=5)
             nc.sync.dma_start(out=wk_raw[g, q][:], in_=wk_v[g, q])
 
         def load_wv(g, first, last):
-            nc.sync.dma_start(out=wv_bytes[:, g, :, first:last], in_=wv_v[g][:, :, first:last])
+            nc.sync.dma_start(out=wv_bytes[:, g, first:last, :], in_=wv_v[g][:, first:last, :])
 
-        def load_scale():
-            nc.sync.dma_start(out=wv_scale[:], in_=scale_v)
+        def load_scale(first, last):
+            nc.sync.dma_start(out=wv_scale[:, first:last, 0:PACK], in_=scale_v[:, first:last, :])
 
         def load_gain():
             nc.sync.dma_start(out=gain_row[0:1, :], in_=norm2_w.rearrange("(o d) -> o d", o=1))
@@ -127,12 +127,12 @@ def tile_block_pc_kernel(tc, h_attn, norm2_w, ffn_wk, ffn_wv_bytes, ffn_wv_scale
                 out=wk_codes[g, q][:].bitcast(FP8X4), scales=wk_scales[g, q][:], in_=wk_grouped[g, q][:])
 
         wv_planes, wv_grouped = {}, {}
-        planes_pool = {True: stage2, False: stage4}
+        planes_pool = {True: stage3, False: stage4}
 
         def widen(u, on_vector, first, last):
             g, c0, w = u
             if first == 0:
-                wv_planes[u] = planes_pool[on_vector].tile([P, PACK, w], BF16, align_bytes=64, name="wv_planes")
+                wv_planes[u] = planes_pool[on_vector].tile([P, PACK, w], BF16, align_bytes=64, name="wv_planes_v" if on_vector else "wv_planes_s")
             for t in range(first, last):
                 values = wv_bytes[:, g, t, c0:c0 + w].bitcast(FP8)
                 scale = wv_scale[:, g, t:t + 1]
@@ -178,39 +178,44 @@ def tile_block_pc_kernel(tc, h_attn, norm2_w, ffn_wk, ffn_wv_bytes, ffn_wv_scale
         relu, k_grouped = {}, {}
 
         def first_product(g, i):
-            bank = work_bank([P, PACK, P], F32)
-            for t in range(PACK):
+            a, u = divmod(i, 2)
+            tokens = slice(2 * P * a, 2 * P * (a + 1))
+            bank = work_bank([P, 2, 2 * P], F32)
+            for e in range(2):
+                t = 2 * u + e
                 for q in range(Q):
                     nc.tensor.matmul_mx(
-                        out=bank[:, t, :],
+                        out=bank[:, e, :],
                         lhsT=wk_codes[g, q][:, t * P:(t + 1) * P].bitcast(FP8X4),
                         lhsT_scale=wk_scales[g, q][:, t * P:(t + 1) * P],
-                        rhs=h_codes[:, i, q, :].bitcast(FP8X4),
-                        rhs_scale=h_scales[:, i, q, :],
+                        rhs=h_codes[:, q, tokens].bitcast(FP8X4),
+                        rhs_scale=h_scales[:, q, tokens],
                         start=(q == 0),
                         stop=(q == Q - 1),
                     )
             banks["hidden", g, i] = bank
 
         def rectify(g, i):
-            if i % 2 == 0:
-                relu[g, i // 2] = stage2.tile([P, 2, P, PACK], F32, align_bytes=64, name="relu")
+            a, u = divmod(i, 2)
+            if u == 0:
+                relu[g, a] = stage2.tile([P, 2, 2 * P, 2], F32, align_bytes=64, name="relu")
             nc.scalar.activation(
-                out=relu[g, i // 2][:, i % 2, :, :], in_=banks["hidden", g, i][:].rearrange("p t n -> p n t"), func=ACT.Relu)
+                out=relu[g, a][:, u, :, :], in_=banks["hidden", g, i][:].rearrange("p e n -> p n e"), func=ACT.Relu)
 
         def square(g, a):
             if a == 0:
-                k_grouped[g] = stage3.tile([P, NT, P, PACK], BF16, align_bytes=64, name="k_grouped")
-            nc.scalar.activation(out=k_grouped[g][:, 2 * a:2 * a + 2, :, :], in_=relu[g, a][:], func=ACT.Square)
+                k_grouped[g] = stage3.tile([P, 2, 2 * P, 2, 2], BF16, align_bytes=64, name="k_grouped")
+            nc.scalar.activation(
+                out=k_grouped[g][:, a, :, :, :], in_=relu[g, a][:].rearrange("p u n e -> p n u e"), func=ACT.Square)
 
         def quantize_k(g):
             nc.vector.quantize_mx(
                 out=k_codes[:, g, :].bitcast(FP8X4),
                 scales=k_scales[:, g, :],
-                in_=k_grouped[g][:].rearrange("p i n t -> p (i n t)"),
+                in_=k_grouped[g][:].rearrange("p a n u e -> p (a n u e)"),
             )
 
-        acc, result = {}, {}
+        acc, passes, result = {}, {}, {}
         bank_of = {(0, 0): "acc0", (0, 1): "acc1", (0, 2): "acc2", (0, 3): "acc3",
                    (1, 0): "work2", (1, 1): "work3", (2, 0): "acc0", (2, 1): "acc1"}
 
@@ -219,16 +224,17 @@ def tile_block_pc_kernel(tc, h_attn, norm2_w, ffn_wk, ffn_wv_bytes, ffn_wv_scale
             share = HALF // w
             for i in range(first, last):
                 b, r = divmod(i, share)
-                if g == 0 and r == 0:
+                if (sl, b) not in acc:
                     acc[sl, b] = psum.tile([P, share, w], F32, name=bank_of[sl, b])
+                passes[sl, b] = passes.get((sl, b), 0) + 1
                 nc.tensor.matmul_mx(
                     out=acc[sl, b][:, r, :],
                     lhsT=k_codes[:, g, i * P:(i + 1) * P].bitcast(FP8X4),
                     lhsT_scale=k_scales[:, g, i * P:(i + 1) * P],
                     rhs=wv_codes[:, g, c0:c0 + w].bitcast(FP8X4),
                     rhs_scale=wv_scales[:, g, c0:c0 + w],
-                    start=(g == 0 and r == 0),
-                    stop=(g == G - 1 and r == share - 1),
+                    start=(passes[sl, b] == 1),
+                    stop=(passes[sl, b] == G * share),
                 )
 
         def finish(sl, b):
@@ -283,54 +289,61 @@ def tile_block_pc_kernel(tc, h_attn, norm2_w, ffn_wk, ffn_wv_bytes, ffn_wv_scale
             )
 
         def quantize_hn(i):
-            nc.vector.quantize_mx(
-                out=h_codes[:, i, :, :].rearrange("p q n -> p (q n)").bitcast(FP8X4),
-                scales=h_scales[:, i, :, :].rearrange("p q n -> p (q n)"),
-                in_=hn_grouped[i][:],
-            )
+            for q in range(Q):
+                nc.vector.quantize_mx(
+                    out=h_codes[:, q, i * P:(i + 1) * P].bitcast(FP8X4),
+                    scales=h_scales[:, q, i * P:(i + 1) * P],
+                    in_=hn_grouped[i][:, q * K_PASS:(q + 1) * K_PASS],
+                )
 
         nc.vector.memset(ones[:], 1.0)
         nc.vector.memset(gain_row[:], 0.0)
         make_identity(nc, ident_bf16[:])
         make_identity(nc, ident_f32[:])
+        warm = keep.tile([P, 1], F32, align_bytes=64, name="warm")
+        nc.scalar.activation(out=warm[:], in_=ones[:, 0:1], func=ACT.Abs_reciprocal_sqrt)
 
-        sync = [(load_h, 0), (load_scale,), (load_wv, 0, 0, HALF), (load_h, 1), (load_gain,), (load_h, 2),
-                (load_wk, 0, 1), (load_h, 3), (load_wv, 0, HALF, D), (load_wk, 0, 0), (load_wk, 1, 0), (load_wk, 1, 1)]
+        sync = [(load_scale, 0, 1), (load_wv, 0, 0, 1), (load_wv, 0, 1, 2), (load_h, 0), (load_wv, 0, 2, 4), (load_gain,), (load_h, 1),
+                (load_wk, 0, 1), (load_h, 2), (load_h, 3), (load_wk, 0, 0), (load_wk, 1, 0), (load_scale, 1, G), (load_wv, 1, 0, PACK),
+                (load_wk, 1, 1)]
         for g in range(2, G):
-            sync += [(load_wk, g, 0), (load_wk, g, 1), (load_wv, g - 1, 0, D)]
-        sync += [(load_wv, G - 1, 0, D)]
+            sync += [(load_wk, g, 0), (load_wk, g, 1), (load_wv, g, 0, PACK)]
         sync += [(store, 0, b) for b in range(4)] + [(store, 1, 0), (store, 1, 1), (store, 2, 0), (store, 2, 1)]
 
-        def planes(u):
-            return [(widen, u, False, t, t + 1) for t in range(PACK)]
+        def planes(u, on_vector=False):
+            return [(widen, u, on_vector, t, t + 1) for t in range(PACK)]
 
-        early = planes(upper[0])
+        early, fill = planes(upper[0]), planes(lower[1])
+        first, second = planes(lower[0], True), planes(upper[0], True)
         tensor = [(spread_gain,), (wk_on_tensor, 0, 1, 0), (turn_hn, 0), (wk_on_tensor, 0, 1, 1), (turn_hn, 1),
-                  (wk_on_tensor, 1, 0, 0), (turn_hn, 2), (wk_on_tensor, 1, 0, 1)]
-        scalar = [(sum_squares, 0), (sum_squares, 1), (root, 0), (sum_squares, 2), (root, 1), (sum_squares, 3), (root, 2),
-                  early[0], (root, 3), early[1], (wk_out, 0, 1, 0), (hn_out, 0), early[2], (wk_out, 0, 1, 1), (hn_out, 1), early[3],
-                  (wk_out, 1, 0, 0), (hn_out, 2), (wk_out, 1, 0, 1)]
-        vector = [(widen, lower[0], True, 0, 4), (wv_on_vector, lower[0]), (normalize, 0), (normalize, 1), (quantize_wv, lower[0]),
-                  (wk_on_vector, 0, 0), (quantize_hn, 0), (normalize, 2), (quantize_wk, 0, 0), (quantize_wk, 0, 1), (quantize_hn, 1),
-                  (normalize, 3), (wk_on_vector, 1, 1), (quantize_hn, 2), (quantize_wk, 1, 0), (quantize_wk, 1, 1), (quantize_hn, 3)]
+                  (wk_on_tensor, 1, 0, 0), (wk_on_tensor, 1, 0, 1)]
+        scalar = [early[0], (sum_squares, 0), early[3], (root, 0), (sum_squares, 1), (sum_squares, 2), (root, 1), (sum_squares, 3), (root, 2),
+                  (wk_out, 0, 1, 0), (root, 3), (hn_out, 0), (wk_out, 0, 1, 1), (hn_out, 1), fill[0], (wk_out, 1, 0, 0), fill[1],
+                  (wk_out, 1, 0, 1)]
+        vector = first[:2] + second[1:2] + first[2:] + second[2:3] + [
+                  (wv_on_vector, lower[0]), (normalize, 0), (quantize_wv, lower[0]),
+                  (normalize, 1), (wk_on_vector, 0, 0), (quantize_hn, 0), (quantize_wk, 0, 1), (quantize_hn, 1),
+                  (quantize_wk, 0, 0), (normalize, 2), (normalize, 3), (wk_on_vector, 1, 1), (quantize_hn, 2), (quantize_wk, 1, 0),
+                  (quantize_wk, 1, 1), (quantize_hn, 3)]
         lower_products = [(second_product, 0, g, i, i + 1) for g in range(G) for i in range(NT)]
-        a, b, c = upper[2], upper[3], upper[4]
+        a, b = upper[3], upper[4]
         taken = 0
+        rest = fill[2:]
         for g in range(G):
             if g + 2 < G:
                 mm = [[(wk_on_tensor, g + 2, 0, half)] for half in range(2)]
                 fill = [[(wk_out, g + 2, 0, half)] for half in range(2)]
             elif g == G - 2:
-                mm = [[], []]
-                fill = [planes(a)[:2], planes(a)[2:]]
+                mm = [[(wv_on_tensor, upper[0], half)] for half in range(2)]
+                fill = [[(wv_out, upper[0], half)] + planes(a)[2 * half:2 * half + 2] for half in range(2)]
             else:
                 mm = [[(wv_on_tensor, a, half)] for half in range(2)]
-                fill = [[(wv_out, a, half), planes(b)[half]] for half in range(2)]
+                fill = [planes(b)[:2] + [(wv_out, a, 0)], [(wv_out, a, 1)]]
             tensor += [(first_product, g, 0), (first_product, g, 1)]
             scalar += [(rectify, g, 0), (rectify, g, 1)]
             if g == 0:
-                tensor += [(turn_hn, 3)]
-                scalar += [(hn_out, 3)]
+                tensor += [(turn_hn, 2), (turn_hn, 3)]
+                scalar += [rest[0], (hn_out, 2), rest[1], (hn_out, 3)]
             tensor += mm[0] + [(first_product, g, 2), (first_product, g, 3)] + mm[1]
             scalar += fill[0] + [(square, g, 0), (rectify, g, 2), (rectify, g, 3)] + fill[1] + [(square, g, 1)]
             upto = max(0, min(NT * (g - 1), taken + PACE))
@@ -338,36 +351,27 @@ def tile_block_pc_kernel(tc, h_attn, norm2_w, ffn_wk, ffn_wv_bytes, ffn_wv_scale
             taken = upto
             if g + 2 < G:
                 u = lower[g + 1]
-                vector += [(wk_on_vector, g + 2, 1), (widen, u, True, 0, 4), (quantize_wk, g + 2, 1), (quantize_wk, g + 2, 0),
+                vector += [(wk_on_vector, g + 2, 1), (widen, lower[g + 2], True, 0, 4), (quantize_wk, g + 2, 1), (quantize_wk, g + 2, 0),
                            (wv_on_vector, u), (quantize_k, g), (quantize_wv, u)]
             elif g == G - 2:
-                vector += [(widen, lower[G - 1], True, 0, 4), (wv_on_vector, upper[0]), (wv_on_vector, lower[G - 1]), (quantize_k, g),
-                           (quantize_wv, upper[0]), (widen, upper[1], True, 0, 4), (quantize_wv, lower[G - 1])]
+                vector += [(wv_on_vector, lower[G - 1]), (widen, upper[1], True, 0, 4), (quantize_wv, lower[G - 1]), (wv_on_vector, upper[1]),
+                           (quantize_wv, upper[0]), (quantize_k, g), (widen, upper[2], True, 0, 4), (quantize_wv, upper[1])]
             else:
-                vector += [(wv_on_vector, upper[1]), (quantize_wv, a), (quantize_k, g), (quantize_wv, upper[1])]
-        done = [G, 0, 0]
-
-        def products(upto, slices):
-            jobs = []
-            for sl in slices:
-                jobs += [(second_product, sl, g, 0, NT) for g in range(done[sl], upto[sl])]
-                done[sl] = max(done[sl], upto[sl])
-            return jobs
+                vector += [(wv_on_vector, upper[2]), (quantize_wv, a), (quantize_wv, upper[2]), (quantize_k, g)]
+        def products(sl, groups):
+            return [(second_product, sl, g, 0, NT) for g in groups]
 
         todo = upper[5:]
-        scalar += planes(b)[2:] + planes(c) + planes(todo[0]) + [(wv_out, b, 0), (wv_out, b, 1)]
-        for u in todo[1:]:
-            scalar += planes(u)
-        tensor += lower_products[taken:] + [(wv_on_tensor, b, 0), (wv_on_tensor, b, 1)]
-        tensor += products([G, 3, 3], (1, 2)) + products([G, 5, 5], (1, 2))
-        vector += [(finish, 0, 0), (finish, 0, 1), (finish, 0, 2), (wv_on_vector, c), (finish, 0, 3), (wv_on_vector, todo[0]),
-                   (quantize_wv, c), (quantize_wv, b)]
-        for n in range(1, len(todo) - 1):
-            vector += [(wv_on_vector, todo[n]), (quantize_wv, todo[n - 1])]
-        vector += [(quantize_wv, todo[-2]), (wv_on_vector, todo[-1]), (finish, 1, 0), (quantize_wv, todo[-1]),
-                   (finish, 1, 1), (finish, 2, 0), (finish, 2, 1)]
-        for g, c0, w in todo:
-            tensor += products([g + 1 if c0 == SLICES[sl][0] else 0 for sl in range(3)], (1, 2))
+        scalar += planes(b)[2:] + planes(todo[0]) + planes(todo[1]) + planes(todo[2])[:2] + [(wv_out, b, 0)] + planes(todo[2])[2:]
+        scalar += [(wv_out, b, 1)] + planes(todo[3]) + planes(todo[4])
+        tensor += lower_products[taken:-NT] + products(1, (0, 1)) + lower_products[-NT:] + [(wv_on_tensor, b, 0), (wv_on_tensor, b, 1)]
+        tensor += products(1, (2, 3, 5)) + products(2, (0, 1, 2, 3)) + products(1, (6, 4)) + products(2, (4,)) + products(1, (7,))
+        tensor += products(2, (7, 5, 6))
+        vector += [(widen, todo[5], True, 0, 4), (finish, 0, 0), (wv_on_vector, todo[0]), (finish, 0, 1), (quantize_wv, todo[0]),
+                   (wv_on_vector, todo[1]), (finish, 0, 2), (quantize_wv, todo[1]), (finish, 0, 3),
+                   (wv_on_vector, todo[2]), (quantize_wv, b), (wv_on_vector, todo[5]), (quantize_wv, todo[2]),
+                   (wv_on_vector, todo[3]), (quantize_wv, todo[5]), (quantize_wv, todo[3]),
+                   (wv_on_vector, todo[4]), (finish, 1, 0), (quantize_wv, todo[4]), (finish, 1, 1), (finish, 2, 0), (finish, 2, 1)]
 
         def widened(u):
             return [job for job in vector + scalar if job[0] is widen and job[1] == u]
@@ -396,7 +400,9 @@ def tile_block_pc_kernel(tc, h_attn, norm2_w, ffn_wk, ffn_wv_bytes, ffn_wv_scale
             if f is quantize_wk:
                 return [(wk_out,) + a + (1,)] if (wk_out,) + a + (1,) in scalar else [(wk_on_vector,) + a]
             if f is widen:
-                return [(load_scale,)] + [j for j in sync if j[0] is load_wv and j[1] == a[0][0] and j[2] <= a[0][1] < j[3]]
+                return [j for j in sync if j[0] is load_scale and j[1] <= a[0][0] < j[2]] + [
+                    j for j in sync if j[0] is load_wv and j[1] == a[0][0] and j[2] < a[3]] + [
+                    j for j in widened(a[0]) if j[3] == 0 < a[2]]
             if f in (wv_on_vector, wv_on_tensor):
                 return widened(a[0])
             if f is wv_out:
@@ -404,7 +410,7 @@ def tile_block_pc_kernel(tc, h_attn, norm2_w, ffn_wk, ffn_wv_bytes, ffn_wv_scale
             if f is quantize_wv:
                 return grouped_by(a[0])
             if f is first_product:
-                return [(quantize_wk, a[0], q) for q in range(Q)] + [(quantize_hn, a[1])]
+                return [(quantize_wk, a[0], q) for q in range(Q)] + [(quantize_hn, a[1] // 2 * 2), (quantize_hn, a[1] // 2 * 2 + 1)]
             if f is rectify:
                 return [(first_product,) + a]
             if f is quantize_k:
@@ -414,7 +420,7 @@ def tile_block_pc_kernel(tc, h_attn, norm2_w, ffn_wk, ffn_wv_bytes, ffn_wv_scale
                 unit = [u for u in lower + upper if u[0] == a[1] and u[1] <= c0 < u[1] + u[2]][0]
                 return [(quantize_k, a[1]), (quantize_wv, unit)] + freed.get(a[:2], [])
             if f is finish:
-                return [j for j in tensor if j[:3] == (second_product, a[0], G - 1)]
+                return [j for j in tensor if j[:2] == (second_product, a[0]) and j[3] <= (a[1] + 1) * (HALF // SLICES[a[0]][1]) - 1 < j[4]]
             if f is store:
                 return [(finish,) + a]
             return []
@@ -422,13 +428,13 @@ def tile_block_pc_kernel(tc, h_attn, norm2_w, ffn_wk, ffn_wv_bytes, ffn_wv_scale
         def last_readers(job):
             f, a = job[0], job[1:]
             if f is load_wk:
-                return "wk_raw", 6, [j for j in tensor + vector if j[0] in (wk_on_tensor, wk_on_vector) and j[1:3] == a]
+                return "wk_raw", 5, [j for j in tensor + vector if j[0] in (wk_on_tensor, wk_on_vector) and j[1:3] == a]
             if f is wk_on_vector or (f is wk_out and a[2] == 0):
                 return "wk_grouped", 3, [(quantize_wk,) + a[:2]]
             if f is quantize_wk:
                 return "wk_codes", 6, [(first_product, a[0], NT - 1)]
             if f is widen and a[2] == 0:
-                return ("planes", a[1]), 2 if a[1] else 4, [
+                return ("planes", a[1]), 3 if a[1] else 4, [
                     j for j in tensor + vector if j[0] in (wv_on_tensor, wv_on_vector) and j[1] == a[0]]
             if f is wv_on_vector or (f is wv_out and a[1] == 0):
                 return "wv_grouped", 3, [(quantize_wv, a[0])]

@@ -27,7 +27,8 @@ HALF = D // 2
 SLICES = ((0, 512), (512, 256), (768, 256))
 WHOLE = 5
 V_UPPER = 2
-PACE = 3
+LAST = 5
+RUN = 2
 
 
 def tile_block_pc_kernel(tc, h_attn, norm2_w, ffn_wk, ffn_wv_bytes, ffn_wv_scale, out):
@@ -107,14 +108,14 @@ def tile_block_pc_kernel(tc, h_attn, norm2_w, ffn_wk, ffn_wv_bytes, ffn_wv_scale
 
         def wk_out(g, q, b):
             if b == 0:
-                wk_grouped[g, q] = stage3.tile([P, K_PASS * PACK], BF16, align_bytes=64, name="wk_grouped")
+                wk_grouped[g, q] = stage4.tile([P, K_PASS * PACK], BF16, align_bytes=64, name="wk_grouped")
             nc.scalar.copy(
                 out=wk_grouped[g, q][:].bitcast(F32).rearrange("p (t w) -> p t w", t=PACK)[:, :, 128 * b:128 * b + 128],
                 in_=banks["wk", g, q, b][:].rearrange("p t m j -> p t (m j)").bitcast(F32),
             )
 
         def wk_on_vector(g, q):
-            wk_grouped[g, q] = stage3.tile([P, K_PASS * PACK], BF16, align_bytes=64, name="wk_grouped")
+            wk_grouped[g, q] = stage4.tile([P, K_PASS * PACK], BF16, align_bytes=64, name="wk_grouped")
             nc.vector.tensor_copy(
                 out=wk_grouped[g, q][:].rearrange("p (t m j) -> p m j t", t=PACK, j=PACK),
                 in_=wk_raw[g, q][:].rearrange("p j (m t) -> p m j t", t=PACK),
@@ -145,8 +146,15 @@ def tile_block_pc_kernel(tc, h_attn, norm2_w, ffn_wk, ffn_wv_bytes, ffn_wv_scale
         def wv_on_vector(u):
             wv_grouped[u] = stage3.tile([P, u[2] * PACK], BF16, align_bytes=64, name="wv_grouped")
             nc.vector.tensor_copy(
-                out=wv_grouped[u][:].rearrange("p (c i t) -> p c t i", i=4, t=PACK),
-                in_=wv_planes[u][:].rearrange("p t (c i) -> p c t i", i=4),
+                out=wv_grouped[u][:].rearrange("p (c i t) -> p c t i", i=RUN, t=PACK),
+                in_=wv_planes[u][:].rearrange("p t (c i) -> p c t i", i=RUN),
+            )
+
+        def wv_on_scalar(u):
+            wv_grouped[u] = stage3.tile([P, u[2] * PACK], BF16, align_bytes=64, name="wv_grouped")
+            nc.scalar.copy(
+                out=wv_grouped[u][:].rearrange("p (c i t) -> p c t i", i=RUN, t=PACK),
+                in_=wv_planes[u][:].rearrange("p t (c i) -> p c t i", i=RUN),
             )
 
         def wv_on_tensor(u, b):
@@ -258,7 +266,7 @@ def tile_block_pc_kernel(tc, h_attn, norm2_w, ffn_wk, ffn_wv_bytes, ffn_wv_scale
                 gain_all.append(bank)
 
         def sum_squares(i):
-            squares = stage2.tile([P, D], BF16, align_bytes=64, name="squares")
+            squares = stage3.tile([P, D], BF16, align_bytes=64, name="k_grouped")
             nc.scalar.activation(out=squares[:], in_=h_sb[:, i, :], func=ACT.Square, accum_out=sumsq[:, i:i + 1])
 
         def root(i):
@@ -303,7 +311,7 @@ def tile_block_pc_kernel(tc, h_attn, norm2_w, ffn_wk, ffn_wv_bytes, ffn_wv_scale
         warm = keep.tile([P, 1], F32, align_bytes=64, name="warm")
         nc.scalar.activation(out=warm[:], in_=ones[:, 0:1], func=ACT.Abs_reciprocal_sqrt)
 
-        sync = [(load_scale, 0, 1), (load_wv, 0, 0, 1), (load_wv, 0, 1, 2), (load_h, 0), (load_wv, 0, 2, 4), (load_gain,), (load_h, 1),
+        sync = [(load_scale, 0, 1), (load_wv, 0, 0, 1), (load_wv, 0, 1, 2), (load_wv, 0, 2, 4), (load_h, 0), (load_gain,), (load_h, 1),
                 (load_wk, 0, 1), (load_h, 2), (load_h, 3), (load_wk, 0, 0), (load_wk, 1, 0), (load_scale, 1, G), (load_wv, 1, 0, PACK),
                 (load_wk, 1, 1)]
         for g in range(2, G):
@@ -314,20 +322,20 @@ def tile_block_pc_kernel(tc, h_attn, norm2_w, ffn_wk, ffn_wv_bytes, ffn_wv_scale
             return [(widen, u, on_vector, t, t + 1) for t in range(PACK)]
 
         early, fill = planes(upper[0]), planes(lower[1])
-        first, second = planes(lower[0], True), planes(upper[0], True)
         tensor = [(spread_gain,), (wk_on_tensor, 0, 1, 0), (turn_hn, 0), (wk_on_tensor, 0, 1, 1), (turn_hn, 1),
-                  (wk_on_tensor, 1, 0, 0), (wk_on_tensor, 1, 0, 1)]
-        scalar = [early[0], (sum_squares, 0), early[3], (root, 0), (sum_squares, 1), (sum_squares, 2), (root, 1), (sum_squares, 3), (root, 2),
-                  (wk_out, 0, 1, 0), (root, 3), (hn_out, 0), (wk_out, 0, 1, 1), (hn_out, 1), fill[0], (wk_out, 1, 0, 0), fill[1],
+                  (wk_on_tensor, 1, 0, 0), (turn_hn, 2), (wk_on_tensor, 1, 0, 1)]
+        scalar = [early[0], early[1], (sum_squares, 0), early[2], (root, 0), (sum_squares, 1), early[3], (root, 1), (sum_squares, 2),
+                  (sum_squares, 3), (root, 2),
+                  (wk_out, 0, 1, 0), (root, 3), (hn_out, 0), (wk_out, 0, 1, 1), (hn_out, 1), fill[0], (wk_out, 1, 0, 0), (hn_out, 2), fill[1],
                   (wk_out, 1, 0, 1)]
-        vector = first[:2] + second[1:2] + first[2:] + second[2:3] + [
-                  (wv_on_vector, lower[0]), (normalize, 0), (quantize_wv, lower[0]),
-                  (normalize, 1), (wk_on_vector, 0, 0), (quantize_hn, 0), (quantize_wk, 0, 1), (quantize_hn, 1),
-                  (quantize_wk, 0, 0), (normalize, 2), (normalize, 3), (wk_on_vector, 1, 1), (quantize_hn, 2), (quantize_wk, 1, 0),
+        vector = planes(lower[0], True) + [
+                  (wv_on_vector, lower[0]), (quantize_wv, lower[0]), (normalize, 0),
+                  (normalize, 1), (wk_on_vector, 0, 0), (normalize, 2), (quantize_hn, 0), (quantize_wk, 0, 0), (quantize_wk, 0, 1), (quantize_hn, 1),
+                  (normalize, 3), (wk_on_vector, 1, 1), (quantize_hn, 2), (quantize_wk, 1, 0),
                   (quantize_wk, 1, 1), (quantize_hn, 3)]
         lower_products = [(second_product, 0, g, i, i + 1) for g in range(G) for i in range(NT)]
         a, b = upper[3], upper[4]
-        taken = 0
+        todo = upper[5:]
         rest = fill[2:]
         for g in range(G):
             if g + 2 < G:
@@ -335,49 +343,50 @@ def tile_block_pc_kernel(tc, h_attn, norm2_w, ffn_wk, ffn_wv_bytes, ffn_wv_scale
                 fill = [[(wk_out, g + 2, 0, half)] for half in range(2)]
             elif g == G - 2:
                 mm = [[(wv_on_tensor, upper[0], half)] for half in range(2)]
-                fill = [[(wv_out, upper[0], half)] + planes(a)[2 * half:2 * half + 2] for half in range(2)]
+                fill = [[(wv_out, upper[0], half)] for half in range(2)]
             else:
-                mm = [[(wv_on_tensor, a, half)] for half in range(2)]
-                fill = [planes(b)[:2] + [(wv_out, a, 0)], [(wv_out, a, 1)]]
+                mm = [[], []]
+                fill = [planes(a)[:1], planes(a)[1:2]]
             tensor += [(first_product, g, 0), (first_product, g, 1)]
             scalar += [(rectify, g, 0), (rectify, g, 1)]
             if g == 0:
-                tensor += [(turn_hn, 2), (turn_hn, 3)]
-                scalar += [rest[0], (hn_out, 2), rest[1], (hn_out, 3)]
+                tensor += [(turn_hn, 3)]
+                scalar += [rest[0], (hn_out, 3), rest[1]]
             tensor += mm[0] + [(first_product, g, 2), (first_product, g, 3)] + mm[1]
             scalar += fill[0] + [(square, g, 0), (rectify, g, 2), (rectify, g, 3)] + fill[1] + [(square, g, 1)]
-            upto = max(0, min(NT * (g - 1), taken + PACE))
-            tensor += lower_products[taken:upto]
-            taken = upto
+            if g >= 2:
+                tensor += lower_products[NT * (g - 2):NT * (g - 1)]
             if g + 2 < G:
                 u = lower[g + 1]
                 vector += [(wk_on_vector, g + 2, 1), (widen, lower[g + 2], True, 0, 4), (quantize_wk, g + 2, 1), (quantize_wk, g + 2, 0),
                            (wv_on_vector, u), (quantize_k, g), (quantize_wv, u)]
             elif g == G - 2:
-                vector += [(wv_on_vector, lower[G - 1]), (widen, upper[1], True, 0, 4), (quantize_wv, lower[G - 1]), (wv_on_vector, upper[1]),
-                           (quantize_wv, upper[0]), (quantize_k, g), (widen, upper[2], True, 0, 4), (quantize_wv, upper[1])]
+                vector += [(wv_on_vector, lower[G - 1]), (quantize_k, g), (widen, upper[1], True, 0, 4), (quantize_wv, upper[0]),
+                           (wv_on_vector, upper[1]), (quantize_wv, lower[G - 1]), (quantize_wv, upper[1])]
             else:
-                vector += [(wv_on_vector, upper[2]), (quantize_wv, a), (quantize_wv, upper[2]), (quantize_k, g)]
+                vector += [(quantize_k, g), (widen, upper[2], True, 0, 4)]
         def products(sl, groups):
             return [(second_product, sl, g, 0, NT) for g in groups]
 
-        todo = upper[5:]
-        scalar += planes(b)[2:] + planes(todo[0]) + planes(todo[1]) + planes(todo[2])[:2] + [(wv_out, b, 0)] + planes(todo[2])[2:]
-        scalar += [(wv_out, b, 1)] + planes(todo[3]) + planes(todo[4])
-        tensor += lower_products[taken:-NT] + products(1, (0, 1)) + lower_products[-NT:] + [(wv_on_tensor, b, 0), (wv_on_tensor, b, 1)]
-        tensor += products(1, (2, 3, 5)) + products(2, (0, 1, 2, 3)) + products(1, (6, 4)) + products(2, (4,)) + products(1, (7,))
-        tensor += products(2, (7, 5, 6))
-        vector += [(widen, todo[5], True, 0, 4), (finish, 0, 0), (wv_on_vector, todo[0]), (finish, 0, 1), (quantize_wv, todo[0]),
-                   (wv_on_vector, todo[1]), (finish, 0, 2), (quantize_wv, todo[1]), (finish, 0, 3),
-                   (wv_on_vector, todo[2]), (quantize_wv, b), (wv_on_vector, todo[5]), (quantize_wv, todo[2]),
-                   (wv_on_vector, todo[3]), (quantize_wv, todo[5]), (quantize_wv, todo[3]),
-                   (wv_on_vector, todo[4]), (finish, 1, 0), (quantize_wv, todo[4]), (finish, 1, 1), (finish, 2, 0), (finish, 2, 1)]
+        scalar += planes(a)[2:] + planes(b) + [(wv_out, a, 0)] + planes(todo[0]) + [(wv_out, a, 1), (wv_out, b, 0)] + planes(todo[1])
+        scalar += [(wv_out, b, 1)]
+        for u in todo[2:LAST]:
+            scalar += planes(u)
+        tensor += lower_products[NT * (G - 2):-NT] + products(1, (0, 1)) + lower_products[-NT:]
+        tensor += [(wv_on_tensor, u, half) for u in (a, b) for half in range(2)]
+        tensor += products(1, (2, 3, 5)) + products(2, (0, 1)) + products(1, (4, 6)) + products(2, (2, 3)) + products(1, (7,))
+        tensor += products(2, (4, 7, 5, 6))
+        vector += [(finish, 0, 0), (wv_on_vector, upper[2]), (finish, 0, 1), (quantize_wv, upper[2]), (finish, 0, 2),
+                   (wv_on_vector, todo[0]), (quantize_wv, a), (quantize_wv, todo[0]), (finish, 0, 3), (wv_on_vector, todo[1]), (quantize_wv, b),
+                   (quantize_wv, todo[1]), (widen, todo[5], True, 0, 4), (wv_on_vector, todo[2]), (wv_on_vector, todo[5]),
+                   (quantize_wv, todo[2]), (wv_on_vector, todo[3]), (quantize_wv, todo[5]), (wv_on_vector, todo[4]),
+                   (quantize_wv, todo[3]), (quantize_wv, todo[4]), (finish, 1, 0), (finish, 1, 1), (finish, 2, 0), (finish, 2, 1)]
 
         def widened(u):
             return [job for job in vector + scalar if job[0] is widen and job[1] == u]
 
         def grouped_by(u):
-            return [job for job in vector + scalar if job[0] in (wv_on_vector, wv_out) and job[1] == u]
+            return [job for job in vector + scalar if job[0] in (wv_on_vector, wv_on_scalar, wv_out) and job[1] == u]
 
         def needs(job):
             f, a = job[0], job[1:]
@@ -403,7 +412,7 @@ def tile_block_pc_kernel(tc, h_attn, norm2_w, ffn_wk, ffn_wv_bytes, ffn_wv_scale
                 return [j for j in sync if j[0] is load_scale and j[1] <= a[0][0] < j[2]] + [
                     j for j in sync if j[0] is load_wv and j[1] == a[0][0] and j[2] < a[3]] + [
                     j for j in widened(a[0]) if j[3] == 0 < a[2]]
-            if f in (wv_on_vector, wv_on_tensor):
+            if f in (wv_on_vector, wv_on_scalar, wv_on_tensor):
                 return widened(a[0])
             if f is wv_out:
                 return [(wv_on_tensor,) + a]
@@ -430,13 +439,13 @@ def tile_block_pc_kernel(tc, h_attn, norm2_w, ffn_wk, ffn_wv_bytes, ffn_wv_scale
             if f is load_wk:
                 return "wk_raw", 5, [j for j in tensor + vector if j[0] in (wk_on_tensor, wk_on_vector) and j[1:3] == a]
             if f is wk_on_vector or (f is wk_out and a[2] == 0):
-                return "wk_grouped", 3, [(quantize_wk,) + a[:2]]
+                return "wk_grouped", 4, [(quantize_wk,) + a[:2]]
             if f is quantize_wk:
                 return "wk_codes", 6, [(first_product, a[0], NT - 1)]
             if f is widen and a[2] == 0:
                 return ("planes", a[1]), 3 if a[1] else 4, [
-                    j for j in tensor + vector if j[0] in (wv_on_tensor, wv_on_vector) and j[1] == a[0]]
-            if f is wv_on_vector or (f is wv_out and a[1] == 0):
+                    j for j in tensor + vector + scalar if j[0] in (wv_on_tensor, wv_on_vector, wv_on_scalar) and j[1] == a[0]]
+            if f in (wv_on_vector, wv_on_scalar) or (f is wv_out and a[1] == 0):
                 return "wv_grouped", 3, [(quantize_wv, a[0])]
             if f is square and a[1] == 0:
                 return "k_grouped", 3, [(quantize_k, a[0])]

@@ -27,7 +27,7 @@ HALF = D // 2
 SLICES = ((0, 512), (512, 256), (768, 256))
 WHOLE = 5
 V_UPPER = 2
-LAST = 5
+LAST = 4
 RUN = 2
 
 
@@ -40,8 +40,8 @@ def tile_block_pc_kernel(tc, h_attn, norm2_w, ffn_wk, ffn_wv_bytes, ffn_wv_scale
     scale_v = ffn_wv_scale.rearrange("(g p t) o -> p g (t o)", p=P, t=PACK)
 
     lower = [(g, 0, HALF) for g in range(G)]
-    upper = [(g, HALF, HALF) for g in range(WHOLE)]
-    upper += [(g, 512, 256) for g in range(WHOLE, G)] + [(g, 768, 256) for g in range(WHOLE, G)]
+    upper = [(g, HALF, HALF) for g in (0, 1, 2, 3, G - 1)]
+    upper += [(g, 512, 256) for g in (4, 5, 6)] + [(g, 768, 256) for g in (4, 5, 6)]
 
     with ExitStack() as ctx:
         keep = ctx.enter_context(tc.tile_pool(name="keep", bufs=1))
@@ -117,18 +117,18 @@ def tile_block_pc_kernel(tc, h_attn, norm2_w, ffn_wk, ffn_wv_bytes, ffn_wv_scale
         def wk_on_vector(g, q):
             wk_grouped[g, q] = stage4.tile([P, K_PASS * PACK], BF16, align_bytes=64, name="wk_grouped")
             nc.vector.tensor_copy(
-                out=wk_grouped[g, q][:].rearrange("p (t m j) -> p m j t", t=PACK, j=PACK),
-                in_=wk_raw[g, q][:].rearrange("p j (m t) -> p m j t", t=PACK),
+                out=wk_grouped[g, q][:].rearrange("p (u e m j) -> p m u j e", u=2, e=2, j=PACK),
+                in_=wk_raw[g, q][:].rearrange("p j (m u e) -> p m u j e", u=2, e=2),
             )
 
         def quantize_wk(g, q):
-            wk_codes[g, q] = stage6.tile([P, K_PASS], U32, align_bytes=64, name="wk_codes")
-            wk_scales[g, q] = stage6.tile([P, K_PASS], U8, align_bytes=64, name="wk_scales")
+            wk_codes[g, q] = stage6.tile([P, K_PASS], U32, align_bytes=64, name="wk_codes", bufs=5)
+            wk_scales[g, q] = stage6.tile([P, K_PASS], U8, align_bytes=64, name="wk_scales", bufs=5)
             nc.vector.quantize_mx(
                 out=wk_codes[g, q][:].bitcast(FP8X4), scales=wk_scales[g, q][:], in_=wk_grouped[g, q][:])
 
         wv_planes, wv_grouped = {}, {}
-        planes_pool = {True: stage3, False: stage4}
+        planes_pool = {True: stage4, False: stage4}
 
         def widen(u, on_vector, first, last):
             g, c0, w = u
@@ -225,7 +225,7 @@ def tile_block_pc_kernel(tc, h_attn, norm2_w, ffn_wk, ffn_wv_bytes, ffn_wv_scale
 
         acc, passes, result = {}, {}, {}
         bank_of = {(0, 0): "acc0", (0, 1): "acc1", (0, 2): "acc2", (0, 3): "acc3",
-                   (1, 0): "work2", (1, 1): "work3", (2, 0): "acc0", (2, 1): "acc1"}
+                   (1, 0): "work0", (1, 1): "work1", (2, 0): "acc0", (2, 1): "acc1"}
 
         def second_product(sl, g, first, last):
             c0, w = SLICES[sl]
@@ -249,7 +249,7 @@ def tile_block_pc_kernel(tc, h_attn, norm2_w, ffn_wk, ffn_wv_bytes, ffn_wv_scale
             c0, w = SLICES[sl]
             share = HALF // w
             tiles = slice(b * share, (b + 1) * share)
-            result[sl, b] = stage4.tile([P, share, w], F32, align_bytes=64, name="result")
+            result[sl, b] = stage6.tile([P, share, w], F32, align_bytes=64, name="result", bufs=5)
             nc.vector.tensor_tensor(out=result[sl, b][:], in0=acc[sl, b][:], in1=h_sb[:, tiles, c0:c0 + w], op=ALU.add)
 
         def store(sl, b):
@@ -311,76 +311,77 @@ def tile_block_pc_kernel(tc, h_attn, norm2_w, ffn_wk, ffn_wv_bytes, ffn_wv_scale
         warm = keep.tile([P, 1], F32, align_bytes=64, name="warm")
         nc.scalar.activation(out=warm[:], in_=ones[:, 0:1], func=ACT.Abs_reciprocal_sqrt)
 
-        sync = [(load_scale, 0, 1), (load_wv, 0, 0, 1), (load_wv, 0, 1, 2), (load_wv, 0, 2, 4), (load_h, 0), (load_gain,), (load_h, 1),
+        sync = [(load_scale, 0, 1), (load_wv, 0, 0, 1), (load_wv, 0, 1, 2), (load_wv, 0, 2, 3), (load_wv, 0, 3, 4), (load_h, 0), (load_gain,), (load_h, 1),
                 (load_wk, 0, 1), (load_h, 2), (load_h, 3), (load_wk, 0, 0), (load_wk, 1, 0), (load_scale, 1, G), (load_wv, 1, 0, PACK),
                 (load_wk, 1, 1)]
         for g in range(2, G):
             sync += [(load_wk, g, 0), (load_wk, g, 1), (load_wv, g, 0, PACK)]
-        sync += [(store, 0, b) for b in range(4)] + [(store, 1, 0), (store, 1, 1), (store, 2, 0), (store, 2, 1)]
+        sync += [(store, 0, b) for b in range(4)] + [(store, 2, 0), (store, 2, 1), (store, 1, 0), (store, 1, 1)]
 
         def planes(u, on_vector=False):
             return [(widen, u, on_vector, t, t + 1) for t in range(PACK)]
 
         early, fill = planes(upper[0]), planes(lower[1])
         tensor = [(spread_gain,), (wk_on_tensor, 0, 1, 0), (turn_hn, 0), (wk_on_tensor, 0, 1, 1), (turn_hn, 1),
-                  (wk_on_tensor, 1, 0, 0), (turn_hn, 2), (wk_on_tensor, 1, 0, 1)]
+                  (wk_on_tensor, 1, 0, 0), (turn_hn, 2), (wk_on_tensor, 1, 0, 1), (turn_hn, 3)]
         scalar = [early[0], early[1], (sum_squares, 0), early[2], (root, 0), (sum_squares, 1), early[3], (root, 1), (sum_squares, 2),
                   (sum_squares, 3), (root, 2),
-                  (wk_out, 0, 1, 0), (root, 3), (hn_out, 0), (wk_out, 0, 1, 1), (hn_out, 1), fill[0], (wk_out, 1, 0, 0), (hn_out, 2), fill[1],
-                  (wk_out, 1, 0, 1)]
+                  (wk_out, 0, 1, 0), (root, 3), (hn_out, 0), (wk_out, 0, 1, 1), (hn_out, 1), fill[0], (wk_out, 1, 0, 0), fill[1], (hn_out, 2),
+                  (wk_out, 1, 0, 1), (hn_out, 3)] + fill[2:]
         vector = planes(lower[0], True) + [
                   (wv_on_vector, lower[0]), (quantize_wv, lower[0]), (normalize, 0),
-                  (normalize, 1), (wk_on_vector, 0, 0), (normalize, 2), (quantize_hn, 0), (quantize_wk, 0, 0), (quantize_wk, 0, 1), (quantize_hn, 1),
-                  (normalize, 3), (wk_on_vector, 1, 1), (quantize_hn, 2), (quantize_wk, 1, 0),
-                  (quantize_wk, 1, 1), (quantize_hn, 3)]
+                  (normalize, 1), (wk_on_vector, 0, 0), (normalize, 2), (quantize_hn, 0), (normalize, 3), (quantize_wk, 0, 0), (quantize_wk, 0, 1),
+                  (quantize_hn, 1), (wk_on_vector, 1, 1), (quantize_hn, 2), (quantize_hn, 3), (quantize_wk, 1, 0), (quantize_wk, 1, 1)]
         lower_products = [(second_product, 0, g, i, i + 1) for g in range(G) for i in range(NT)]
-        a, b = upper[3], upper[4]
-        todo = upper[5:]
-        rest = fill[2:]
+        a, d = upper[3], upper[4]
+        left, right = upper[5:8], upper[8:11]
         for g in range(G):
             if g + 2 < G:
                 mm = [[(wk_on_tensor, g + 2, 0, half)] for half in range(2)]
                 fill = [[(wk_out, g + 2, 0, half)] for half in range(2)]
+                if g < 2:
+                    mm[1] += [(wv_on_tensor, upper[0], g)]
+                    fill[1] += [(wv_out, upper[0], g)]
+                if g == G - 3:
+                    fill[0] += planes(a)
             elif g == G - 2:
-                mm = [[(wv_on_tensor, upper[0], half)] for half in range(2)]
-                fill = [[(wv_out, upper[0], half)] for half in range(2)]
+                mm = [[(wv_on_tensor, a, half)] for half in range(2)]
+                fill = [[(wv_out, a, half)] for half in range(2)]
             else:
-                mm = [[], []]
-                fill = [planes(a)[:1], planes(a)[1:2]]
+                mm = [[(wv_on_tensor, upper[1], half)] for half in range(2)]
+                fill = [[(wv_out, upper[1], half)] for half in range(2)]
             tensor += [(first_product, g, 0), (first_product, g, 1)]
             scalar += [(rectify, g, 0), (rectify, g, 1)]
-            if g == 0:
-                tensor += [(turn_hn, 3)]
-                scalar += [rest[0], (hn_out, 3), rest[1]]
             tensor += mm[0] + [(first_product, g, 2), (first_product, g, 3)] + mm[1]
             scalar += fill[0] + [(square, g, 0), (rectify, g, 2), (rectify, g, 3)] + fill[1] + [(square, g, 1)]
-            if g >= 2:
-                tensor += lower_products[NT * (g - 2):NT * (g - 1)]
+            if g >= 1:
+                tensor += lower_products[NT * (g - 1):NT * g]
             if g + 2 < G:
                 u = lower[g + 1]
-                vector += [(wk_on_vector, g + 2, 1), (widen, lower[g + 2], True, 0, 4), (quantize_wk, g + 2, 1), (quantize_wk, g + 2, 0),
-                           (wv_on_vector, u), (quantize_k, g), (quantize_wv, u)]
+                vector += [(wk_on_vector, g + 2, 1), (widen, lower[g + 2], True, 0, 4), (quantize_wk, g + 2, 1)]
+                vector += [(wv_on_vector, u), (quantize_wk, g + 2, 0), (quantize_wv, u), (quantize_k, g)]
+                if g == 1:
+                    vector += [(quantize_wv, upper[0])]
             elif g == G - 2:
-                vector += [(wv_on_vector, lower[G - 1]), (quantize_k, g), (widen, upper[1], True, 0, 4), (quantize_wv, upper[0]),
-                           (wv_on_vector, upper[1]), (quantize_wv, lower[G - 1]), (quantize_wv, upper[1])]
+                vector += [(widen, upper[1], True, 0, 4), (wv_on_vector, lower[G - 1]), (widen, upper[2], True, 0, 4),
+                           (quantize_wv, lower[G - 1]), (quantize_wv, a), (quantize_k, g)]
             else:
-                vector += [(quantize_k, g), (widen, upper[2], True, 0, 4)]
+                vector += [(widen, d, True, 0, 4), (widen, right[2], True, 0, 4), (wv_on_vector, d), (wv_on_vector, right[2]),
+                           (quantize_wv, d), (quantize_wv, upper[1]), (quantize_wv, right[2]), (quantize_k, g)]
         def products(sl, groups):
             return [(second_product, sl, g, 0, NT) for g in groups]
 
-        scalar += planes(a)[2:] + planes(b) + [(wv_out, a, 0)] + planes(todo[0]) + [(wv_out, a, 1), (wv_out, b, 0)] + planes(todo[1])
-        scalar += [(wv_out, b, 1)]
-        for u in todo[2:LAST]:
+        late = right[:2] + left
+        scalar += planes(late[0]) + [(wv_out, upper[2], 0), (wv_out, upper[2], 1)]
+        for u in late[1:]:
             scalar += planes(u)
-        tensor += lower_products[NT * (G - 2):-NT] + products(1, (0, 1)) + lower_products[-NT:]
-        tensor += [(wv_on_tensor, u, half) for u in (a, b) for half in range(2)]
-        tensor += products(1, (2, 3, 5)) + products(2, (0, 1)) + products(1, (4, 6)) + products(2, (2, 3)) + products(1, (7,))
-        tensor += products(2, (4, 7, 5, 6))
-        vector += [(finish, 0, 0), (wv_on_vector, upper[2]), (finish, 0, 1), (quantize_wv, upper[2]), (finish, 0, 2),
-                   (wv_on_vector, todo[0]), (quantize_wv, a), (quantize_wv, todo[0]), (finish, 0, 3), (wv_on_vector, todo[1]), (quantize_wv, b),
-                   (quantize_wv, todo[1]), (widen, todo[5], True, 0, 4), (wv_on_vector, todo[2]), (wv_on_vector, todo[5]),
-                   (quantize_wv, todo[2]), (wv_on_vector, todo[3]), (quantize_wv, todo[5]), (wv_on_vector, todo[4]),
-                   (quantize_wv, todo[3]), (quantize_wv, todo[4]), (finish, 1, 0), (finish, 1, 1), (finish, 2, 0), (finish, 2, 1)]
+        tensor += [(wv_on_tensor, upper[2], half) for half in range(2)]
+        tensor += products(1, (0, 3)) + lower_products[-NT:]
+        tensor += products(1, (1, 7)) + products(2, (0, 1, 3, 6, 7, 4, 2, 5)) + products(1, (2, 4, 5, 6))
+        vector += [(wv_on_vector, late[0]), (finish, 0, 0), (quantize_wv, late[0]), (finish, 0, 1), (quantize_wv, upper[2]),
+                   (wv_on_vector, late[1]), (finish, 0, 2), (quantize_wv, late[1]), (wv_on_vector, late[2]), (finish, 0, 3),
+                   (quantize_wv, late[2]), (wv_on_vector, late[3]), (wv_on_vector, late[4]), (quantize_wv, late[3]),
+                   (quantize_wv, late[4]), (finish, 2, 0), (finish, 2, 1), (finish, 1, 0), (finish, 1, 1)]
 
         def widened(u):
             return [job for job in vector + scalar if job[0] is widen and job[1] == u]
@@ -441,9 +442,9 @@ def tile_block_pc_kernel(tc, h_attn, norm2_w, ffn_wk, ffn_wv_bytes, ffn_wv_scale
             if f is wk_on_vector or (f is wk_out and a[2] == 0):
                 return "wk_grouped", 4, [(quantize_wk,) + a[:2]]
             if f is quantize_wk:
-                return "wk_codes", 6, [(first_product, a[0], NT - 1)]
+                return "wk_codes", 5, [(first_product, a[0], NT - 1)]
             if f is widen and a[2] == 0:
-                return ("planes", a[1]), 3 if a[1] else 4, [
+                return ("planes", a[1]), 4, [
                     j for j in tensor + vector + scalar if j[0] in (wv_on_tensor, wv_on_vector, wv_on_scalar) and j[1] == a[0]]
             if f in (wv_on_vector, wv_on_scalar) or (f is wv_out and a[1] == 0):
                 return "wv_grouped", 3, [(quantize_wv, a[0])]
@@ -454,12 +455,12 @@ def tile_block_pc_kernel(tc, h_attn, norm2_w, ffn_wk, ffn_wv_bytes, ffn_wv_scale
             if f is hn_out:
                 return "hn_grouped", 2, [(quantize_hn, a[0])]
             if f is finish:
-                return "result", 4, [(store,) + a]
+                return "result", 5, [(store,) + a]
             return None, 0, []
 
         emptied_by = {wk_on_tensor: wk_out, wv_on_tensor: wv_out, first_product: rectify, turn_hn: hn_out}
         bank_user = {}
-        freed = {(0, 0): [(normalize, NT - 1)], (1, 0): [(rectify, G - 1, NT - 1)], (2, 0): [(finish, 0, 0), (finish, 0, 1)]}
+        freed = {(0, 0): [(normalize, NT - 1)], (1, 0): [(rectify, G - 1, NT - 1), (wv_out, upper[1], 1)], (2, 0): [(finish, 0, 0), (finish, 0, 1)]}
         written, rings = set(), {}
         queues = [sync, tensor, scalar, vector]
         at = [0] * len(queues)
@@ -475,7 +476,7 @@ def tile_block_pc_kernel(tc, h_attn, norm2_w, ffn_wk, ffn_wv_bytes, ffn_wv_scale
                 if ring is not None and len(rings.setdefault(ring, [])) >= depth:
                     wanted += rings[ring][-depth]
                 if job[0] in emptied_by:
-                    bank = count % (2 if (rectify, G - 1, NT - 1) in written else 4)
+                    bank = count % 4
                     wanted += bank_user.get(bank, [])
                 if all(w in written for w in wanted):
                     if ring is not None:

@@ -324,12 +324,12 @@ def tile_block_pc_kernel(tc, h_attn, norm2_w, ffn_wk, ffn_wv_bytes, ffn_wv_scale
         early, fill = planes(upper[0]), planes(lower[1])
         tensor = [(spread_gain,), (wk_on_tensor, 0, 1, 0), (turn_hn, 0), (wk_on_tensor, 0, 1, 1), (turn_hn, 1),
                   (wk_on_tensor, 1, 0, 0), (turn_hn, 2), (wk_on_tensor, 1, 0, 1), (turn_hn, 3)]
-        scalar = [early[0], early[1], (sum_squares, 0), early[2], (root, 0), (sum_squares, 1), early[3], (root, 1), (sum_squares, 2),
+        scalar = [early[0], early[1], (sum_squares, 0), (root, 0), (sum_squares, 1), (root, 1), (sum_squares, 2),
                   (sum_squares, 3), (root, 2),
                   (wk_out, 0, 1, 0), (root, 3), (hn_out, 0), (wk_out, 0, 1, 1), (hn_out, 1), fill[0], (wk_out, 1, 0, 0), fill[1], (hn_out, 2),
                   (wk_out, 1, 0, 1), (hn_out, 3)] + fill[2:]
         vector = planes(lower[0], True) + [
-                  (wv_on_vector, lower[0]), (quantize_wv, lower[0]), (normalize, 0),
+                  (widen, upper[0], True, 2, 3), (wv_on_vector, lower[0]), (widen, upper[0], True, 3, 4), (quantize_wv, lower[0]), (normalize, 0),
                   (normalize, 1), (wk_on_vector, 0, 0), (normalize, 2), (quantize_hn, 0), (normalize, 3), (quantize_wk, 0, 0), (quantize_wk, 0, 1),
                   (quantize_hn, 1), (wk_on_vector, 1, 1), (quantize_hn, 2), (quantize_hn, 3), (quantize_wk, 1, 0), (quantize_wk, 1, 1)]
         lower_products = [(second_product, 0, g, i, i + 1) for g in range(G) for i in range(NT)]
@@ -343,10 +343,11 @@ def tile_block_pc_kernel(tc, h_attn, norm2_w, ffn_wk, ffn_wv_bytes, ffn_wv_scale
                     mm[1] += [(wv_on_tensor, upper[0], g)]
                     fill[1] += [(wv_out, upper[0], g)]
                 if g == G - 3:
-                    fill[0] += planes(a)
+                    mm = [mm[half] + [(wv_on_tensor, lower[G - 2], half)] for half in range(2)]
+                    fill = [fill[half] + [planes(a)[half], (wv_out, lower[G - 2], half)] for half in range(2)]
             elif g == G - 2:
-                mm = [[(wv_on_tensor, a, half)] for half in range(2)]
-                fill = [[(wv_out, a, half)] for half in range(2)]
+                mm = [[(wv_on_tensor, lower[G - 1], half)] for half in range(2)]
+                fill = [[(wv_out, lower[G - 1], half)] for half in range(2)]
             else:
                 mm = [[(wv_on_tensor, upper[1], half)] for half in range(2)]
                 fill = [[(wv_out, upper[1], half)] for half in range(2)]
@@ -359,29 +360,29 @@ def tile_block_pc_kernel(tc, h_attn, norm2_w, ffn_wk, ffn_wv_bytes, ffn_wv_scale
             if g + 2 < G:
                 u = lower[g + 1]
                 vector += [(wk_on_vector, g + 2, 1), (widen, lower[g + 2], True, 0, 4), (quantize_wk, g + 2, 1)]
-                vector += [(wv_on_vector, u), (quantize_wk, g + 2, 0), (quantize_wv, u), (quantize_k, g)]
+                between = (wv_on_vector, u) if g < G - 3 else (widen, upper[1], True, 0, 4)
+                vector += [between, (quantize_wk, g + 2, 0), (quantize_wv, u), (quantize_k, g)]
                 if g == 1:
                     vector += [(quantize_wv, upper[0])]
             elif g == G - 2:
-                vector += [(widen, upper[1], True, 0, 4), (wv_on_vector, lower[G - 1]), (widen, upper[2], True, 0, 4),
-                           (quantize_wv, lower[G - 1]), (quantize_wv, a), (quantize_k, g)]
+                vector += [(widen, upper[2], True, 0, 4), (widen, d, True, 0, 4), (wv_on_vector, upper[2]),
+                           (quantize_wv, lower[G - 1]), (quantize_wv, upper[2]), (quantize_k, g), (wv_on_vector, d)]
             else:
-                vector += [(widen, d, True, 0, 4), (widen, right[2], True, 0, 4), (wv_on_vector, d), (wv_on_vector, right[2]),
-                           (quantize_wv, d), (quantize_wv, upper[1]), (quantize_wv, right[2]), (quantize_k, g)]
+                vector += [(widen, a, True, 2, 4), (widen, right[2], True, 0, 4), (quantize_wv, d), (wv_on_vector, a),
+                           (quantize_wv, upper[1]), (quantize_k, g), (wv_on_vector, right[2]), (quantize_wv, a), (quantize_wv, right[2])]
         def products(sl, groups):
             return [(second_product, sl, g, 0, NT) for g in groups]
 
-        late = right[:2] + left
-        scalar += planes(late[0]) + [(wv_out, upper[2], 0), (wv_out, upper[2], 1)]
+        late = [a] + right[:2] + left
         for u in late[1:]:
             scalar += planes(u)
-        tensor += [(wv_on_tensor, upper[2], half) for half in range(2)]
-        tensor += products(1, (0, 3)) + lower_products[-NT:]
-        tensor += products(1, (1, 7)) + products(2, (0, 1, 3, 6, 7, 4, 2, 5)) + products(1, (2, 4, 5, 6))
-        vector += [(wv_on_vector, late[0]), (finish, 0, 0), (quantize_wv, late[0]), (finish, 0, 1), (quantize_wv, upper[2]),
-                   (wv_on_vector, late[1]), (finish, 0, 2), (quantize_wv, late[1]), (wv_on_vector, late[2]), (finish, 0, 3),
-                   (quantize_wv, late[2]), (wv_on_vector, late[3]), (wv_on_vector, late[4]), (quantize_wv, late[3]),
-                   (quantize_wv, late[4]), (finish, 2, 0), (finish, 2, 1), (finish, 1, 0), (finish, 1, 1)]
+        scalar += [(wv_on_scalar, late[4])]
+        tensor += products(1, (0, 2, 1)) + lower_products[-NT:]
+        tensor += products(1, (7, 3)) + products(2, (0, 1, 2, 7, 3, 6, 4, 5)) + products(1, (4, 6, 5))
+        vector += [(finish, 0, 0), (finish, 0, 1), (wv_on_vector, late[1]), (wv_on_vector, late[2]), (quantize_wv, late[1]),
+                   (quantize_wv, late[2]), (wv_on_vector, late[3]), (finish, 0, 2), (quantize_wv, late[3]),
+                   (wv_on_vector, late[5]), (finish, 0, 3), (quantize_wv, late[5]), (quantize_wv, late[4]),
+                   (finish, 2, 0), (finish, 2, 1), (finish, 1, 0), (finish, 1, 1)]
 
         def widened(u):
             return [job for job in vector + scalar if job[0] is widen and job[1] == u]

@@ -82,8 +82,9 @@ def tile_block_pc_kernel(tc, h_attn, norm2_w, ffn_wk, ffn_wv_bytes, ffn_wv_scale
         def load_wv(g, first, last):
             nc.sync.dma_start(out=wv_bytes[:, g, first:last, :], in_=wv_v[g][:, first:last, :])
 
-        def load_scale(first, last):
-            nc.sync.dma_start(out=wv_scale[:, first:last, 0:PACK], in_=scale_v[:, first:last, :])
+        def load_scale():
+            nc.scalar.dma_start(out=wv_scale[:, 0:1, 0:PACK], in_=scale_v[:, 0:1, :])
+            nc.scalar.dma_start(out=wv_scale[:, 1:G, 0:PACK], in_=scale_v[:, 1:G, :])
 
         def load_gain():
             nc.sync.dma_start(out=gain_row[0:1, :], in_=norm2_w.rearrange("(o d) -> o d", o=1))
@@ -275,18 +276,22 @@ def tile_block_pc_kernel(tc, h_attn, norm2_w, ffn_wk, ffn_wv_bytes, ffn_wv_scale
 
         def normalize(i):
             hn[i] = stage2.tile([P, D], BF16, align_bytes=64, name="hn")
-            for c in range(2):
-                cols = slice(c * 512, (c + 1) * 512)
-                nc.vector.scalar_tensor_tensor(
-                    out=hn[i][:, cols], in0=h_sb[:, i, cols], scalar=rstd[:, i:i + 1], in1=gain_all[c][:],
-                    op0=ALU.mult, op1=ALU.mult)
+            for v in range(2):
+                for q in range(Q):
+                    values = h_sb[:, i, q * K_PASS:(q + 1) * K_PASS].rearrange("p (m v e) -> p v m e", v=2, e=2)
+                    gains = gain_all[q][:].rearrange("p (m v e) -> p v m e", v=2, e=2)
+                    first = q * K_PASS + v * 2 * P
+                    nc.vector.scalar_tensor_tensor(
+                        out=hn[i][:, first:first + 2 * P].rearrange("p (m e) -> p m e", e=2),
+                        in0=values[:, v, :, :], scalar=rstd[:, i:i + 1], in1=gains[:, v, :, :],
+                        op0=ALU.mult, op1=ALU.mult)
 
         def turn_hn(i):
             bank = work_bank([P, Q, 2, P], F32)
             words = hn[i][:].bitcast(F32)
             for q in range(Q):
                 for v in range(2):
-                    nc.tensor.transpose(bank[:, q, v, :], words[:, 256 * q + v:256 * (q + 1):2], ident_f32[:])
+                    nc.tensor.transpose(bank[:, q, v, :], words[:, (2 * q + v) * P:(2 * q + v + 1) * P], ident_f32[:])
             banks["hn", i] = bank
 
         def hn_out(i):
@@ -308,11 +313,12 @@ def tile_block_pc_kernel(tc, h_attn, norm2_w, ffn_wk, ffn_wv_bytes, ffn_wv_scale
         nc.vector.memset(gain_row[:], 0.0)
         make_identity(nc, ident_bf16[:])
         make_identity(nc, ident_f32[:])
+        load_scale()
         warm = keep.tile([P, 1], F32, align_bytes=64, name="warm")
         nc.scalar.activation(out=warm[:], in_=ones[:, 0:1], func=ACT.Abs_reciprocal_sqrt)
 
-        sync = [(load_scale, 0, 1), (load_wv, 0, 0, 1), (load_wv, 0, 1, 2), (load_wv, 0, 2, 3), (load_wv, 0, 3, 4), (load_h, 0), (load_gain,), (load_h, 1),
-                (load_wk, 0, 1), (load_h, 2), (load_h, 3), (load_wk, 0, 0), (load_wk, 1, 0), (load_scale, 1, G), (load_wv, 1, 0, PACK),
+        sync = [(load_wv, 0, 0, 1), (load_wv, 0, 1, 2), (load_wv, 0, 2, 3), (load_wv, 0, 3, 4), (load_h, 0), (load_gain,), (load_h, 1),
+                (load_wk, 0, 1), (load_h, 2), (load_wk, 0, 0), (load_h, 3), (load_wk, 1, 0), (load_wv, 1, 0, PACK),
                 (load_wk, 1, 1)]
         for g in range(2, G):
             sync += [(load_wk, g, 0), (load_wk, g, 1), (load_wv, g, 0, PACK)]
@@ -325,8 +331,7 @@ def tile_block_pc_kernel(tc, h_attn, norm2_w, ffn_wk, ffn_wv_bytes, ffn_wv_scale
         tensor = [(spread_gain,), (wk_on_tensor, 0, 1, 0), (turn_hn, 0), (wk_on_tensor, 0, 1, 1), (turn_hn, 1),
                   (wk_on_tensor, 1, 0, 0), (turn_hn, 2), (wk_on_tensor, 1, 0, 1), (turn_hn, 3)]
         scalar = [early[0], early[1], (sum_squares, 0), (root, 0), (sum_squares, 1), (root, 1), (sum_squares, 2),
-                  (sum_squares, 3), (root, 2),
-                  (wk_out, 0, 1, 0), (root, 3), (hn_out, 0), (wk_out, 0, 1, 1), (hn_out, 1), fill[0], (wk_out, 1, 0, 0), fill[1], (hn_out, 2),
+                  (wk_out, 0, 1, 0), (root, 2), (sum_squares, 3), (hn_out, 0), (root, 3), (wk_out, 0, 1, 1), (hn_out, 1), fill[0], (wk_out, 1, 0, 0), fill[1], (hn_out, 2),
                   (wk_out, 1, 0, 1), (hn_out, 3)] + fill[2:]
         vector = planes(lower[0], True) + [
                   (widen, upper[0], True, 2, 3), (wv_on_vector, lower[0]), (widen, upper[0], True, 3, 4), (quantize_wv, lower[0]), (normalize, 0),
@@ -368,8 +373,8 @@ def tile_block_pc_kernel(tc, h_attn, norm2_w, ffn_wk, ffn_wv_bytes, ffn_wv_scale
                 vector += [(widen, upper[2], True, 0, 4), (widen, d, True, 0, 4), (wv_on_vector, upper[2]),
                            (quantize_wv, lower[G - 1]), (quantize_wv, upper[2]), (quantize_k, g), (wv_on_vector, d)]
             else:
-                vector += [(widen, a, True, 2, 4), (widen, right[2], True, 0, 4), (quantize_wv, d), (wv_on_vector, a),
-                           (quantize_wv, upper[1]), (quantize_k, g), (wv_on_vector, right[2]), (quantize_wv, a), (quantize_wv, right[2])]
+                vector += [(widen, a, True, 2, 4), (widen, right[2], True, 0, 4), (wv_on_vector, a), (quantize_wv, upper[1]),
+                           (quantize_wv, d), (quantize_k, g), (wv_on_vector, right[2]), (quantize_wv, a)]
         def products(sl, groups):
             return [(second_product, sl, g, 0, NT) for g in groups]
 
@@ -379,7 +384,7 @@ def tile_block_pc_kernel(tc, h_attn, norm2_w, ffn_wk, ffn_wv_bytes, ffn_wv_scale
         scalar += [(wv_on_scalar, late[4])]
         tensor += products(1, (0, 2, 1)) + lower_products[-NT:]
         tensor += products(1, (7, 3)) + products(2, (0, 1, 2, 7, 3, 6, 4, 5)) + products(1, (4, 6, 5))
-        vector += [(finish, 0, 0), (finish, 0, 1), (wv_on_vector, late[1]), (wv_on_vector, late[2]), (quantize_wv, late[1]),
+        vector += [(finish, 0, 0), (finish, 0, 1), (quantize_wv, right[2]), (wv_on_vector, late[1]), (wv_on_vector, late[2]), (quantize_wv, late[1]),
                    (quantize_wv, late[2]), (wv_on_vector, late[3]), (finish, 0, 2), (quantize_wv, late[3]),
                    (wv_on_vector, late[5]), (finish, 0, 3), (quantize_wv, late[5]), (quantize_wv, late[4]),
                    (finish, 2, 0), (finish, 2, 1), (finish, 1, 0), (finish, 1, 1)]
@@ -411,7 +416,7 @@ def tile_block_pc_kernel(tc, h_attn, norm2_w, ffn_wk, ffn_wv_bytes, ffn_wv_scale
             if f is quantize_wk:
                 return [(wk_out,) + a + (1,)] if (wk_out,) + a + (1,) in scalar else [(wk_on_vector,) + a]
             if f is widen:
-                return [j for j in sync if j[0] is load_scale and j[1] <= a[0][0] < j[2]] + [
+                return [
                     j for j in sync if j[0] is load_wv and j[1] == a[0][0] and j[2] < a[3]] + [
                     j for j in widened(a[0]) if j[3] == 0 < a[2]]
             if f in (wv_on_vector, wv_on_scalar, wv_on_tensor):

@@ -118,8 +118,12 @@ def tile_block_pc_kernel(tc, h_attn, norm2_w, ffn_wk, ffn_wv_bytes, ffn_wv_scale
         def wk_on_vector(g, q):
             wk_grouped[g, q] = stage4.tile([P, K_PASS * PACK], BF16, align_bytes=64, name="wk_grouped")
             nc.vector.tensor_copy(
-                out=wk_grouped[g, q][:].rearrange("p (u e m j) -> p m u j e", u=2, e=2, j=PACK),
-                in_=wk_raw[g, q][:].rearrange("p j (m u e) -> p m u j e", u=2, e=2),
+                out=wk_grouped[g, q][:].rearrange("p (u e m j) -> p u m j e", u=2, e=2, j=PACK)[:, 0, :, :, :],
+                in_=wk_raw[g, q][:].rearrange("p j (m u e) -> p u m j e", u=2, e=2)[:, 0, :, :, :],
+            )
+            nc.vector.tensor_copy(
+                out=wk_grouped[g, q][:].rearrange("p (u e m j) -> p u m j e", u=2, e=2, j=PACK)[:, 1, :, :, :],
+                in_=wk_raw[g, q][:].rearrange("p j (m u e) -> p u m j e", u=2, e=2)[:, 1, :, :, :],
             )
 
         def quantize_wk(g, q):
@@ -226,7 +230,7 @@ def tile_block_pc_kernel(tc, h_attn, norm2_w, ffn_wk, ffn_wv_bytes, ffn_wv_scale
 
         acc, passes, result = {}, {}, {}
         bank_of = {(0, 0): "acc0", (0, 1): "acc1", (0, 2): "acc2", (0, 3): "acc3",
-                   (1, 0): "work0", (1, 1): "work1", (2, 0): "acc0", (2, 1): "acc1"}
+                   (1, 0): "work2", (1, 1): "work3", (2, 0): "acc0", (2, 1): "acc1"}
 
         def second_product(sl, g, first, last):
             c0, w = SLICES[sl]
@@ -348,8 +352,7 @@ def tile_block_pc_kernel(tc, h_attn, norm2_w, ffn_wk, ffn_wv_bytes, ffn_wv_scale
                     mm[1] += [(wv_on_tensor, upper[0], g)]
                     fill[1] += [(wv_out, upper[0], g)]
                 if g == G - 3:
-                    mm = [mm[half] + [(wv_on_tensor, lower[G - 2], half)] for half in range(2)]
-                    fill = [fill[half] + [planes(a)[half], (wv_out, lower[G - 2], half)] for half in range(2)]
+                    fill = [fill[half] + [planes(a)[half]] for half in range(2)]
             elif g == G - 2:
                 mm = [[(wv_on_tensor, lower[G - 1], half)] for half in range(2)]
                 fill = [[(wv_out, lower[G - 1], half)] for half in range(2)]
@@ -365,12 +368,12 @@ def tile_block_pc_kernel(tc, h_attn, norm2_w, ffn_wk, ffn_wv_bytes, ffn_wv_scale
             if g + 2 < G:
                 u = lower[g + 1]
                 vector += [(wk_on_vector, g + 2, 1), (widen, lower[g + 2], True, 0, 4), (quantize_wk, g + 2, 1)]
-                between = (wv_on_vector, u) if g < G - 3 else (widen, upper[1], True, 0, 4)
+                between = (wv_on_vector, u)
                 vector += [between, (quantize_wk, g + 2, 0), (quantize_wv, u), (quantize_k, g)]
                 if g == 1:
                     vector += [(quantize_wv, upper[0])]
             elif g == G - 2:
-                vector += [(widen, upper[2], True, 0, 4), (widen, d, True, 0, 4), (wv_on_vector, upper[2]),
+                vector += [(widen, upper[1], True, 0, 4), (widen, upper[2], True, 0, 4), (widen, d, True, 0, 4), (wv_on_vector, upper[2]),
                            (quantize_wv, lower[G - 1]), (quantize_wv, upper[2]), (quantize_k, g), (wv_on_vector, d)]
             else:
                 vector += [(widen, a, True, 2, 4), (widen, right[2], True, 0, 4), (wv_on_vector, a), (quantize_wv, upper[1]),

@@ -82,9 +82,8 @@ def tile_block_pc_kernel(tc, h_attn, norm2_w, ffn_wk, ffn_wv_bytes, ffn_wv_scale
         def load_wv(g, first, last):
             nc.sync.dma_start(out=wv_bytes[:, g, first:last, :], in_=wv_v[g][:, first:last, :])
 
-        def load_scale():
-            nc.scalar.dma_start(out=wv_scale[:, 0:1, 0:PACK], in_=scale_v[:, 0:1, :])
-            nc.scalar.dma_start(out=wv_scale[:, 1:G, 0:PACK], in_=scale_v[:, 1:G, :])
+        def load_scale(first, last):
+            nc.sync.dma_start(out=wv_scale[:, first:last, 0:PACK], in_=scale_v[:, first:last, :])
 
         def load_gain():
             nc.sync.dma_start(out=gain_row[0:1, :], in_=norm2_w.rearrange("(o d) -> o d", o=1))
@@ -230,7 +229,7 @@ def tile_block_pc_kernel(tc, h_attn, norm2_w, ffn_wk, ffn_wv_bytes, ffn_wv_scale
 
         acc, passes, result = {}, {}, {}
         bank_of = {(0, 0): "acc0", (0, 1): "acc1", (0, 2): "acc2", (0, 3): "acc3",
-                   (1, 0): "work2", (1, 1): "work3", (2, 0): "acc0", (2, 1): "acc1"}
+                   (1, 0): "work0", (1, 1): "work1", (2, 0): "work2", (2, 1): "work3"}
 
         def second_product(sl, g, first, last):
             c0, w = SLICES[sl]
@@ -317,12 +316,11 @@ def tile_block_pc_kernel(tc, h_attn, norm2_w, ffn_wk, ffn_wv_bytes, ffn_wv_scale
         nc.vector.memset(gain_row[:], 0.0)
         make_identity(nc, ident_bf16[:])
         make_identity(nc, ident_f32[:])
-        load_scale()
         warm = keep.tile([P, 1], F32, align_bytes=64, name="warm")
         nc.scalar.activation(out=warm[:], in_=ones[:, 0:1], func=ACT.Abs_reciprocal_sqrt)
 
-        sync = [(load_wv, 0, 0, 1), (load_wv, 0, 1, 2), (load_wv, 0, 2, 3), (load_wv, 0, 3, 4), (load_h, 0), (load_gain,), (load_h, 1),
-                (load_wk, 0, 1), (load_h, 2), (load_wk, 0, 0), (load_h, 3), (load_wk, 1, 0), (load_wv, 1, 0, PACK),
+        sync = [(load_scale, 0, 1), (load_wv, 0, 0, 1), (load_wv, 0, 1, 2), (load_wv, 0, 2, 3), (load_wv, 0, 3, 4), (load_h, 0), (load_gain,), (load_h, 1),
+                (load_wk, 0, 1), (load_h, 2), (load_wk, 0, 0), (load_h, 3), (load_wk, 1, 0), (load_scale, 1, G), (load_wv, 1, 0, PACK),
                 (load_wk, 1, 1)]
         for g in range(2, G):
             sync += [(load_wk, g, 0), (load_wk, g, 1), (load_wv, g, 0, PACK)]
@@ -336,11 +334,11 @@ def tile_block_pc_kernel(tc, h_attn, norm2_w, ffn_wk, ffn_wv_bytes, ffn_wv_scale
                   (wk_on_tensor, 1, 0, 0), (turn_hn, 2), (wk_on_tensor, 1, 0, 1), (turn_hn, 3)]
         scalar = [early[0], early[1], (sum_squares, 0), (root, 0), (sum_squares, 1), (root, 1), (sum_squares, 2),
                   (wk_out, 0, 1, 0), (root, 2), (sum_squares, 3), (hn_out, 0), (root, 3), (wk_out, 0, 1, 1), (hn_out, 1), fill[0], (wk_out, 1, 0, 0), fill[1], (hn_out, 2),
-                  (wk_out, 1, 0, 1), (hn_out, 3)] + fill[2:]
+                  (wk_out, 1, 0, 1), (hn_out, 3), fill[2]]
         vector = planes(lower[0], True) + [
                   (widen, upper[0], True, 2, 3), (wv_on_vector, lower[0]), (widen, upper[0], True, 3, 4), (quantize_wv, lower[0]), (normalize, 0),
                   (normalize, 1), (wk_on_vector, 0, 0), (normalize, 2), (quantize_hn, 0), (normalize, 3), (quantize_wk, 0, 0), (quantize_wk, 0, 1),
-                  (quantize_hn, 1), (wk_on_vector, 1, 1), (quantize_hn, 2), (quantize_hn, 3), (quantize_wk, 1, 0), (quantize_wk, 1, 1)]
+                  (quantize_hn, 1), (wk_on_vector, 1, 1), (quantize_hn, 2), (widen, lower[1], True, 3, 4), (quantize_hn, 3), (quantize_wk, 1, 0), (quantize_wk, 1, 1)]
         lower_products = [(second_product, 0, g, i, i + 1) for g in range(G) for i in range(NT)]
         a, d = upper[3], upper[4]
         left, right = upper[5:8], upper[8:11]
@@ -352,7 +350,8 @@ def tile_block_pc_kernel(tc, h_attn, norm2_w, ffn_wk, ffn_wv_bytes, ffn_wv_scale
                     mm[1] += [(wv_on_tensor, upper[0], g)]
                     fill[1] += [(wv_out, upper[0], g)]
                 if g == G - 3:
-                    fill = [fill[half] + [planes(a)[half]] for half in range(2)]
+                    mm = [mm[half] + [(wv_on_tensor, lower[G - 2], half)] for half in range(2)]
+                    fill = [fill[half] + [planes(a)[half], (wv_out, lower[G - 2], half)] for half in range(2)]
             elif g == G - 2:
                 mm = [[(wv_on_tensor, lower[G - 1], half)] for half in range(2)]
                 fill = [[(wv_out, lower[G - 1], half)] for half in range(2)]
@@ -368,16 +367,16 @@ def tile_block_pc_kernel(tc, h_attn, norm2_w, ffn_wk, ffn_wv_bytes, ffn_wv_scale
             if g + 2 < G:
                 u = lower[g + 1]
                 vector += [(wk_on_vector, g + 2, 1), (widen, lower[g + 2], True, 0, 4), (quantize_wk, g + 2, 1)]
-                between = (wv_on_vector, u)
+                between = (wv_on_vector, u) if g < G - 3 else (widen, upper[1], True, 0, 4)
                 vector += [between, (quantize_wk, g + 2, 0), (quantize_wv, u), (quantize_k, g)]
                 if g == 1:
                     vector += [(quantize_wv, upper[0])]
             elif g == G - 2:
-                vector += [(widen, upper[1], True, 0, 4), (widen, upper[2], True, 0, 4), (widen, d, True, 0, 4), (wv_on_vector, upper[2]),
+                vector += [(widen, upper[2], True, 0, 4), (widen, d, True, 0, 4), (wv_on_vector, upper[2]), (widen, a, True, 2, 4),
                            (quantize_wv, lower[G - 1]), (quantize_wv, upper[2]), (quantize_k, g), (wv_on_vector, d)]
             else:
-                vector += [(widen, a, True, 2, 4), (widen, right[2], True, 0, 4), (wv_on_vector, a), (quantize_wv, upper[1]),
-                           (quantize_wv, d), (quantize_k, g), (wv_on_vector, right[2]), (quantize_wv, a)]
+                vector += [(widen, right[2], True, 0, 4), (wv_on_vector, a), (quantize_wv, d),
+                           (quantize_wv, upper[1]), (quantize_k, g), (wv_on_vector, right[2]), (quantize_wv, a)]
         def products(sl, groups):
             return [(second_product, sl, g, 0, NT) for g in groups]
 
@@ -385,8 +384,8 @@ def tile_block_pc_kernel(tc, h_attn, norm2_w, ffn_wk, ffn_wv_bytes, ffn_wv_scale
         for u in late[1:]:
             scalar += planes(u)
         scalar += [(wv_on_scalar, late[4])]
-        tensor += products(1, (0, 2, 1)) + lower_products[-NT:]
-        tensor += products(1, (7, 3)) + products(2, (0, 1, 2, 7, 3, 6, 4, 5)) + products(1, (4, 6, 5))
+        tensor += products(1, (0, 2)) + products(2, (0, 2)) + products(1, (1,)) + lower_products[-NT:]
+        tensor += products(2, (1, 7, 3, 6)) + products(1, (7, 3)) + products(2, (4, 5)) + products(1, (4, 6, 5))
         vector += [(finish, 0, 0), (finish, 0, 1), (quantize_wv, right[2]), (wv_on_vector, late[1]), (wv_on_vector, late[2]), (quantize_wv, late[1]),
                    (quantize_wv, late[2]), (wv_on_vector, late[3]), (finish, 0, 2), (quantize_wv, late[3]),
                    (wv_on_vector, late[5]), (finish, 0, 3), (quantize_wv, late[5]), (quantize_wv, late[4]),
@@ -419,7 +418,7 @@ def tile_block_pc_kernel(tc, h_attn, norm2_w, ffn_wk, ffn_wv_bytes, ffn_wv_scale
             if f is quantize_wk:
                 return [(wk_out,) + a + (1,)] if (wk_out,) + a + (1,) in scalar else [(wk_on_vector,) + a]
             if f is widen:
-                return [
+                return [j for j in sync if j[0] is load_scale and j[1] <= a[0][0] < j[2]] + [
                     j for j in sync if j[0] is load_wv and j[1] == a[0][0] and j[2] < a[3]] + [
                     j for j in widened(a[0]) if j[3] == 0 < a[2]]
             if f in (wv_on_vector, wv_on_scalar, wv_on_tensor):
@@ -469,7 +468,7 @@ def tile_block_pc_kernel(tc, h_attn, norm2_w, ffn_wk, ffn_wv_bytes, ffn_wv_scale
 
         emptied_by = {wk_on_tensor: wk_out, wv_on_tensor: wv_out, first_product: rectify, turn_hn: hn_out}
         bank_user = {}
-        freed = {(0, 0): [(normalize, NT - 1)], (1, 0): [(rectify, G - 1, NT - 1), (wv_out, upper[1], 1)], (2, 0): [(finish, 0, 0), (finish, 0, 1)]}
+        freed = {(0, 0): [(normalize, NT - 1)], (1, 0): [(rectify, G - 1, NT - 1), (wv_out, upper[1], 1)], (2, 0): [(rectify, G - 1, NT - 1), (wv_out, upper[1], 1)]}
         written, rings = set(), {}
         queues = [sync, tensor, scalar, vector]
         at = [0] * len(queues)

@@ -24,11 +24,14 @@ G = FF // K_PASS
 Q = D // K_PASS
 HALF = D // 2
 
-SLICES = ((0, 512), (512, 256), (768, 256))
-WHOLE = 5
-V_UPPER = 2
-LAST = 4
+QUARTER = D // 4
+
+SLICES = ((0, HALF), (HALF, QUARTER), (HALF + QUARTER, QUARTER))
+WORK_BANKS = 4
 RUN = 2
+LAG = 2
+DEPTH = {"wk_raw": 5, "wk_grouped": 4, "wk_codes": 5, "wk_scales": 5, "planes_vector": 4, "planes_scalar": 4,
+         "wv_grouped": 3, "relu": 2, "k_grouped": 3, "hn": 2, "hn_grouped": 2, "result": 5}
 
 
 def tile_block_pc_kernel(tc, h_attn, norm2_w, ffn_wk, ffn_wv_bytes, ffn_wv_scale, out):
@@ -39,16 +42,16 @@ def tile_block_pc_kernel(tc, h_attn, norm2_w, ffn_wk, ffn_wv_bytes, ffn_wv_scale
     wv_v = ffn_wv_bytes.rearrange("(g p t) n -> g p t n", p=P, t=PACK)
     scale_v = ffn_wv_scale.rearrange("(g p t) o -> p g (t o)", p=P, t=PACK)
 
+    split = (4, 5, 6)
     lower = [(g, 0, HALF) for g in range(G)]
-    upper = [(g, HALF, HALF) for g in (0, 1, 2, 3, G - 1)]
-    upper += [(g, 512, 256) for g in (4, 5, 6)] + [(g, 768, 256) for g in (4, 5, 6)]
+    upper = {g: (g, HALF, HALF) for g in range(G) if g not in split}
+    left = [(g,) + SLICES[1] for g in split]
+    right = [(g,) + SLICES[2] for g in split]
+    units = lower + [upper[g] for g in upper] + left + right
 
     with ExitStack() as ctx:
         keep = ctx.enter_context(tc.tile_pool(name="keep", bufs=1))
-        stage2 = ctx.enter_context(tc.tile_pool(name="stage2", bufs=2))
-        stage3 = ctx.enter_context(tc.tile_pool(name="stage3", bufs=3))
-        stage4 = ctx.enter_context(tc.tile_pool(name="stage4", bufs=4))
-        stage6 = ctx.enter_context(tc.tile_pool(name="stage6", bufs=6))
+        stream = ctx.enter_context(tc.tile_pool(name="stream", bufs=1))
         psum = ctx.enter_context(tc.psum_pool(name="psum", bufs=1))
         ctx.enter_context(tc.manual_schedule())
 
@@ -68,15 +71,19 @@ def tile_block_pc_kernel(tc, h_attn, norm2_w, ffn_wk, ffn_wv_bytes, ffn_wv_scale
         sumsq = keep.tile([P, NT], F32, align_bytes=64, name="sumsq")
         rstd = keep.tile([P, NT], F32, align_bytes=64, name="rstd")
 
-        turn = [0]
+        def buffer(shape, dtype, tag):
+            return stream.tile(shape, dtype, align_bytes=64, name=tag, bufs=DEPTH[tag])
 
-        def work_bank(shape, dtype):
-            return psum.tile(shape, dtype, name="work%d" % turn[0])
+        banks = {}
+
+        def work_bank(key, shape, dtype):
+            banks[key] = psum.tile(shape, dtype, name="work%d" % (len(banks) % WORK_BANKS))
+            return banks[key]
 
         wk_raw = {}
 
         def load_wk(g, q):
-            wk_raw[g, q] = stage6.tile([P, PACK, K_PASS], BF16, align_bytes=64, name="wk_raw", bufs=5)
+            wk_raw[g, q] = buffer([P, PACK, K_PASS], BF16, "wk_raw")
             nc.sync.dma_start(out=wk_raw[g, q][:], in_=wk_v[g, q])
 
         def load_wv(g, first, last):
@@ -91,108 +98,101 @@ def tile_block_pc_kernel(tc, h_attn, norm2_w, ffn_wk, ffn_wv_bytes, ffn_wv_scale
         def load_h(i):
             nc.sync.dma_start(out=h_sb[:, i, :], in_=h_v[i])
 
-        wk_grouped, wk_codes, wk_scales, banks = {}, {}, {}, {}
+        wk_grouped, wk_codes, wk_scales = {}, {}, {}
 
         def wk_on_tensor(g, q, b):
-            bank = work_bank([P, PACK, 64, PACK], BF16)
-            for a in range(2):
-                c0 = 256 * b + 128 * a
+            bank = work_bank(("wk", g, q, b), [P, PACK, 64, PACK], BF16)
+            for part in range(2):
+                c0 = 2 * P * b + P * part
                 nc.tensor.matmul(
-                    bank[:, :, 32 * a:32 * a + 32, :].rearrange("p t m j -> p j m t"),
+                    bank[:, :, 32 * part:32 * part + 32, :].rearrange("p t m j -> p j m t"),
                     lhsT=ident_bf16[:],
-                    rhs=wk_raw[g, q][:, :, c0:c0 + 128].rearrange("p j (m t) -> p j m t", t=PACK),
+                    rhs=wk_raw[g, q][:, :, c0:c0 + P].rearrange("p j (m t) -> p j m t", t=PACK),
                     start=True,
                     stop=True,
                 )
-            banks["wk", g, q, b] = bank
 
         def wk_out(g, q, b):
             if b == 0:
-                wk_grouped[g, q] = stage4.tile([P, K_PASS * PACK], BF16, align_bytes=64, name="wk_grouped")
+                wk_grouped[g, q] = buffer([P, K_PASS * PACK], BF16, "wk_grouped")
             nc.scalar.copy(
-                out=wk_grouped[g, q][:].bitcast(F32).rearrange("p (t w) -> p t w", t=PACK)[:, :, 128 * b:128 * b + 128],
+                out=wk_grouped[g, q][:].bitcast(F32).rearrange("p (t w) -> p t w", t=PACK)[:, :, P * b:P * b + P],
                 in_=banks["wk", g, q, b][:].rearrange("p t m j -> p t (m j)").bitcast(F32),
             )
 
         def wk_on_vector(g, q):
-            wk_grouped[g, q] = stage4.tile([P, K_PASS * PACK], BF16, align_bytes=64, name="wk_grouped")
-            nc.vector.tensor_copy(
-                out=wk_grouped[g, q][:].rearrange("p (u e m j) -> p u m j e", u=2, e=2, j=PACK)[:, 0, :, :, :],
-                in_=wk_raw[g, q][:].rearrange("p j (m u e) -> p u m j e", u=2, e=2)[:, 0, :, :, :],
-            )
-            nc.vector.tensor_copy(
-                out=wk_grouped[g, q][:].rearrange("p (u e m j) -> p u m j e", u=2, e=2, j=PACK)[:, 1, :, :, :],
-                in_=wk_raw[g, q][:].rearrange("p j (m u e) -> p u m j e", u=2, e=2)[:, 1, :, :, :],
-            )
+            wk_grouped[g, q] = buffer([P, K_PASS * PACK], BF16, "wk_grouped")
+            for u in range(2):
+                nc.vector.tensor_copy(
+                    out=wk_grouped[g, q][:].rearrange("p (u e m j) -> p u m j e", u=2, e=2, j=PACK)[:, u, :, :, :],
+                    in_=wk_raw[g, q][:].rearrange("p j (m u e) -> p u m j e", u=2, e=2)[:, u, :, :, :],
+                )
 
         def quantize_wk(g, q):
-            wk_codes[g, q] = stage6.tile([P, K_PASS], U32, align_bytes=64, name="wk_codes", bufs=5)
-            wk_scales[g, q] = stage6.tile([P, K_PASS], U8, align_bytes=64, name="wk_scales", bufs=5)
+            wk_codes[g, q] = buffer([P, K_PASS], U32, "wk_codes")
+            wk_scales[g, q] = buffer([P, K_PASS], U8, "wk_scales")
             nc.vector.quantize_mx(
                 out=wk_codes[g, q][:].bitcast(FP8X4), scales=wk_scales[g, q][:], in_=wk_grouped[g, q][:])
 
         wv_planes, wv_grouped = {}, {}
-        planes_pool = {True: stage4, False: stage4}
 
-        def widen(u, on_vector, first, last):
-            g, c0, w = u
+        def widen(unit, on_vector, first, last):
+            g, c0, w = unit
             if first == 0:
-                wv_planes[u] = planes_pool[on_vector].tile([P, PACK, w], BF16, align_bytes=64, name="wv_planes_v" if on_vector else "wv_planes_s")
+                wv_planes[unit] = buffer([P, PACK, w], BF16, "planes_vector" if on_vector else "planes_scalar")
             for t in range(first, last):
                 values = wv_bytes[:, g, t, c0:c0 + w].bitcast(FP8)
                 scale = wv_scale[:, g, t:t + 1]
                 if on_vector:
                     nc.vector.tensor_scalar(
-                        out=wv_planes[u][:, t, :], in0=values, scalar1=scale, scalar2=None, op0=ALU.mult)
+                        out=wv_planes[unit][:, t, :], in0=values, scalar1=scale, scalar2=None, op0=ALU.mult)
                 else:
-                    nc.scalar.activation(out=wv_planes[u][:, t, :], in_=values, func=ACT.Copy, scale=scale)
+                    nc.scalar.activation(out=wv_planes[unit][:, t, :], in_=values, func=ACT.Copy, scale=scale)
 
-        def wv_on_vector(u):
-            wv_grouped[u] = stage3.tile([P, u[2] * PACK], BF16, align_bytes=64, name="wv_grouped")
-            nc.vector.tensor_copy(
-                out=wv_grouped[u][:].rearrange("p (c i t) -> p c t i", i=RUN, t=PACK),
-                in_=wv_planes[u][:].rearrange("p t (c i) -> p c t i", i=RUN),
-            )
+        def interleaving_views(unit):
+            wv_grouped[unit] = buffer([P, unit[2] * PACK], BF16, "wv_grouped")
+            return (wv_grouped[unit][:].rearrange("p (c i t) -> p c t i", i=RUN, t=PACK),
+                    wv_planes[unit][:].rearrange("p t (c i) -> p c t i", i=RUN))
 
-        def wv_on_scalar(u):
-            wv_grouped[u] = stage3.tile([P, u[2] * PACK], BF16, align_bytes=64, name="wv_grouped")
-            nc.scalar.copy(
-                out=wv_grouped[u][:].rearrange("p (c i t) -> p c t i", i=RUN, t=PACK),
-                in_=wv_planes[u][:].rearrange("p t (c i) -> p c t i", i=RUN),
-            )
+        def wv_on_vector(unit):
+            grouped, spread = interleaving_views(unit)
+            nc.vector.tensor_copy(out=grouped, in_=spread)
 
-        def wv_on_tensor(u, b):
-            bank = work_bank([P, 256, PACK], BF16)
-            for a in range(2):
-                c0 = 256 * b + 128 * a
+        def wv_on_scalar(unit):
+            grouped, spread = interleaving_views(unit)
+            nc.scalar.copy(out=grouped, in_=spread)
+
+        def wv_on_tensor(unit, b):
+            bank = work_bank(("wv", unit, b), [P, 2 * P, PACK], BF16)
+            for part in range(2):
+                c0 = 2 * P * b + P * part
                 nc.tensor.matmul(
-                    bank[:, 128 * a:128 * a + 128, :].rearrange("p n t -> p t n"),
+                    bank[:, P * part:P * part + P, :].rearrange("p n t -> p t n"),
                     lhsT=ident_bf16[:],
-                    rhs=wv_planes[u][:, :, c0:c0 + 128],
+                    rhs=wv_planes[unit][:, :, c0:c0 + P],
                     start=True,
                     stop=True,
                 )
-            banks["wv", u, b] = bank
 
-        def wv_out(u, b):
+        def wv_out(unit, b):
             if b == 0:
-                wv_grouped[u] = stage3.tile([P, u[2] * PACK], BF16, align_bytes=64, name="wv_grouped")
+                wv_grouped[unit] = buffer([P, unit[2] * PACK], BF16, "wv_grouped")
             nc.scalar.copy(
-                out=wv_grouped[u][:].bitcast(F32)[:, 512 * b:512 * b + 512],
-                in_=banks["wv", u, b][:].rearrange("p n t -> p (n t)").bitcast(F32),
+                out=wv_grouped[unit][:].bitcast(F32)[:, HALF * b:HALF * b + HALF],
+                in_=banks["wv", unit, b][:].rearrange("p n t -> p (n t)").bitcast(F32),
             )
 
-        def quantize_wv(u):
-            g, c0, w = u
+        def quantize_wv(unit):
+            g, c0, w = unit
             nc.vector.quantize_mx(
-                out=wv_codes[:, g, c0:c0 + w].bitcast(FP8X4), scales=wv_scales[:, g, c0:c0 + w], in_=wv_grouped[u][:])
+                out=wv_codes[:, g, c0:c0 + w].bitcast(FP8X4), scales=wv_scales[:, g, c0:c0 + w], in_=wv_grouped[unit][:])
 
         relu, k_grouped = {}, {}
 
         def first_product(g, i):
             a, u = divmod(i, 2)
             tokens = slice(2 * P * a, 2 * P * (a + 1))
-            bank = work_bank([P, 2, 2 * P], F32)
+            bank = work_bank(("hidden", g, i), [P, 2, 2 * P], F32)
             for e in range(2):
                 t = 2 * u + e
                 for q in range(Q):
@@ -205,18 +205,17 @@ def tile_block_pc_kernel(tc, h_attn, norm2_w, ffn_wk, ffn_wv_bytes, ffn_wv_scale
                         start=(q == 0),
                         stop=(q == Q - 1),
                     )
-            banks["hidden", g, i] = bank
 
         def rectify(g, i):
             a, u = divmod(i, 2)
             if u == 0:
-                relu[g, a] = stage2.tile([P, 2, 2 * P, 2], F32, align_bytes=64, name="relu")
+                relu[g, a] = buffer([P, 2, 2 * P, 2], F32, "relu")
             nc.scalar.activation(
                 out=relu[g, a][:, u, :, :], in_=banks["hidden", g, i][:].rearrange("p e n -> p n e"), func=ACT.Relu)
 
         def square(g, a):
             if a == 0:
-                k_grouped[g] = stage3.tile([P, 2, 2 * P, 2, 2], BF16, align_bytes=64, name="k_grouped")
+                k_grouped[g] = buffer([P, 2, 2 * P, 2, 2], BF16, "k_grouped")
             nc.scalar.activation(
                 out=k_grouped[g][:, a, :, :, :], in_=relu[g, a][:].rearrange("p u n e -> p n u e"), func=ACT.Square)
 
@@ -228,8 +227,6 @@ def tile_block_pc_kernel(tc, h_attn, norm2_w, ffn_wk, ffn_wv_bytes, ffn_wv_scale
             )
 
         acc, passes, result = {}, {}, {}
-        bank_of = {(0, 0): "acc0", (0, 1): "acc1", (0, 2): "acc2", (0, 3): "acc3",
-                   (1, 0): "work0", (1, 1): "work1", (2, 0): "work2", (2, 1): "work3"}
 
         def second_product(sl, g, first, last):
             c0, w = SLICES[sl]
@@ -237,7 +234,7 @@ def tile_block_pc_kernel(tc, h_attn, norm2_w, ffn_wk, ffn_wv_bytes, ffn_wv_scale
             for i in range(first, last):
                 b, r = divmod(i, share)
                 if (sl, b) not in acc:
-                    acc[sl, b] = psum.tile([P, share, w], F32, name=bank_of[sl, b])
+                    acc[sl, b] = psum.tile([P, share, w], F32, name="acc%d" % b if sl == 0 else "work%d" % (2 * (sl - 1) + b))
                 passes[sl, b] = passes.get((sl, b), 0) + 1
                 nc.tensor.matmul_mx(
                     out=acc[sl, b][:, r, :],
@@ -253,7 +250,7 @@ def tile_block_pc_kernel(tc, h_attn, norm2_w, ffn_wk, ffn_wv_bytes, ffn_wv_scale
             c0, w = SLICES[sl]
             share = HALF // w
             tiles = slice(b * share, (b + 1) * share)
-            result[sl, b] = stage6.tile([P, share, w], F32, align_bytes=64, name="result", bufs=5)
+            result[sl, b] = buffer([P, share, w], F32, "result")
             nc.vector.tensor_tensor(out=result[sl, b][:], in0=acc[sl, b][:], in1=h_sb[:, tiles, c0:c0 + w], op=ALU.add)
 
         def store(sl, b):
@@ -264,13 +261,14 @@ def tile_block_pc_kernel(tc, h_attn, norm2_w, ffn_wk, ffn_wv_bytes, ffn_wv_scale
         gain_all, hn, hn_grouped = [], {}, {}
 
         def spread_gain():
-            for c in range(2):
-                bank = psum.tile([P, 512], F32, name="acc%d" % c)
-                nc.tensor.matmul(bank[:], lhsT=ones[:], rhs=gain_row[:, c * 512:(c + 1) * 512], start=True, stop=True)
+            for q in range(Q):
+                bank = psum.tile([P, K_PASS], F32, name="acc%d" % q)
+                nc.tensor.matmul(
+                    bank[:], lhsT=ones[:], rhs=gain_row[:, q * K_PASS:(q + 1) * K_PASS], start=True, stop=True)
                 gain_all.append(bank)
 
         def sum_squares(i):
-            squares = stage3.tile([P, D], BF16, align_bytes=64, name="k_grouped")
+            squares = buffer([P, D], BF16, "k_grouped")
             nc.scalar.activation(out=squares[:], in_=h_sb[:, i, :], func=ACT.Square, accum_out=sumsq[:, i:i + 1])
 
         def root(i):
@@ -278,7 +276,7 @@ def tile_block_pc_kernel(tc, h_attn, norm2_w, ffn_wk, ffn_wv_bytes, ffn_wv_scale
                 out=rstd[:, i:i + 1], in_=sumsq[:, i:i + 1], func=ACT.Abs_reciprocal_sqrt, scale=1.0 / D, bias=EPS)
 
         def normalize(i):
-            hn[i] = stage2.tile([P, D], BF16, align_bytes=64, name="hn")
+            hn[i] = buffer([P, D], BF16, "hn")
             for v in range(2):
                 for q in range(Q):
                     values = h_sb[:, i, q * K_PASS:(q + 1) * K_PASS].rearrange("p (m v e) -> p v m e", v=2, e=2)
@@ -290,15 +288,14 @@ def tile_block_pc_kernel(tc, h_attn, norm2_w, ffn_wk, ffn_wv_bytes, ffn_wv_scale
                         op0=ALU.mult, op1=ALU.mult)
 
         def turn_hn(i):
-            bank = work_bank([P, Q, 2, P], F32)
+            bank = work_bank(("hn", i), [P, Q, 2, P], F32)
             words = hn[i][:].bitcast(F32)
             for q in range(Q):
                 for v in range(2):
                     nc.tensor.transpose(bank[:, q, v, :], words[:, (2 * q + v) * P:(2 * q + v + 1) * P], ident_f32[:])
-            banks["hn", i] = bank
 
         def hn_out(i):
-            hn_grouped[i] = stage2.tile([P, Q * P * PACK], BF16, align_bytes=64, name="hn_grouped")
+            hn_grouped[i] = buffer([P, Q * P * PACK], BF16, "hn_grouped")
             nc.scalar.copy(
                 out=hn_grouped[i][:].bitcast(F32).rearrange("p (q n v) -> p q n v", q=Q, v=2),
                 in_=banks["hn", i][:].rearrange("p q v n -> p q n v"),
@@ -319,182 +316,177 @@ def tile_block_pc_kernel(tc, h_attn, norm2_w, ffn_wk, ffn_wv_bytes, ffn_wv_scale
         warm = keep.tile([P, 1], F32, align_bytes=64, name="warm")
         nc.scalar.activation(out=warm[:], in_=ones[:, 0:1], func=ACT.Abs_reciprocal_sqrt)
 
-        sync = [(load_scale, 0, 1), (load_wv, 0, 0, 1), (load_wv, 0, 1, 2), (load_wv, 0, 2, 3), (load_wv, 0, 3, 4), (load_h, 0), (load_gain,), (load_h, 1),
-                (load_wk, 0, 1), (load_h, 2), (load_wk, 0, 0), (load_h, 3), (load_wk, 1, 0), (load_scale, 1, G), (load_wv, 1, 0, PACK),
-                (load_wk, 1, 1)]
-        for g in range(2, G):
-            sync += [(load_wk, g, 0), (load_wk, g, 1), (load_wv, g, 0, PACK)]
-        sync += [(store, 0, b) for b in range(4)] + [(store, 2, 0), (store, 2, 1), (store, 1, 0), (store, 1, 1)]
 
-        def planes(u, on_vector=False):
-            return [(widen, u, on_vector, t, t + 1) for t in range(PACK)]
+        def planes(unit):
+            return [(widen, unit, False, t, t + 1) for t in range(PACK)]
 
-        early, fill = planes(upper[0]), planes(lower[1])
-        tensor = [(spread_gain,), (wk_on_tensor, 0, 1, 0), (turn_hn, 0), (wk_on_tensor, 0, 1, 1), (turn_hn, 1),
-                  (wk_on_tensor, 1, 0, 0), (turn_hn, 2), (wk_on_tensor, 1, 0, 1), (turn_hn, 3)]
-        scalar = [early[0], early[1], (sum_squares, 0), (root, 0), (sum_squares, 1), (root, 1), (sum_squares, 2),
-                  (wk_out, 0, 1, 0), (root, 2), (sum_squares, 3), (hn_out, 0), (root, 3), (wk_out, 0, 1, 1), (hn_out, 1), fill[0], (wk_out, 1, 0, 0), fill[1], (hn_out, 2),
-                  (wk_out, 1, 0, 1), (hn_out, 3), fill[2]]
-        vector = planes(lower[0], True) + [
-                  (widen, upper[0], True, 2, 3), (wv_on_vector, lower[0]), (widen, upper[0], True, 3, 4), (quantize_wv, lower[0]), (normalize, 0),
-                  (normalize, 1), (wk_on_vector, 0, 0), (normalize, 2), (quantize_hn, 0), (normalize, 3), (quantize_wk, 0, 0), (quantize_wk, 0, 1),
-                  (quantize_hn, 1), (wk_on_vector, 1, 1), (quantize_hn, 2), (widen, lower[1], True, 3, 4), (quantize_hn, 3), (quantize_wk, 1, 0), (quantize_wk, 1, 1)]
-        lower_products = [(second_product, 0, g, i, i + 1) for g in range(G) for i in range(NT)]
-        a, d = upper[3], upper[4]
-        left, right = upper[5:8], upper[8:11]
-        for g in range(G):
-            if g + 2 < G:
-                mm = [[(wk_on_tensor, g + 2, 0, half)] for half in range(2)]
-                fill = [[(wk_out, g + 2, 0, half)] for half in range(2)]
-                if g < 2:
-                    mm[1] += [(wv_on_tensor, upper[0], g)]
-                    fill[1] += [(wv_out, upper[0], g)]
-                if g == G - 3:
-                    mm = [mm[half] + [(wv_on_tensor, lower[G - 2], half)] for half in range(2)]
-                    fill = [fill[half] + [planes(a)[half], (wv_out, lower[G - 2], half)] for half in range(2)]
-            elif g == G - 2:
-                mm = [[(wv_on_tensor, lower[G - 1], half)] for half in range(2)]
-                fill = [[(wv_out, lower[G - 1], half)] for half in range(2)]
-            else:
-                mm = [[(wv_on_tensor, upper[1], half)] for half in range(2)]
-                fill = [[(wv_out, upper[1], half)] for half in range(2)]
-            tensor += [(first_product, g, 0), (first_product, g, 1)]
-            scalar += [(rectify, g, 0), (rectify, g, 1)]
-            tensor += mm[0] + [(first_product, g, 2), (first_product, g, 3)] + mm[1]
-            scalar += fill[0] + [(square, g, 0), (rectify, g, 2), (rectify, g, 3)] + fill[1] + [(square, g, 1)]
-            if g >= 1:
-                tensor += lower_products[NT * (g - 1):NT * g]
-            if g + 2 < G:
-                u = lower[g + 1]
-                vector += [(wk_on_vector, g + 2, 1), (widen, lower[g + 2], True, 0, 4), (quantize_wk, g + 2, 1)]
-                between = (wv_on_vector, u) if g < G - 3 else (widen, upper[1], True, 0, 4)
-                vector += [between, (quantize_wk, g + 2, 0), (quantize_wv, u), (quantize_k, g)]
-                if g == 1:
-                    vector += [(quantize_wv, upper[0])]
-            elif g == G - 2:
-                vector += [(widen, upper[2], True, 0, 4), (widen, d, True, 0, 4), (wv_on_vector, upper[2]), (widen, a, True, 2, 4),
-                           (quantize_wv, lower[G - 1]), (quantize_wv, upper[2]), (quantize_k, g), (wv_on_vector, d)]
-            else:
-                vector += [(widen, right[2], True, 0, 4), (wv_on_vector, a), (quantize_wv, d),
-                           (quantize_wv, upper[1]), (quantize_k, g), (wv_on_vector, right[2]), (quantize_wv, a)]
+        def halves(job, *key):
+            return [[(job,) + key + (b,)] for b in range(2)]
+
         def products(sl, groups):
             return [(second_product, sl, g, 0, NT) for g in groups]
 
-        late = [a] + right[:2] + left
-        for u in late[1:]:
-            scalar += planes(u)
-        scalar += [(wv_on_scalar, late[4])]
-        tensor += products(1, (0, 2)) + products(2, (0, 2)) + products(1, (1,)) + lower_products[-NT:]
+        sync = [(load_scale, 0, 1)] + [(load_wv, 0, t, t + 1) for t in range(PACK)]
+        sync += [(load_h, 0), (load_gain,), (load_h, 1), (load_wk, 0, 1), (load_h, 2), (load_wk, 0, 0), (load_h, 3),
+                 (load_wk, 1, 0), (load_scale, 1, G), (load_wv, 1, 0, PACK), (load_wk, 1, 1)]
+        for g in range(2, G):
+            sync += [(load_wk, g, 0), (load_wk, g, 1), (load_wv, g, 0, PACK)]
+        sync += [(store, 0, b) for b in range(NT)] + [(store, sl, b) for sl in (2, 1) for b in range(2)]
+
+        opening, spare = planes(upper[0]), planes(lower[1])
+        tensor = [(spread_gain,)]
+        for i in range(NT):
+            g, b = divmod(i, 2)
+            tensor += [(wk_on_tensor, g, 1 - g, b), (turn_hn, i)]
+        scalar = opening[:2] + [
+            (sum_squares, 0), (root, 0), (sum_squares, 1), (root, 1), (sum_squares, 2), (wk_out, 0, 1, 0), (root, 2),
+            (sum_squares, 3), (hn_out, 0), (root, 3), (wk_out, 0, 1, 1), (hn_out, 1), spare[0], (wk_out, 1, 0, 0),
+            spare[1], (hn_out, 2), (wk_out, 1, 0, 1), (hn_out, 3), spare[2]]
+        vector = [(widen, lower[0], True, t, t + 1) for t in range(PACK)] + [
+            (widen, upper[0], True, 2, 3), (wv_on_vector, lower[0]), (widen, upper[0], True, 3, 4), (quantize_wv, lower[0]),
+            (normalize, 0), (normalize, 1), (wk_on_vector, 0, 0), (normalize, 2), (quantize_hn, 0), (normalize, 3),
+            (quantize_wk, 0, 0), (quantize_wk, 0, 1), (quantize_hn, 1), (wk_on_vector, 1, 1), (quantize_hn, 2),
+            (widen, lower[1], True, 3, 4), (quantize_hn, 3), (quantize_wk, 1, 0), (quantize_wk, 1, 1)]
+
+        slice0 = [(second_product, 0, g, i, i + 1) for g in range(G) for i in range(NT)]
+        last_ahead = G - 3
+
+        def paced(g):
+            return NT * g - g // LAG
+
+        for g in range(G):
+            if g <= last_ahead:
+                fills, empties = halves(wk_on_tensor, g + 2, 0), halves(wk_out, g + 2, 0)
+            else:
+                unit = lower[G - 1] if g == G - 2 else upper[1]
+                fills, empties = halves(wv_on_tensor, unit), halves(wv_out, unit)
+            if g < 2:
+                fills[1] += halves(wv_on_tensor, upper[0])[g]
+                empties[1] += halves(wv_out, upper[0])[g]
+            if g == last_ahead:
+                for b in range(2):
+                    fills[b] += halves(wv_on_tensor, lower[g + 1])[b]
+                    empties[b] += [planes(upper[3])[b]] + halves(wv_out, lower[g + 1])[b]
+            for a in range(2):
+                tensor += [(first_product, g, 2 * a), (first_product, g, 2 * a + 1)] + fills[a]
+                scalar += [(rectify, g, 2 * a), (rectify, g, 2 * a + 1)] + empties[a] + [(square, g, a)]
+            tensor += slice0[paced(max(g - 1, 0)):paced(g)]
+            if g <= last_ahead:
+                between = (wv_on_vector, lower[g + 1]) if g < last_ahead else (widen, upper[1], True, 0, PACK)
+                vector += [(wk_on_vector, g + 2, 1), (widen, lower[g + 2], True, 0, PACK), (quantize_wk, g + 2, 1), between,
+                           (quantize_wk, g + 2, 0), (quantize_wv, lower[g + 1]), (quantize_k, g)]
+            if g == 1:
+                vector += [(quantize_wv, upper[0])]
+        vector += [
+            (widen, upper[2], True, 0, PACK), (widen, upper[7], True, 0, PACK), (wv_on_vector, upper[2]),
+            (widen, upper[3], True, 2, PACK), (quantize_wv, lower[7]), (quantize_wv, upper[2]), (quantize_k, 6),
+            (wv_on_vector, upper[7]), (widen, right[2], True, 0, PACK), (wv_on_vector, upper[3]), (quantize_wv, upper[7]),
+            (quantize_wv, upper[1]), (quantize_k, 7), (wv_on_vector, right[2]), (quantize_wv, upper[3])]
+
+        for unit in right[:2] + left:
+            scalar += planes(unit)
+        scalar += [(wv_on_scalar, left[1])]
+        tensor += slice0[paced(G - 1):-NT] + products(1, (0, 2)) + products(2, (0, 2)) + slice0[-NT:] + products(1, (1,))
         tensor += products(2, (1, 7, 3, 6)) + products(1, (7, 3)) + products(2, (4, 5)) + products(1, (4, 6, 5))
-        vector += [(finish, 0, 0), (finish, 0, 1), (quantize_wv, right[2]), (wv_on_vector, late[1]), (wv_on_vector, late[2]), (quantize_wv, late[1]),
-                   (quantize_wv, late[2]), (wv_on_vector, late[3]), (finish, 0, 2), (quantize_wv, late[3]),
-                   (wv_on_vector, late[5]), (finish, 0, 3), (quantize_wv, late[5]), (quantize_wv, late[4]),
-                   (finish, 2, 0), (finish, 2, 1), (finish, 1, 0), (finish, 1, 1)]
+        vector += [
+            (finish, 0, 0), (finish, 0, 1), (quantize_wv, right[2]), (wv_on_vector, right[0]), (wv_on_vector, right[1]),
+            (quantize_wv, right[0]), (quantize_wv, right[1]), (wv_on_vector, left[0]), (finish, 0, 2), (quantize_wv, left[0]),
+            (wv_on_vector, left[2]), (finish, 0, 3), (quantize_wv, left[2]), (quantize_wv, left[1]),
+            (finish, 2, 0), (finish, 2, 1), (finish, 1, 0), (finish, 1, 1)]
 
-        def widened(u):
-            return [job for job in vector + scalar if job[0] is widen and job[1] == u]
+        jobs = sync + tensor + scalar + vector
+        emptied_by = {wk_on_tensor: wk_out, wv_on_tensor: wv_out, first_product: rectify, turn_hn: hn_out}
+        filled_by = {emptied_by[f]: f for f in emptied_by}
+        steps_done = [(rectify, G - 1, NT - 1), (wv_out, upper[1], 1)]
 
-        def grouped_by(u):
-            return [job for job in vector + scalar if job[0] in (wv_on_vector, wv_on_scalar, wv_out) and job[1] == u]
+        def those(kinds, *key):
+            return [job for job in jobs if job[0] in kinds and job[1:1 + len(key)] == key]
 
-        def needs(job):
+        def makers(job):
             f, a = job[0], job[1:]
+            if f in filled_by:
+                return [(filled_by[f],) + a]
             if f is spread_gain:
                 return [(load_gain,)]
             if f is sum_squares:
-                return [(load_h, a[0])]
+                return [(load_h,) + a]
             if f is normalize:
-                return [(root, a[0]), (spread_gain,)]
+                return [(root,) + a, (spread_gain,)]
             if f is turn_hn:
-                return [(normalize, a[0])]
-            if f is hn_out:
-                return [(turn_hn, a[0])]
+                return [(normalize,) + a]
             if f is quantize_hn:
-                return [(hn_out, a[0])]
+                return [(hn_out,) + a]
             if f in (wk_on_tensor, wk_on_vector):
-                return [(load_wk, a[0], a[1])]
-            if f is wk_out:
-                return [(wk_on_tensor,) + a]
+                return [(load_wk,) + a[:2]]
             if f is quantize_wk:
-                return [(wk_out,) + a + (1,)] if (wk_out,) + a + (1,) in scalar else [(wk_on_vector,) + a]
+                return those((wk_out, wk_on_vector), *a)
             if f is widen:
-                return [j for j in sync if j[0] is load_scale and j[1] <= a[0][0] < j[2]] + [
-                    j for j in sync if j[0] is load_wv and j[1] == a[0][0] and j[2] < a[3]] + [
-                    j for j in widened(a[0]) if j[3] == 0 < a[2]]
+                unit, on_vector, first, last = a
+                return ([j for j in those((load_scale,)) if j[1] <= unit[0] < j[2]]
+                        + [j for j in those((load_wv,), unit[0]) if j[2] < last]
+                        + [j for j in those((widen,), unit) if j[3] == 0 < first])
             if f in (wv_on_vector, wv_on_scalar, wv_on_tensor):
-                return widened(a[0])
-            if f is wv_out:
-                return [(wv_on_tensor,) + a]
+                return those((widen,), a[0])
             if f is quantize_wv:
-                return grouped_by(a[0])
+                return those((wv_on_vector, wv_on_scalar, wv_out), *a)
             if f is first_product:
-                return [(quantize_wk, a[0], q) for q in range(Q)] + [(quantize_hn, a[1] // 2 * 2), (quantize_hn, a[1] // 2 * 2 + 1)]
-            if f is rectify:
-                return [(first_product,) + a]
+                return those((quantize_wk,), a[0]) + [(quantize_hn, a[1] // 2 * 2), (quantize_hn, a[1] // 2 * 2 + 1)]
             if f is quantize_k:
                 return [(square, a[0], 1)]
             if f is second_product:
                 c0 = SLICES[a[0]][0]
-                unit = [u for u in lower + upper if u[0] == a[1] and u[1] <= c0 < u[1] + u[2]][0]
-                return [(quantize_k, a[1]), (quantize_wv, unit)] + freed.get(a[:2], [])
+                return ([(quantize_wv, u) for u in units if u[0] == a[1] and u[1] <= c0 < u[1] + u[2]]
+                        + [(quantize_k, a[1])] + ([(normalize, NT - 1)] if a[0] == 0 else steps_done))
             if f is finish:
-                return [j for j in tensor if j[:2] == (second_product, a[0]) and j[3] <= (a[1] + 1) * (HALF // SLICES[a[0]][1]) - 1 < j[4]]
+                last_tile = (a[1] + 1) * (HALF // SLICES[a[0]][1]) - 1
+                return [j for j in those((second_product,), a[0]) if j[3] <= last_tile < j[4]]
             if f is store:
                 return [(finish,) + a]
             return []
 
-        def last_readers(job):
+        def takes(job):
             f, a = job[0], job[1:]
+            if f in emptied_by:
+                return "work", [(emptied_by[f],) + a]
             if f is load_wk:
-                return "wk_raw", 5, [j for j in tensor + vector if j[0] in (wk_on_tensor, wk_on_vector) and j[1:3] == a]
+                return "wk_raw", those((wk_on_tensor, wk_on_vector), *a)
             if f is wk_on_vector or (f is wk_out and a[2] == 0):
-                return "wk_grouped", 4, [(quantize_wk,) + a[:2]]
+                return "wk_grouped", [(quantize_wk,) + a[:2]]
             if f is quantize_wk:
-                return "wk_codes", 5, [(first_product, a[0], NT - 1)]
+                return "wk_codes", [(first_product, a[0], NT - 1)]
             if f is widen and a[2] == 0:
-                return ("planes", a[1]), 4, [
-                    j for j in tensor + vector + scalar if j[0] in (wv_on_tensor, wv_on_vector, wv_on_scalar) and j[1] == a[0]]
+                tag = "planes_vector" if a[1] else "planes_scalar"
+                return tag, those((wv_on_tensor, wv_on_vector, wv_on_scalar), a[0])
             if f in (wv_on_vector, wv_on_scalar) or (f is wv_out and a[1] == 0):
-                return "wv_grouped", 3, [(quantize_wv, a[0])]
+                return "wv_grouped", [(quantize_wv, a[0])]
             if f is square and a[1] == 0:
-                return "k_grouped", 3, [(quantize_k, a[0])]
+                return "k_grouped", [(quantize_k, a[0])]
             if f is normalize:
-                return "hn", 2, [(turn_hn, a[0])]
+                return "hn", [(turn_hn,) + a]
             if f is hn_out:
-                return "hn_grouped", 2, [(quantize_hn, a[0])]
+                return "hn_grouped", [(quantize_hn,) + a]
             if f is finish:
-                return "result", 5, [(store,) + a]
-            return None, 0, []
+                return "result", [(store,) + a]
+            return None, []
 
-        emptied_by = {wk_on_tensor: wk_out, wv_on_tensor: wv_out, first_product: rectify, turn_hn: hn_out}
-        bank_user = {}
-        freed = {(0, 0): [(normalize, NT - 1)], (1, 0): [(rectify, G - 1, NT - 1), (wv_out, upper[1], 1)], (2, 0): [(rectify, G - 1, NT - 1), (wv_out, upper[1], 1)]}
-        written, rings = set(), {}
         queues = [sync, tensor, scalar, vector]
         at = [0] * len(queues)
-        count = 0
-        while any(at[e] < len(queues[e]) for e in range(len(queues))):
-            moved = False
+        written, readers_of = set(), {}
+        while len(written) < len(jobs):
+            before = len(written)
             for e in range(len(queues)):
                 if at[e] == len(queues[e]):
                     continue
                 job = queues[e][at[e]]
-                wanted = list(needs(job))
-                ring, depth, readers = last_readers(job)
-                if ring is not None and len(rings.setdefault(ring, [])) >= depth:
-                    wanted += rings[ring][-depth]
-                if job[0] in emptied_by:
-                    bank = count % 4
-                    wanted += bank_user.get(bank, [])
+                wanted = makers(job)
+                tag, readers = takes(job)
+                taken = readers_of.setdefault(tag, [])
+                depth = DEPTH.get(tag, WORK_BANKS)
+                if tag is not None and len(taken) >= depth:
+                    wanted = wanted + taken[-depth]
                 if all(w in written for w in wanted):
-                    if ring is not None:
-                        rings[ring].append(readers)
-                    if job[0] in emptied_by:
-                        turn[0] = bank
-                        bank_user[bank] = [(emptied_by[job[0]],) + job[1:]]
-                        count += 1
+                    taken.append(readers)
                     job[0](*job[1:])
                     written.add(job)
                     at[e] += 1
-                    moved = True
-            assert moved, [queues[e][at[e]:at[e] + 1] for e in range(len(queues))]
+            assert len(written) > before, "the lists wait for each other"

@@ -23,15 +23,20 @@ NT = S // P
 G = FF // K_PASS
 Q = D // K_PASS
 HALF = D // 2
-
 QUARTER = D // 4
+BANK = 512
+RUN = 2
 
 SLICES = ((0, HALF), (HALF, QUARTER), (HALF + QUARTER, QUARTER))
-WORK_BANKS = 4
-RUN = 2
+WHOLE = [(0, D)]
+HALVES = [(0, HALF), (HALF, HALF)]
+BY_SLICE = list(SLICES)
+WIDENED = {g: WHOLE if g in (0, 6, 7) else HALVES if g in (1, 2) else BY_SLICE for g in range(G)}
+QUANTIZED = {g: HALVES if g == 0 else WIDENED[g] for g in range(G)}
 LAG = 2
-DEPTH = {"wk_raw": 5, "wk_grouped": 4, "wk_codes": 5, "wk_scales": 5, "planes_vector": 4, "planes_scalar": 4,
-         "wv_grouped": 3, "relu": 2, "k_grouped": 3, "hn": 2, "hn_grouped": 2, "result": 5}
+BANKS = ("acc", "work")
+DEPTH = {"acc": 4, "work": 4, "wk_raw": 4, "wk_grouped": 2, "wk_codes": 2, "wk_scales": 2, "wv_bytes": 7, "planes_wide": 2, "planes": 4,
+         "wv_grouped_wide": 2, "wv_grouped": 3, "relu": 2, "k_grouped": 3, "result": 6}
 
 
 def tile_block_pc_kernel(tc, h_attn, norm2_w, ffn_wk, ffn_wv_bytes, ffn_wv_scale, out):
@@ -42,13 +47,6 @@ def tile_block_pc_kernel(tc, h_attn, norm2_w, ffn_wk, ffn_wv_bytes, ffn_wv_scale
     wv_v = ffn_wv_bytes.rearrange("(g p t) n -> g p t n", p=P, t=PACK)
     scale_v = ffn_wv_scale.rearrange("(g p t) o -> p g (t o)", p=P, t=PACK)
 
-    split = (4, 5, 6)
-    lower = [(g, 0, HALF) for g in range(G)]
-    upper = {g: (g, HALF, HALF) for g in range(G) if g not in split}
-    left = [(g,) + SLICES[1] for g in split]
-    right = [(g,) + SLICES[2] for g in split]
-    units = lower + [upper[g] for g in upper] + left + right
-
     with ExitStack() as ctx:
         keep = ctx.enter_context(tc.tile_pool(name="keep", bufs=1))
         stream = ctx.enter_context(tc.tile_pool(name="stream", bufs=1))
@@ -58,7 +56,6 @@ def tile_block_pc_kernel(tc, h_attn, norm2_w, ffn_wk, ffn_wv_bytes, ffn_wv_scale
         h_sb = keep.tile([P, NT, D], BF16, align_bytes=64, name="h_sb")
         h_codes = keep.tile([P, Q, S], U32, align_bytes=64, name="h_codes")
         h_scales = keep.tile([P, Q, S], U8, align_bytes=64, name="h_scales")
-        wv_bytes = keep.tile([P, G, PACK, D], U8, align_bytes=64, name="wv_bytes")
         wv_scale = keep.tile([P, G, 2 * PACK], F32, align_bytes=64, name="wv_scale")
         wv_codes = keep.tile([P, G, D], U32, align_bytes=64, name="wv_codes")
         wv_scales = keep.tile([P, G, D], U8, align_bytes=64, name="wv_scales")
@@ -71,23 +68,41 @@ def tile_block_pc_kernel(tc, h_attn, norm2_w, ffn_wk, ffn_wv_bytes, ffn_wv_scale
         sumsq = keep.tile([P, NT], F32, align_bytes=64, name="sumsq")
         rstd = keep.tile([P, NT], F32, align_bytes=64, name="rstd")
 
-        def buffer(shape, dtype, tag):
-            return stream.tile(shape, dtype, align_bytes=64, name=tag, bufs=DEPTH[tag])
+        held, taken = {}, {}
 
-        banks = {}
+        def buffer(key, shape=None, dtype=None):
+            if key not in held:
+                tag = key[0]
+                turn = len(taken.setdefault(tag, []))
+                taken[tag].append(key)
+                if tag in BANKS:
+                    held[key] = psum.tile(shape, dtype, name="%s%d" % (tag, turn % DEPTH[tag]))
+                else:
+                    held[key] = stream.tile(shape, dtype, align_bytes=64, name=tag, bufs=DEPTH[tag])
+            return held[key]
 
-        def work_bank(key, shape, dtype):
-            banks[key] = psum.tile(shape, dtype, name="work%d" % (len(banks) % WORK_BANKS))
-            return banks[key]
+        def covering(runs, g, c):
+            return [(c0, w) for c0, w in runs[g] if c0 <= c < c0 + w][0]
 
-        wk_raw = {}
+        def planes_key(g, c):
+            c0, w = covering(WIDENED, g, c)
+            return ("planes_wide" if w > HALF else "planes", g, c0, w)
 
-        def load_wk(g, q):
-            wk_raw[g, q] = buffer([P, PACK, K_PASS], BF16, "wk_raw")
-            nc.sync.dma_start(out=wk_raw[g, q][:], in_=wk_v[g, q])
+        def grouped_key(g, c):
+            c0, w = covering(QUANTIZED, g, c)
+            return ("wv_grouped_wide" if w > HALF else "wv_grouped", g, c0, w)
+
+        def acc_key(sl, i):
+            return ("acc" if sl == 0 else "work", "sum", sl, i // (BANK // SLICES[sl][1]))
+
+        def load_wk(g, q, b0, b1):
+            raw = buffer(("wk_raw", g, q), [P, PACK, K_PASS], BF16)
+            cols = slice(2 * P * b0, 2 * P * b1)
+            nc.sync.dma_start(out=raw[:, :, cols], in_=wk_v[g, q][:, :, cols])
 
         def load_wv(g, first, last):
-            nc.sync.dma_start(out=wv_bytes[:, g, first:last, :], in_=wv_v[g][:, first:last, :])
+            raw = buffer(("wv_bytes", g), [P, PACK, D], U8)
+            nc.sync.dma_start(out=raw[:, first:last, :], in_=wv_v[g][:, first:last, :])
 
         def load_scale(first, last):
             nc.sync.dma_start(out=wv_scale[:, first:last, 0:PACK], in_=scale_v[:, first:last, :])
@@ -98,108 +113,118 @@ def tile_block_pc_kernel(tc, h_attn, norm2_w, ffn_wk, ffn_wv_bytes, ffn_wv_scale
         def load_h(i):
             nc.sync.dma_start(out=h_sb[:, i, :], in_=h_v[i])
 
-        wk_grouped, wk_codes, wk_scales = {}, {}, {}
+        def wk_grouped(g, q):
+            return buffer(("wk_grouped", g), [P, Q * K_PASS * PACK], BF16)[:, q * K_PASS * PACK:(q + 1) * K_PASS * PACK]
 
-        def wk_on_tensor(g, q, b):
-            bank = work_bank(("wk", g, q, b), [P, PACK, 64, PACK], BF16)
-            for part in range(2):
+        def wk_on_tensor(g, q, b, first=0, last=2):
+            bank = buffer(("work", "wk", g, q, b), [P, PACK, 64, PACK], BF16)
+            for part in range(first, last):
                 c0 = 2 * P * b + P * part
                 nc.tensor.matmul(
                     bank[:, :, 32 * part:32 * part + 32, :].rearrange("p t m j -> p j m t"),
                     lhsT=ident_bf16[:],
-                    rhs=wk_raw[g, q][:, :, c0:c0 + P].rearrange("p j (m t) -> p j m t", t=PACK),
+                    rhs=buffer(("wk_raw", g, q))[:, :, c0:c0 + P].rearrange("p j (m t) -> p j m t", t=PACK),
                     start=True,
                     stop=True,
                 )
 
         def wk_out(g, q, b):
-            if b == 0:
-                wk_grouped[g, q] = buffer([P, K_PASS * PACK], BF16, "wk_grouped")
             nc.scalar.copy(
-                out=wk_grouped[g, q][:].bitcast(F32).rearrange("p (t w) -> p t w", t=PACK)[:, :, P * b:P * b + P],
-                in_=banks["wk", g, q, b][:].rearrange("p t m j -> p t (m j)").bitcast(F32),
+                out=wk_grouped(g, q).bitcast(F32).rearrange("p (t w) -> p t w", t=PACK)[:, :, P * b:P * b + P],
+                in_=buffer(("work", "wk", g, q, b))[:].rearrange("p t m j -> p t (m j)").bitcast(F32),
             )
 
         def wk_on_vector(g, q):
-            wk_grouped[g, q] = buffer([P, K_PASS * PACK], BF16, "wk_grouped")
             for u in range(2):
                 nc.vector.tensor_copy(
-                    out=wk_grouped[g, q][:].rearrange("p (u e m j) -> p u m j e", u=2, e=2, j=PACK)[:, u, :, :, :],
-                    in_=wk_raw[g, q][:].rearrange("p j (m u e) -> p u m j e", u=2, e=2)[:, u, :, :, :],
+                    out=wk_grouped(g, q).rearrange("p (u e m j) -> p u m j e", u=2, e=2, j=PACK)[:, u, :, :, :],
+                    in_=buffer(("wk_raw", g, q))[:].rearrange("p j (m u e) -> p u m j e", u=2, e=2)[:, u, :, :, :],
                 )
 
-        def quantize_wk(g, q):
-            wk_codes[g, q] = buffer([P, K_PASS], U32, "wk_codes")
-            wk_scales[g, q] = buffer([P, K_PASS], U8, "wk_scales")
+        def wk_operand(g):
+            return (buffer(("wk_codes", g), [P, Q * K_PASS], U32), buffer(("wk_scales", g), [P, Q * K_PASS], U8))
+
+        def quantize_wk(g, q0, q1):
+            codes, scales = wk_operand(g)
             nc.vector.quantize_mx(
-                out=wk_codes[g, q][:].bitcast(FP8X4), scales=wk_scales[g, q][:], in_=wk_grouped[g, q][:])
+                out=codes[:, q0 * K_PASS:q1 * K_PASS].bitcast(FP8X4),
+                scales=scales[:, q0 * K_PASS:q1 * K_PASS],
+                in_=buffer(("wk_grouped", g))[:, q0 * K_PASS * PACK:q1 * K_PASS * PACK],
+            )
 
-        wv_planes, wv_grouped = {}, {}
+        def planes(g, c0, w):
+            key = planes_key(g, c0)
+            return buffer(key, [P, PACK, key[3]], BF16)[:, :, c0 - key[2]:c0 - key[2] + w]
 
-        def widen(unit, on_vector, first, last):
-            g, c0, w = unit
-            if first == 0:
-                wv_planes[unit] = buffer([P, PACK, w], BF16, "planes_vector" if on_vector else "planes_scalar")
+        def grouped(g, c0, w):
+            key = grouped_key(g, c0)
+            return buffer(key, [P, key[3] * PACK], BF16)[:, (c0 - key[2]) * PACK:(c0 - key[2] + w) * PACK]
+
+        def fp8_plane(g, c0, w, t):
+            return buffer(("wv_bytes", g))[:, t, c0:c0 + w].bitcast(FP8)
+
+        def widen_on_vector(g, c0, w, first, last):
             for t in range(first, last):
-                values = wv_bytes[:, g, t, c0:c0 + w].bitcast(FP8)
-                scale = wv_scale[:, g, t:t + 1]
-                if on_vector:
-                    nc.vector.tensor_scalar(
-                        out=wv_planes[unit][:, t, :], in0=values, scalar1=scale, scalar2=None, op0=ALU.mult)
-                else:
-                    nc.scalar.activation(out=wv_planes[unit][:, t, :], in_=values, func=ACT.Copy, scale=scale)
+                nc.vector.tensor_scalar(
+                    out=planes(g, c0, w)[:, t, :], in0=fp8_plane(g, c0, w, t), scalar1=wv_scale[:, g, t:t + 1],
+                    scalar2=None, op0=ALU.mult)
 
-        def interleaving_views(unit):
-            wv_grouped[unit] = buffer([P, unit[2] * PACK], BF16, "wv_grouped")
-            return (wv_grouped[unit][:].rearrange("p (c i t) -> p c t i", i=RUN, t=PACK),
-                    wv_planes[unit][:].rearrange("p t (c i) -> p c t i", i=RUN))
+        def widen_on_scalar(g, c0, w, first, last):
+            for t in range(first, last):
+                nc.scalar.activation(
+                    out=planes(g, c0, w)[:, t, :], in_=fp8_plane(g, c0, w, t), func=ACT.Copy, scale=wv_scale[:, g, t:t + 1])
 
-        def wv_on_vector(unit):
-            grouped, spread = interleaving_views(unit)
-            nc.vector.tensor_copy(out=grouped, in_=spread)
+        def interleaving_views(g, c0, w):
+            return (grouped(g, c0, w).rearrange("p (c i t) -> p c t i", i=RUN, t=PACK),
+                    planes(g, c0, w).rearrange("p t (c i) -> p c t i", i=RUN))
 
-        def wv_on_scalar(unit):
-            grouped, spread = interleaving_views(unit)
-            nc.scalar.copy(out=grouped, in_=spread)
+        def wv_on_vector(g, c0, w):
+            together, apart = interleaving_views(g, c0, w)
+            nc.vector.tensor_copy(out=together, in_=apart)
 
-        def wv_on_tensor(unit, b):
-            bank = work_bank(("wv", unit, b), [P, 2 * P, PACK], BF16)
+        def wv_on_scalar(g, c0, w):
+            together, apart = interleaving_views(g, c0, w)
+            nc.scalar.copy(out=together, in_=apart)
+
+        def wv_on_gpsimd(g, c0, w):
+            nc.gpsimd.tensor_scalar(
+                out=grouped(g, c0, w).rearrange("p (n t) -> p n t", t=PACK),
+                in0=planes(g, c0, w).rearrange("p t n -> p n t"),
+                scalar1=1.0, scalar2=0.0, op0=ALU.mult, op1=ALU.add)
+
+        def wv_on_tensor(g, c0):
+            bank = buffer(("work", "wv", g, c0), [P, QUARTER, PACK], BF16)
             for part in range(2):
-                c0 = 2 * P * b + P * part
                 nc.tensor.matmul(
                     bank[:, P * part:P * part + P, :].rearrange("p n t -> p t n"),
                     lhsT=ident_bf16[:],
-                    rhs=wv_planes[unit][:, :, c0:c0 + P],
+                    rhs=planes(g, c0 + P * part, P),
                     start=True,
                     stop=True,
                 )
 
-        def wv_out(unit, b):
-            if b == 0:
-                wv_grouped[unit] = buffer([P, unit[2] * PACK], BF16, "wv_grouped")
+        def wv_out(g, c0):
             nc.scalar.copy(
-                out=wv_grouped[unit][:].bitcast(F32)[:, HALF * b:HALF * b + HALF],
-                in_=banks["wv", unit, b][:].rearrange("p n t -> p (n t)").bitcast(F32),
+                out=grouped(g, c0, QUARTER).bitcast(F32),
+                in_=buffer(("work", "wv", g, c0))[:].rearrange("p n t -> p (n t)").bitcast(F32),
             )
 
-        def quantize_wv(unit):
-            g, c0, w = unit
+        def quantize_wv(g, c0, w):
             nc.vector.quantize_mx(
-                out=wv_codes[:, g, c0:c0 + w].bitcast(FP8X4), scales=wv_scales[:, g, c0:c0 + w], in_=wv_grouped[unit][:])
-
-        relu, k_grouped = {}, {}
+                out=wv_codes[:, g, c0:c0 + w].bitcast(FP8X4), scales=wv_scales[:, g, c0:c0 + w], in_=grouped(g, c0, w))
 
         def first_product(g, i):
             a, u = divmod(i, 2)
             tokens = slice(2 * P * a, 2 * P * (a + 1))
-            bank = work_bank(("hidden", g, i), [P, 2, 2 * P], F32)
+            bank = buffer(("work", "hidden", g, i), [P, 2, 2 * P], F32)
+            codes, scales = wk_operand(g)
             for e in range(2):
-                t = 2 * u + e
                 for q in range(Q):
+                    cols = slice(q * K_PASS + (2 * u + e) * P, q * K_PASS + (2 * u + e + 1) * P)
                     nc.tensor.matmul_mx(
                         out=bank[:, e, :],
-                        lhsT=wk_codes[g, q][:, t * P:(t + 1) * P].bitcast(FP8X4),
-                        lhsT_scale=wk_scales[g, q][:, t * P:(t + 1) * P],
+                        lhsT=codes[:, cols].bitcast(FP8X4),
+                        lhsT_scale=scales[:, cols],
                         rhs=h_codes[:, q, tokens].bitcast(FP8X4),
                         rhs_scale=h_scales[:, q, tokens],
                         start=(q == 0),
@@ -208,67 +233,61 @@ def tile_block_pc_kernel(tc, h_attn, norm2_w, ffn_wk, ffn_wv_bytes, ffn_wv_scale
 
         def rectify(g, i):
             a, u = divmod(i, 2)
-            if u == 0:
-                relu[g, a] = buffer([P, 2, 2 * P, 2], F32, "relu")
             nc.scalar.activation(
-                out=relu[g, a][:, u, :, :], in_=banks["hidden", g, i][:].rearrange("p e n -> p n e"), func=ACT.Relu)
+                out=buffer(("relu", g, a), [P, 2, 2 * P, 2], F32)[:, u, :, :],
+                in_=buffer(("work", "hidden", g, i))[:].rearrange("p e n -> p n e"), func=ACT.Relu)
 
         def square(g, a):
-            if a == 0:
-                k_grouped[g] = buffer([P, 2, 2 * P, 2, 2], BF16, "k_grouped")
             nc.scalar.activation(
-                out=k_grouped[g][:, a, :, :, :], in_=relu[g, a][:].rearrange("p u n e -> p n u e"), func=ACT.Square)
+                out=buffer(("k_grouped", g), [P, 2, 2 * P, 2, 2], BF16)[:, a, :, :, :],
+                in_=buffer(("relu", g, a))[:].rearrange("p u n e -> p n u e"), func=ACT.Square)
 
-        def quantize_k(g):
+        def quantize_k(g, a0, a1):
+            tokens = slice(2 * P * a0, 2 * P * a1)
             nc.vector.quantize_mx(
-                out=k_codes[:, g, :].bitcast(FP8X4),
-                scales=k_scales[:, g, :],
-                in_=k_grouped[g][:].rearrange("p a n u e -> p (a n u e)"),
+                out=k_codes[:, g, tokens].bitcast(FP8X4),
+                scales=k_scales[:, g, tokens],
+                in_=buffer(("k_grouped", g))[:, a0:a1, :, :, :].rearrange("p a n u e -> p (a n u e)"),
             )
 
-        acc, passes, result = {}, {}, {}
+        passes = {}
 
         def second_product(sl, g, first, last):
             c0, w = SLICES[sl]
-            share = HALF // w
+            share = BANK // w
             for i in range(first, last):
-                b, r = divmod(i, share)
-                if (sl, b) not in acc:
-                    acc[sl, b] = psum.tile([P, share, w], F32, name="acc%d" % b if sl == 0 else "work%d" % (2 * (sl - 1) + b))
-                passes[sl, b] = passes.get((sl, b), 0) + 1
+                key = acc_key(sl, i)
+                passes[key] = passes.get(key, 0) + 1
                 nc.tensor.matmul_mx(
-                    out=acc[sl, b][:, r, :],
+                    out=buffer(key, [P, share, w], F32)[:, i % share, :],
                     lhsT=k_codes[:, g, i * P:(i + 1) * P].bitcast(FP8X4),
                     lhsT_scale=k_scales[:, g, i * P:(i + 1) * P],
                     rhs=wv_codes[:, g, c0:c0 + w].bitcast(FP8X4),
                     rhs_scale=wv_scales[:, g, c0:c0 + w],
-                    start=(passes[sl, b] == 1),
-                    stop=(passes[sl, b] == G * share),
+                    start=(passes[key] == 1),
+                    stop=(passes[key] == G * share),
                 )
 
-        def finish(sl, b):
+        def finish(sl, first, last):
             c0, w = SLICES[sl]
-            share = HALF // w
-            tiles = slice(b * share, (b + 1) * share)
-            result[sl, b] = buffer([P, share, w], F32, "result")
-            nc.vector.tensor_tensor(out=result[sl, b][:], in0=acc[sl, b][:], in1=h_sb[:, tiles, c0:c0 + w], op=ALU.add)
+            share = BANK // w
+            nc.vector.tensor_tensor(
+                out=buffer(("result", sl, first), [P, last - first, w], F32)[:],
+                in0=buffer(acc_key(sl, first))[:, first % share:first % share + last - first, :],
+                in1=h_sb[:, first:last, c0:c0 + w], op=ALU.add)
 
-        def store(sl, b):
+        def store(sl, first, last):
             c0, w = SLICES[sl]
-            share = HALF // w
-            nc.sync.dma_start(out=out_v[:, b * share:(b + 1) * share, c0:c0 + w], in_=result[sl, b][:])
-
-        gain_all, hn, hn_grouped = [], {}, {}
+            nc.sync.dma_start(out=out_v[:, first:last, c0:c0 + w], in_=buffer(("result", sl, first))[:])
 
         def spread_gain():
+            bank = buffer(("acc", "gain"), [P, D], BF16)
             for q in range(Q):
-                bank = psum.tile([P, K_PASS], F32, name="acc%d" % q)
-                nc.tensor.matmul(
-                    bank[:], lhsT=ones[:], rhs=gain_row[:, q * K_PASS:(q + 1) * K_PASS], start=True, stop=True)
-                gain_all.append(bank)
+                cols = slice(q * K_PASS, (q + 1) * K_PASS)
+                nc.tensor.matmul(bank[:, cols], lhsT=ones[:], rhs=gain_row[:, cols], start=True, stop=True)
 
         def sum_squares(i):
-            squares = buffer([P, D], BF16, "k_grouped")
+            squares = buffer(("k_grouped", "squares", i), [P, D], BF16)
             nc.scalar.activation(out=squares[:], in_=h_sb[:, i, :], func=ACT.Square, accum_out=sumsq[:, i:i + 1])
 
         def root(i):
@@ -276,29 +295,26 @@ def tile_block_pc_kernel(tc, h_attn, norm2_w, ffn_wk, ffn_wv_bytes, ffn_wv_scale
                 out=rstd[:, i:i + 1], in_=sumsq[:, i:i + 1], func=ACT.Abs_reciprocal_sqrt, scale=1.0 / D, bias=EPS)
 
         def normalize(i):
-            hn[i] = buffer([P, D], BF16, "hn")
+            hn = buffer(("result", "hn", i), [P, 2, HALF], BF16)
             for v in range(2):
-                for q in range(Q):
-                    values = h_sb[:, i, q * K_PASS:(q + 1) * K_PASS].rearrange("p (m v e) -> p v m e", v=2, e=2)
-                    gains = gain_all[q][:].rearrange("p (m v e) -> p v m e", v=2, e=2)
-                    first = q * K_PASS + v * 2 * P
-                    nc.vector.scalar_tensor_tensor(
-                        out=hn[i][:, first:first + 2 * P].rearrange("p (m e) -> p m e", e=2),
-                        in0=values[:, v, :, :], scalar=rstd[:, i:i + 1], in1=gains[:, v, :, :],
-                        op0=ALU.mult, op1=ALU.mult)
+                nc.vector.scalar_tensor_tensor(
+                    out=hn[:, v, :].rearrange("p (m e) -> p m e", e=2),
+                    in0=h_sb[:, i, :].rearrange("p (m v e) -> p v m e", v=2, e=2)[:, v, :, :],
+                    scalar=rstd[:, i:i + 1],
+                    in1=buffer(("acc", "gain"))[:].rearrange("p (m v e) -> p v m e", v=2, e=2)[:, v, :, :],
+                    op0=ALU.mult, op1=ALU.mult)
 
         def turn_hn(i):
-            bank = work_bank(("hn", i), [P, Q, 2, P], F32)
-            words = hn[i][:].bitcast(F32)
-            for q in range(Q):
-                for v in range(2):
-                    nc.tensor.transpose(bank[:, q, v, :], words[:, (2 * q + v) * P:(2 * q + v + 1) * P], ident_f32[:])
+            bank = buffer(("work", "hn", i), [P, Q, 2, P], F32)
+            for v in range(2):
+                words = buffer(("result", "hn", i))[:, v, :].bitcast(F32)
+                for q in range(Q):
+                    nc.tensor.transpose(bank[:, q, v, :], words[:, q * P:(q + 1) * P], ident_f32[:])
 
         def hn_out(i):
-            hn_grouped[i] = buffer([P, Q * P * PACK], BF16, "hn_grouped")
             nc.scalar.copy(
-                out=hn_grouped[i][:].bitcast(F32).rearrange("p (q n v) -> p q n v", q=Q, v=2),
-                in_=banks["hn", i][:].rearrange("p q v n -> p q n v"),
+                out=buffer(("result", "hn_grouped", i), [P, D], BF16)[:].bitcast(F32).rearrange("p (q n v) -> p q n v", q=Q, v=2),
+                in_=buffer(("work", "hn", i))[:].rearrange("p q v n -> p q n v"),
             )
 
         def quantize_hn(i):
@@ -306,7 +322,7 @@ def tile_block_pc_kernel(tc, h_attn, norm2_w, ffn_wk, ffn_wv_bytes, ffn_wv_scale
                 nc.vector.quantize_mx(
                     out=h_codes[:, q, i * P:(i + 1) * P].bitcast(FP8X4),
                     scales=h_scales[:, q, i * P:(i + 1) * P],
-                    in_=hn_grouped[i][:, q * K_PASS:(q + 1) * K_PASS],
+                    in_=buffer(("result", "hn_grouped", i))[:, q * K_PASS:(q + 1) * K_PASS],
                 )
 
         nc.vector.memset(ones[:], 1.0)
@@ -316,177 +332,165 @@ def tile_block_pc_kernel(tc, h_attn, norm2_w, ffn_wk, ffn_wv_bytes, ffn_wv_scale
         warm = keep.tile([P, 1], F32, align_bytes=64, name="warm")
         nc.scalar.activation(out=warm[:], in_=ones[:, 0:1], func=ACT.Abs_reciprocal_sqrt)
 
+        def cells(name, g, c0, w, *rest):
+            return [(name, g, c) + rest for c in range(c0 // P, (c0 + w) // P)]
 
-        def planes(unit):
-            return [(widen, unit, False, t, t + 1) for t in range(PACK)]
+        def all_planes(g, c0, w):
+            return [cell for t in range(PACK) for cell in cells("plane", g, c0, w, t)]
 
-        def halves(job, *key):
-            return [[(job,) + key + (b,)] for b in range(2)]
+        def widening(g, c0, w, first, last):
+            rows = range(first, last)
+            return ([("scale", g)] + [("byte", g, t) for t in rows], [cell for t in rows for cell in cells("plane", g, c0, w, t)],
+                    [("wv_bytes", g), planes_key(g, c0)])
+
+        def interleaving(g, c0, w):
+            return all_planes(g, c0, w), cells("grouped", g, c0, w), [planes_key(g, c0), grouped_key(g, c0)]
+
+        flow = {
+            load_wk: lambda g, q, b0, b1: ([], [("raw", g, q, b) for b in range(b0, b1)], [("wk_raw", g, q)]),
+            load_wv: lambda g, first, last: ([], [("byte", g, t) for t in range(first, last)], [("wv_bytes", g)]),
+            load_scale: lambda first, last: ([], [("scale", g) for g in range(first, last)], []),
+            load_gain: lambda: ([], [("gain_row",)], []),
+            load_h: lambda i: ([], [("h", i)], []),
+            wk_on_tensor: lambda g, q, b, first=0, last=2: ([("raw", g, q, b)], [("wk_bank", g, q, b, part) for part in range(first, last)], [("wk_raw", g, q), ("work", "wk", g, q, b)]),
+            wk_out: lambda g, q, b: ([("wk_bank", g, q, b, 0), ("wk_bank", g, q, b, 1)], [("wk", g, q, b)], [("wk_grouped", g), ("work", "wk", g, q, b)]),
+            wk_on_vector: lambda g, q: (
+                [("raw", g, q, 0), ("raw", g, q, 1)], [("wk", g, q, 0), ("wk", g, q, 1)], [("wk_raw", g, q), ("wk_grouped", g)]),
+            quantize_wk: lambda g, q0, q1: (
+                [("wk", g, q, b) for q in range(q0, q1) for b in range(2)], [("wk_mx", g, q) for q in range(q0, q1)],
+                [("wk_grouped", g), ("wk_codes", g), ("wk_scales", g)]),
+            widen_on_vector: widening,
+            widen_on_scalar: widening,
+            wv_on_vector: interleaving,
+            wv_on_scalar: interleaving,
+            wv_on_gpsimd: interleaving,
+            wv_on_tensor: lambda g, c0: (
+                all_planes(g, c0, QUARTER), [("wv_bank", g, c0)], [planes_key(g, c0), ("work", "wv", g, c0)]),
+            wv_out: lambda g, c0: (
+                [("wv_bank", g, c0)], cells("grouped", g, c0, QUARTER), [grouped_key(g, c0), ("work", "wv", g, c0)]),
+            quantize_wv: lambda g, c0, w: (cells("grouped", g, c0, w), cells("wv_mx", g, c0, w), [grouped_key(g, c0)]),
+            first_product: lambda g, i: (
+                [("wk_mx", g, q) for q in range(Q)] + [("hn_mx", i // 2 * 2), ("hn_mx", i // 2 * 2 + 1)], [("hidden", g, i)],
+                [("wk_codes", g), ("wk_scales", g), ("work", "hidden", g, i)]),
+            rectify: lambda g, i: ([("hidden", g, i)], [("relu", g, i)], [("work", "hidden", g, i), ("relu", g, i // 2)]),
+            square: lambda g, a: ([("relu", g, 2 * a), ("relu", g, 2 * a + 1)], [("k", g, a)], [("relu", g, a), ("k_grouped", g)]),
+            quantize_k: lambda g, a0, a1: (
+                [("k", g, a) for a in range(a0, a1)], [("k_mx", g, a) for a in range(a0, a1)], [("k_grouped", g)]),
+            second_product: lambda sl, g, first, last: (
+                cells("wv_mx", g, *SLICES[sl]) + [("k_mx", g, i // 2) for i in range(first, last)],
+                [("part",) + acc_key(sl, i) + (g, i) for i in range(first, last)], [acc_key(sl, i) for i in range(first, last)]),
+            finish: lambda sl, first, last: (
+                [("part",) + acc_key(sl, i) + (g, i) for g in range(G) for i in range(NT) if acc_key(sl, i) == acc_key(sl, first)],
+                [("out", sl, first)], [acc_key(sl, first), ("result", sl, first)]),
+            store: lambda sl, first, last: ([("out", sl, first)], [], [("result", sl, first)]),
+            spread_gain: lambda: ([("gain_row",)], [("gain",)], [("acc", "gain")]),
+            sum_squares: lambda i: ([("h", i)], [("sum", i)], [("k_grouped", "squares", i)]),
+            root: lambda i: ([("sum", i)], [("rstd", i)], []),
+            normalize: lambda i: ([("rstd", i), ("gain",)], [("hn", i)], [("acc", "gain"), ("result", "hn", i)]),
+            turn_hn: lambda i: ([("hn", i)], [("hn_bank", i)], [("result", "hn", i), ("work", "hn", i)]),
+            hn_out: lambda i: ([("hn_bank", i)], [("hn_grouped", i)], [("work", "hn", i), ("result", "hn_grouped", i)]),
+            quantize_hn: lambda i: ([("hn_grouped", i)], [("hn_mx", i)], [("result", "hn_grouped", i)]),
+        }
+
+        def by_plane(job, g, c0, w, first=0, last=PACK):
+            return [(job, g, c0, w, t, t + 1) for t in range(first, last)]
 
         def products(sl, groups):
             return [(second_product, sl, g, 0, NT) for g in groups]
 
-        sync = [(load_scale, 0, 1)] + [(load_wv, 0, t, t + 1) for t in range(PACK)]
-        sync += [(load_h, 0), (load_gain,), (load_h, 1), (load_wk, 0, 1), (load_h, 2), (load_wk, 0, 0), (load_h, 3),
-                 (load_wk, 1, 0), (load_scale, 1, G), (load_wv, 1, 0, PACK), (load_wk, 1, 1)]
-        for g in range(2, G):
-            sync += [(load_wk, g, 0), (load_wk, g, 1), (load_wv, g, 0, PACK)]
-        sync += [(store, 0, b) for b in range(NT)] + [(store, sl, b) for sl in (2, 1) for b in range(2)]
+        def wk_half(g, b, q=0):
+            return [(wk_on_tensor, g, q, b)], [(wk_out, g, q, b)]
 
-        opening, spare = planes(upper[0]), planes(lower[1])
-        tensor = [(spread_gain,)]
-        for i in range(NT):
-            g, b = divmod(i, 2)
-            tensor += [(wk_on_tensor, g, 1 - g, b), (turn_hn, i)]
-        scalar = opening[:2] + [
-            (sum_squares, 0), (root, 0), (sum_squares, 1), (root, 1), (sum_squares, 2), (wk_out, 0, 1, 0), (root, 2),
-            (sum_squares, 3), (hn_out, 0), (root, 3), (wk_out, 0, 1, 1), (hn_out, 1), spare[0], (wk_out, 1, 0, 0),
-            spare[1], (hn_out, 2), (wk_out, 1, 0, 1), (hn_out, 3), spare[2]]
-        vector = [(widen, lower[0], True, t, t + 1) for t in range(PACK)] + [
-            (widen, upper[0], True, 2, 3), (wv_on_vector, lower[0]), (widen, upper[0], True, 3, 4), (quantize_wv, lower[0]),
-            (normalize, 0), (normalize, 1), (wk_on_vector, 0, 0), (normalize, 2), (quantize_hn, 0), (normalize, 3),
-            (quantize_wk, 0, 0), (quantize_wk, 0, 1), (quantize_hn, 1), (wk_on_vector, 1, 1), (quantize_hn, 2),
-            (widen, lower[1], True, 3, 4), (quantize_hn, 3), (quantize_wk, 1, 0), (quantize_wk, 1, 1)]
+        def wv_quarter(g, c0):
+            return [(wv_on_tensor, g, c0)], [(wv_out, g, c0)]
+
+        def both(x, y):
+            return x[0] + y[0], x[1] + y[1]
+
+        def lower(g):
+            return [(widen_on_vector, g, 0, HALF, 0, PACK)], [(wv_on_vector, g, 0, HALF)], [(quantize_wv, g, 0, HALF)]
 
         slice0 = [(second_product, 0, g, i, i + 1) for g in range(G) for i in range(NT)]
-        last_ahead = G - 3
+        R, L = SLICES[2], SLICES[1]
+
+        U = (HALF, HALF)
+        sync = [(load_scale, 0, 1), (load_wv, 0, 0, 1), (load_wv, 0, 1, 2), (load_wv, 0, 2, 3), (load_h, 0), (load_wv, 0, 3, 4), (load_gain,),
+                (load_h, 1), (load_wk, 0, 1, 0, 2), (load_h, 2), (load_wk, 0, 0, 0, 2), (load_h, 3), (load_wk, 1, 0, 0, 2), (load_scale, 1, G), (load_wv, 1, 0, 4),
+                (load_wk, 1, 1, 0, 2)]
+        for g in range(2, G):
+            sync += [(load_wk, g, 0, 0, 2), (load_wv, g, 0, PACK), (load_wk, g, 1, 0, 2)]
+        sync += [(store, 0, i, i + 1) for i in range(NT)] + [(store, 2, 0, 2), (store, 2, 2, 4)] + [(store, 1, i, i + 1) for i in range(NT)]
+        gpsimd = []
+        tensor = [(spread_gain,), (wv_on_tensor, 0, HALF), (wv_on_tensor, 0, 768), (turn_hn, 0), (wk_on_tensor, 0, 1, 0), (turn_hn, 1), (wk_on_tensor, 0, 1, 1),
+                  (turn_hn, 2), (wk_on_tensor, 1, 0, 0)]
+        scalar = [(widen_on_scalar, 0, QUARTER, 3 * QUARTER, 1, 2), (sum_squares, 0), (root, 0), (sum_squares, 1), (wv_out, 0, HALF), (root, 1), (sum_squares, 2), (wv_out, 0, 768), (root, 2),
+                  (hn_out, 0), (wk_out, 0, 1, 0), (hn_out, 1), (sum_squares, 3), (wk_out, 0, 1, 1), (root, 3), (hn_out, 2), (wk_out, 1, 0, 0), (widen_on_scalar, 1, 0, HALF, 0, 1)]
+        vector = [(widen_on_vector, 0, 0, D, 0, 1), (widen_on_vector, 0, 0, QUARTER, 1, 2), (widen_on_vector, 0, 0, D, 2, 3), (widen_on_vector, 0, 0, HALF, 3, 4), (widen_on_vector, 0, HALF, HALF, 3, 4),
+            (wv_on_vector, 0, 0, HALF), (normalize, 0), (quantize_wv, 0, 0, HALF), (normalize, 1), (wk_on_vector, 0, 0), (normalize, 2), (quantize_hn, 0), (quantize_wk, 0, 0, 1), (quantize_hn, 1),
+            (widen_on_vector, 1, 0, HALF, 1, 2), (quantize_wk, 0, 1, 2), (normalize, 3), (quantize_hn, 2), (widen_on_vector, 1, 0, HALF, 2, 4), (quantize_wv, 0, *U), (widen_on_vector, 2, 0, HALF, 0, 1), (quantize_hn, 3), (wk_on_vector, 1, 1),
+            (widen_on_vector, 2, 0, HALF, 1, 2), (quantize_wk, 1, 0, 2)]
+        tensor += [(first_product, 0, 0), (first_product, 0, 1), (turn_hn, 3), (wk_on_tensor, 1, 0, 1), (wk_on_tensor, 2, 0, 0, 0, 1), (first_product, 0, 2), (first_product, 0, 3),
+                   (wk_on_tensor, 2, 0, 0, 1, 2), (wv_on_tensor, 1, 0)]
+        scalar += [(rectify, 0, 0), (rectify, 0, 1), (hn_out, 3), (square, 0, 0), (wk_out, 1, 0, 1), (rectify, 0, 2), (rectify, 0, 3), (wk_out, 2, 0, 0), (square, 0, 1), (wv_out, 1, 0)]
+        tensor += [(first_product, 1, 0), (first_product, 1, 1), (wv_on_tensor, 1, QUARTER), (wk_on_tensor, 2, 0, 1), (first_product, 1, 2), (first_product, 1, 3), (wk_on_tensor, 3, 0, 0)] + slice0[:NT - 2]
+        scalar += [(rectify, 1, 0), (rectify, 1, 1), (wv_out, 1, QUARTER), (square, 1, 0), (wk_out, 2, 0, 1), (rectify, 1, 2), (rectify, 1, 3), (wk_out, 3, 0, 0), (square, 1, 1)]
 
         def paced(g):
-            return NT * g - g // LAG
+            return NT * g - 2 - g // LAG
 
-        for g in range(G):
-            if g <= last_ahead:
-                fills, empties = halves(wk_on_tensor, g + 2, 0), halves(wk_out, g + 2, 0)
-            else:
-                unit = lower[G - 1] if g == G - 2 else upper[1]
-                fills, empties = halves(wv_on_tensor, unit), halves(wv_out, unit)
-            if g < 2:
-                fills[1] += halves(wv_on_tensor, upper[0])[g]
-                empties[1] += halves(wv_out, upper[0])[g]
-            if g == last_ahead:
-                for b in range(2):
-                    fills[b] += halves(wv_on_tensor, lower[g + 1])[b]
-                    empties[b] += [planes(upper[3])[b]] + halves(wv_out, lower[g + 1])[b]
+        for g in range(2, G):
+            slot = [wk_half(g + 1, 1) if g + 1 < G else wv_quarter(g, 0), wk_half(g + 2, 0) if g + 2 < G else wv_quarter(g, QUARTER)]
+            if g == 6:
+                slot[1] = both(wv_quarter(g, 0), slot[1])
             for a in range(2):
-                tensor += [(first_product, g, 2 * a), (first_product, g, 2 * a + 1)] + fills[a]
-                scalar += [(rectify, g, 2 * a), (rectify, g, 2 * a + 1)] + empties[a] + [(square, g, a)]
-            tensor += slice0[paced(max(g - 1, 0)):paced(g)]
-            if g <= last_ahead:
-                between = (wv_on_vector, lower[g + 1]) if g < last_ahead else (widen, upper[1], True, 0, PACK)
-                vector += [(wk_on_vector, g + 2, 1), (widen, lower[g + 2], True, 0, PACK), (quantize_wk, g + 2, 1), between,
-                           (quantize_wk, g + 2, 0), (quantize_wv, lower[g + 1]), (quantize_k, g)]
-            if g == 1:
-                vector += [(quantize_wv, upper[0])]
+                tensor += [(first_product, g, 2 * a), (first_product, g, 2 * a + 1)] + slot[a][0]
+                scalar += [(rectify, g, 2 * a), (rectify, g, 2 * a + 1)] + slot[a][1] + [(square, g, a)]
+            tensor += slice0[paced(g - 1):paced(g)]
+        vector += [(wk_on_vector, 2, 1), (widen_on_vector, 2, 0, HALF, 2, 4), (quantize_k, 0, 0, 2)] + lower(2)[1] + lower(3)[0] + lower(1)[2] + [(quantize_wk, 2, 0, 2)] + lower(2)[2]
+        for g in range(2, 5):
+            vector += [(wk_on_vector, g + 1, 1), (quantize_k, g - 1, 0, 2)] + lower(g + 1)[1] + [(quantize_wk, g + 1, 0, 2)] + lower(g + 1)[2]
+            vector += lower(g + 2)[0] if g < 4 else [(widen_on_vector, 6, 0, D, 0, 2)]
+        vector += [(wk_on_vector, 6, 1), (quantize_k, 4, 0, 2), (widen_on_vector, 6, 0, D, 2, 4), (quantize_wk, 6, 0, 2), (wv_on_vector, 6, *U)]
+        vector += [(wk_on_vector, 7, 1), (quantize_k, 5, 0, 2), (widen_on_vector, 7, 0, D, 0, 2), (quantize_wk, 7, 0, 2), (widen_on_vector, 7, 0, D, 2, 4)]
+        vector += [(widen_on_vector, 1, *U, 0, 4), (quantize_wv, 6, 0, D), (quantize_k, 6, 0, 2), (wv_on_vector, 7, *U), (widen_on_vector, 3, *R, 0, 4), (wv_on_vector, 1, *U), (wv_on_vector, 3, *R)]
+        vector += [(quantize_wv, 7, 0, D), (quantize_wv, 1, *U), (quantize_k, 7, 0, 2), (quantize_wv, 3, *R)]
+        for g, run in ((4, R), (5, R), (3, L), (2, U), (5, L), (4, L)):
+            scalar += by_plane(widen_on_scalar, g, *run)
+        scalar += [(wv_on_scalar, 5, *L)]
+        tensor += slice0[paced(G - 1):-NT] + products(2, (0, 6, 1)) + slice0[-NT:] + products(2, (7, 3, 4)) + products(1, (0, 6))
+        tensor += products(2, (5,)) + products(1, (7, 1, 3)) + products(2, (2,)) + products(1, (2,))
+        tensor += [(second_product, 1, g, i, i + 2) for i in (0, 2) for g in (4, 5)]
         vector += [
-            (widen, upper[2], True, 0, PACK), (widen, upper[7], True, 0, PACK), (wv_on_vector, upper[2]),
-            (widen, upper[3], True, 2, PACK), (quantize_wv, lower[7]), (quantize_wv, upper[2]), (quantize_k, 6),
-            (wv_on_vector, upper[7]), (widen, right[2], True, 0, PACK), (wv_on_vector, upper[3]), (quantize_wv, upper[7]),
-            (quantize_wv, upper[1]), (quantize_k, 7), (wv_on_vector, right[2]), (quantize_wv, upper[3])]
+            (wv_on_vector, 4, *R), (finish, 0, 0, 1), (quantize_wv, 4, *R), (wv_on_vector, 5, *R), (finish, 0, 1, 2), (quantize_wv, 5, *R), (wv_on_vector, 3, *L), (finish, 0, 2, 3),
+            (quantize_wv, 3, *L), (wv_on_vector, 2, *U), (finish, 0, 3, 4), (quantize_wv, 2, *U),
+            (wv_on_vector, 4, *L), (finish, 2, 0, 2), (quantize_wv, 4, *L), (quantize_wv, 5, *L),
+            (finish, 2, 2, 4), ] + [(finish, 1, i, i + 1) for i in range(NT)]
 
-        for unit in right[:2] + left:
-            scalar += planes(unit)
-        scalar += [(wv_on_scalar, left[1])]
-        tensor += slice0[paced(G - 1):-NT] + products(1, (0, 2)) + products(2, (0, 2)) + slice0[-NT:] + products(1, (1,))
-        tensor += products(2, (1, 7, 3, 6)) + products(1, (7, 3)) + products(2, (4, 5)) + products(1, (4, 6, 5))
-        vector += [
-            (finish, 0, 0), (finish, 0, 1), (quantize_wv, right[2]), (wv_on_vector, right[0]), (wv_on_vector, right[1]),
-            (quantize_wv, right[0]), (quantize_wv, right[1]), (wv_on_vector, left[0]), (finish, 0, 2), (quantize_wv, left[0]),
-            (wv_on_vector, left[2]), (finish, 0, 3), (quantize_wv, left[2]), (quantize_wv, left[1]),
-            (finish, 2, 0), (finish, 2, 1), (finish, 1, 0), (finish, 1, 1)]
 
-        jobs = sync + tensor + scalar + vector
-        emptied_by = {wk_on_tensor: wk_out, wv_on_tensor: wv_out, first_product: rectify, turn_hn: hn_out}
-        filled_by = {emptied_by[f]: f for f in emptied_by}
-        steps_done = [(rectify, G - 1, NT - 1), (wv_out, upper[1], 1)]
-
-        def those(kinds, *key):
-            return [job for job in jobs if job[0] in kinds and job[1:1 + len(key)] == key]
-
-        def makers(job):
-            f, a = job[0], job[1:]
-            if f in filled_by:
-                return [(filled_by[f],) + a]
-            if f is spread_gain:
-                return [(load_gain,)]
-            if f is sum_squares:
-                return [(load_h,) + a]
-            if f is normalize:
-                return [(root,) + a, (spread_gain,)]
-            if f is turn_hn:
-                return [(normalize,) + a]
-            if f is quantize_hn:
-                return [(hn_out,) + a]
-            if f in (wk_on_tensor, wk_on_vector):
-                return [(load_wk,) + a[:2]]
-            if f is quantize_wk:
-                return those((wk_out, wk_on_vector), *a)
-            if f is widen:
-                unit, on_vector, first, last = a
-                return ([j for j in those((load_scale,)) if j[1] <= unit[0] < j[2]]
-                        + [j for j in those((load_wv,), unit[0]) if j[2] < last]
-                        + [j for j in those((widen,), unit) if j[3] == 0 < first])
-            if f in (wv_on_vector, wv_on_scalar, wv_on_tensor):
-                return those((widen,), a[0])
-            if f is quantize_wv:
-                return those((wv_on_vector, wv_on_scalar, wv_out), *a)
-            if f is first_product:
-                return those((quantize_wk,), a[0]) + [(quantize_hn, a[1] // 2 * 2), (quantize_hn, a[1] // 2 * 2 + 1)]
-            if f is quantize_k:
-                return [(square, a[0], 1)]
-            if f is second_product:
-                c0 = SLICES[a[0]][0]
-                return ([(quantize_wv, u) for u in units if u[0] == a[1] and u[1] <= c0 < u[1] + u[2]]
-                        + [(quantize_k, a[1])] + ([(normalize, NT - 1)] if a[0] == 0 else steps_done))
-            if f is finish:
-                last_tile = (a[1] + 1) * (HALF // SLICES[a[0]][1]) - 1
-                return [j for j in those((second_product,), a[0]) if j[3] <= last_tile < j[4]]
-            if f is store:
-                return [(finish,) + a]
-            return []
-
-        def takes(job):
-            f, a = job[0], job[1:]
-            if f in emptied_by:
-                return "work", [(emptied_by[f],) + a]
-            if f is load_wk:
-                return "wk_raw", those((wk_on_tensor, wk_on_vector), *a)
-            if f is wk_on_vector or (f is wk_out and a[2] == 0):
-                return "wk_grouped", [(quantize_wk,) + a[:2]]
-            if f is quantize_wk:
-                return "wk_codes", [(first_product, a[0], NT - 1)]
-            if f is widen and a[2] == 0:
-                tag = "planes_vector" if a[1] else "planes_scalar"
-                return tag, those((wv_on_tensor, wv_on_vector, wv_on_scalar), a[0])
-            if f in (wv_on_vector, wv_on_scalar) or (f is wv_out and a[1] == 0):
-                return "wv_grouped", [(quantize_wv, a[0])]
-            if f is square and a[1] == 0:
-                return "k_grouped", [(quantize_k, a[0])]
-            if f is normalize:
-                return "hn", [(turn_hn,) + a]
-            if f is hn_out:
-                return "hn_grouped", [(quantize_hn,) + a]
-            if f is finish:
-                return "result", [(store,) + a]
-            return None, []
-
-        queues = [sync, tensor, scalar, vector]
+        queues = [sync, tensor, scalar, vector, gpsimd]
+        jobs = [job for queue in queues for job in queue]
+        users = {}
+        for job in jobs:
+            for key in flow[job[0]](*job[1:])[2]:
+                users.setdefault(key, []).append(job)
         at = [0] * len(queues)
-        written, readers_of = set(), {}
+        written, made = set(), set()
         while len(written) < len(jobs):
             before = len(written)
             for e in range(len(queues)):
                 if at[e] == len(queues[e]):
                     continue
                 job = queues[e][at[e]]
-                wanted = makers(job)
-                tag, readers = takes(job)
-                taken = readers_of.setdefault(tag, [])
-                depth = DEPTH.get(tag, WORK_BANKS)
-                if tag is not None and len(taken) >= depth:
-                    wanted = wanted + taken[-depth]
-                if all(w in written for w in wanted):
-                    taken.append(readers)
+                reads, makes, keys = flow[job[0]](*job[1:])
+                fresh = {}
+                for key in keys:
+                    if key not in held and key not in fresh.setdefault(key[0], []):
+                        fresh[key[0]].append(key)
+                old = [key for tag in fresh for key in taken.get(tag, [])[:max(0, len(taken.get(tag, [])) + len(fresh[tag]) - DEPTH[tag])]]
+                if all(name in made for name in reads) and all(user in written for key in old for user in users[key]):
                     job[0](*job[1:])
                     written.add(job)
+                    for name in makes:
+                        made.add(name)
                     at[e] += 1
-            assert len(written) > before, "the lists wait for each other"
+            assert len(written) > before, "the lists wait for each other: %s" % [queues[e][at[e]:at[e] + 1] for e in range(len(queues))]

@@ -35,8 +35,9 @@ WIDENED = {g: WHOLE if g in (0, 6, 7) else HALVES if g in (1, 2) else BY_SLICE f
 QUANTIZED = {g: HALVES if g == 0 else WIDENED[g] for g in range(G)}
 LAG = 2
 BANKS = ("acc", "work")
-DEPTH = {"acc": 4, "work": 4, "wk_raw": 4, "wk_grouped": 2, "wk_codes": 2, "wk_scales": 2, "wv_bytes": 7, "planes_wide": 2, "planes": 4,
-         "wv_grouped_wide": 2, "wv_grouped": 3, "relu": 2, "k_grouped": 3, "result": 6}
+DEPTH = {"acc": 4, "work": 4, "wk_raw": 5, "grouped_wide": 3, "wk_codes": 3, "wk_scales": 3, "wv_bytes": 7, "planes_wide": 2, "planes": 4,
+         "wv_grouped": 3, "relu": 2, "k_grouped": 3, "result": 5}
+FIRST = 0
 
 
 def tile_block_pc_kernel(tc, h_attn, norm2_w, ffn_wk, ffn_wv_bytes, ffn_wv_scale, out):
@@ -90,7 +91,7 @@ def tile_block_pc_kernel(tc, h_attn, norm2_w, ffn_wk, ffn_wv_bytes, ffn_wv_scale
 
         def grouped_key(g, c):
             c0, w = covering(QUANTIZED, g, c)
-            return ("wv_grouped_wide" if w > HALF else "wv_grouped", g, c0, w)
+            return ("grouped_wide" if w > HALF else "wv_grouped", g, c0, w)
 
         def acc_key(sl, i):
             return ("acc" if sl == 0 else "work", "sum", sl, i // (BANK // SLICES[sl][1]))
@@ -114,7 +115,7 @@ def tile_block_pc_kernel(tc, h_attn, norm2_w, ffn_wk, ffn_wv_bytes, ffn_wv_scale
             nc.sync.dma_start(out=h_sb[:, i, :], in_=h_v[i])
 
         def wk_grouped(g, q):
-            return buffer(("wk_grouped", g), [P, Q * K_PASS * PACK], BF16)[:, q * K_PASS * PACK:(q + 1) * K_PASS * PACK]
+            return buffer(("grouped_wide", g), [P, Q * K_PASS * PACK], BF16)[:, q * K_PASS * PACK:(q + 1) * K_PASS * PACK]
 
         def wk_on_tensor(g, q, b, first=0, last=2):
             bank = buffer(("work", "wk", g, q, b), [P, PACK, 64, PACK], BF16)
@@ -149,7 +150,7 @@ def tile_block_pc_kernel(tc, h_attn, norm2_w, ffn_wk, ffn_wv_bytes, ffn_wv_scale
             nc.vector.quantize_mx(
                 out=codes[:, q0 * K_PASS:q1 * K_PASS].bitcast(FP8X4),
                 scales=scales[:, q0 * K_PASS:q1 * K_PASS],
-                in_=buffer(("wk_grouped", g))[:, q0 * K_PASS * PACK:q1 * K_PASS * PACK],
+                in_=buffer(("grouped_wide", g))[:, q0 * K_PASS * PACK:q1 * K_PASS * PACK],
             )
 
         def planes(g, c0, w):
@@ -268,17 +269,25 @@ def tile_block_pc_kernel(tc, h_attn, norm2_w, ffn_wk, ffn_wv_bytes, ffn_wv_scale
                     stop=(passes[key] == G * share),
                 )
 
+        def result_key(sl, first):
+            return ("relu", "result") if sl == 1 else ("result", sl, first)
+
+        def result(sl, first, last):
+            if sl == 1:
+                return buffer(result_key(sl, first), [P, NT, SLICES[sl][1]], F32)[:, first:last, :]
+            return buffer(result_key(sl, first), [P, last - first, SLICES[sl][1]], F32)[:]
+
         def finish(sl, first, last):
             c0, w = SLICES[sl]
             share = BANK // w
             nc.vector.tensor_tensor(
-                out=buffer(("result", sl, first), [P, last - first, w], F32)[:],
+                out=result(sl, first, last),
                 in0=buffer(acc_key(sl, first))[:, first % share:first % share + last - first, :],
                 in1=h_sb[:, first:last, c0:c0 + w], op=ALU.add)
 
         def store(sl, first, last):
             c0, w = SLICES[sl]
-            nc.sync.dma_start(out=out_v[:, first:last, c0:c0 + w], in_=buffer(("result", sl, first))[:])
+            nc.sync.dma_start(out=out_v[:, first:last, c0:c0 + w], in_=result(sl, first, last))
 
         def spread_gain():
             bank = buffer(("acc", "gain"), [P, D], BF16)
@@ -353,12 +362,12 @@ def tile_block_pc_kernel(tc, h_attn, norm2_w, ffn_wk, ffn_wv_bytes, ffn_wv_scale
             load_gain: lambda: ([], [("gain_row",)], []),
             load_h: lambda i: ([], [("h", i)], []),
             wk_on_tensor: lambda g, q, b, first=0, last=2: ([("raw", g, q, b)], [("wk_bank", g, q, b, part) for part in range(first, last)], [("wk_raw", g, q), ("work", "wk", g, q, b)]),
-            wk_out: lambda g, q, b: ([("wk_bank", g, q, b, 0), ("wk_bank", g, q, b, 1)], [("wk", g, q, b)], [("wk_grouped", g), ("work", "wk", g, q, b)]),
+            wk_out: lambda g, q, b: ([("wk_bank", g, q, b, 0), ("wk_bank", g, q, b, 1)], [("wk", g, q, b)], [("grouped_wide", g), ("work", "wk", g, q, b)]),
             wk_on_vector: lambda g, q: (
-                [("raw", g, q, 0), ("raw", g, q, 1)], [("wk", g, q, 0), ("wk", g, q, 1)], [("wk_raw", g, q), ("wk_grouped", g)]),
+                [("raw", g, q, 0), ("raw", g, q, 1)], [("wk", g, q, 0), ("wk", g, q, 1)], [("wk_raw", g, q), ("grouped_wide", g)]),
             quantize_wk: lambda g, q0, q1: (
                 [("wk", g, q, b) for q in range(q0, q1) for b in range(2)], [("wk_mx", g, q) for q in range(q0, q1)],
-                [("wk_grouped", g), ("wk_codes", g), ("wk_scales", g)]),
+                [("grouped_wide", g), ("wk_codes", g), ("wk_scales", g)]),
             widen_on_vector: widening,
             widen_on_scalar: widening,
             wv_on_vector: interleaving,
@@ -381,8 +390,8 @@ def tile_block_pc_kernel(tc, h_attn, norm2_w, ffn_wk, ffn_wv_bytes, ffn_wv_scale
                 [("part",) + acc_key(sl, i) + (g, i) for i in range(first, last)], [acc_key(sl, i) for i in range(first, last)]),
             finish: lambda sl, first, last: (
                 [("part",) + acc_key(sl, i) + (g, i) for g in range(G) for i in range(NT) if acc_key(sl, i) == acc_key(sl, first)],
-                [("out", sl, first)], [acc_key(sl, first), ("result", sl, first)]),
-            store: lambda sl, first, last: ([("out", sl, first)], [], [("result", sl, first)]),
+                [("out", sl, first)], [acc_key(sl, first), result_key(sl, first)]),
+            store: lambda sl, first, last: ([("out", sl, first)], [], [result_key(sl, first)]),
             spread_gain: lambda: ([("gain_row",)], [("gain",)], [("acc", "gain")]),
             sum_squares: lambda i: ([("h", i)], [("sum", i)], [("k_grouped", "squares", i)]),
             root: lambda i: ([("sum", i)], [("rstd", i)], []),
@@ -414,8 +423,8 @@ def tile_block_pc_kernel(tc, h_attn, norm2_w, ffn_wk, ffn_wv_bytes, ffn_wv_scale
         R, L = SLICES[2], SLICES[1]
 
         U = (HALF, HALF)
-        sync = [(load_scale, 0, 1), (load_wv, 0, 0, 1), (load_wv, 0, 1, 2), (load_wv, 0, 2, 3), (load_h, 0), (load_wv, 0, 3, 4), (load_gain,),
-                (load_h, 1), (load_wk, 0, 1, 0, 2), (load_h, 2), (load_wk, 0, 0, 0, 2), (load_h, 3), (load_wk, 1, 0, 0, 2), (load_scale, 1, G), (load_wv, 1, 0, 4),
+        sync = [(load_scale, 0, 2), (load_wv, 0, 0, 1), (load_wv, 0, 1, 2), (load_wv, 0, 2, 3), (load_h, 0), (load_gain,), (load_wv, 0, 3, 4),
+                (load_h, 1), (load_wv, 1, 0, 2), (load_wk, 0, 1, 0, 2), (load_h, 2), (load_wk, 0, 0, 0, 2), (load_h, 3), (load_wk, 1, 0, 0, 2), (load_wv, 1, 2, 4), (load_scale, 2, G),
                 (load_wk, 1, 1, 0, 2)]
         for g in range(2, G):
             sync += [(load_wk, g, 0, 0, 2), (load_wv, g, 0, PACK), (load_wk, g, 1, 0, 2)]
@@ -423,48 +432,45 @@ def tile_block_pc_kernel(tc, h_attn, norm2_w, ffn_wk, ffn_wv_bytes, ffn_wv_scale
         gpsimd = []
         tensor = [(spread_gain,), (wv_on_tensor, 0, HALF), (wv_on_tensor, 0, 768), (turn_hn, 0), (wk_on_tensor, 0, 1, 0), (turn_hn, 1), (wk_on_tensor, 0, 1, 1),
                   (turn_hn, 2), (wk_on_tensor, 1, 0, 0)]
-        scalar = [(widen_on_scalar, 0, QUARTER, 3 * QUARTER, 1, 2), (sum_squares, 0), (root, 0), (sum_squares, 1), (wv_out, 0, HALF), (root, 1), (sum_squares, 2), (wv_out, 0, 768), (root, 2),
-                  (hn_out, 0), (wk_out, 0, 1, 0), (hn_out, 1), (sum_squares, 3), (wk_out, 0, 1, 1), (root, 3), (hn_out, 2), (wk_out, 1, 0, 0), (widen_on_scalar, 1, 0, HALF, 0, 1)]
-        vector = [(widen_on_vector, 0, 0, D, 0, 1), (widen_on_vector, 0, 0, QUARTER, 1, 2), (widen_on_vector, 0, 0, D, 2, 3), (widen_on_vector, 0, 0, HALF, 3, 4), (widen_on_vector, 0, HALF, HALF, 3, 4),
+        scalar = [(widen_on_scalar, 0, QUARTER, 3 * QUARTER, 1, 2), (sum_squares, 0), (widen_on_scalar, 0, 768, QUARTER, 3, 4), (root, 0), (sum_squares, 1), (widen_on_scalar, 1, 0, QUARTER, 0, 1), (root, 1), (wv_out, 0, HALF), (sum_squares, 2), (wv_out, 0, 768), (root, 2),
+                  (hn_out, 0), (wk_out, 0, 1, 0), (hn_out, 1), (sum_squares, 3), (wk_out, 0, 1, 1), (root, 3), (hn_out, 2), (widen_on_scalar, 1, QUARTER, QUARTER, 0, 1), (wk_out, 1, 0, 0), (widen_on_scalar, 1, 0, HALF, 1, 2)]
+        vector = [(widen_on_vector, 0, 0, D, 0, 1), (widen_on_vector, 0, 0, QUARTER, 1, 2), (widen_on_vector, 0, 0, D, 2, 3), (widen_on_vector, 0, 0, HALF, 3, 4), (widen_on_vector, 0, HALF, QUARTER, 3, 4),
             (wv_on_vector, 0, 0, HALF), (normalize, 0), (quantize_wv, 0, 0, HALF), (normalize, 1), (wk_on_vector, 0, 0), (normalize, 2), (quantize_hn, 0), (quantize_wk, 0, 0, 1), (quantize_hn, 1),
-            (widen_on_vector, 1, 0, HALF, 1, 2), (quantize_wk, 0, 1, 2), (normalize, 3), (quantize_hn, 2), (widen_on_vector, 1, 0, HALF, 2, 4), (quantize_wv, 0, *U), (widen_on_vector, 2, 0, HALF, 0, 1), (quantize_hn, 3), (wk_on_vector, 1, 1),
-            (widen_on_vector, 2, 0, HALF, 1, 2), (quantize_wk, 1, 0, 2)]
-        tensor += [(first_product, 0, 0), (first_product, 0, 1), (turn_hn, 3), (wk_on_tensor, 1, 0, 1), (wk_on_tensor, 2, 0, 0, 0, 1), (first_product, 0, 2), (first_product, 0, 3),
-                   (wk_on_tensor, 2, 0, 0, 1, 2), (wv_on_tensor, 1, 0)]
-        scalar += [(rectify, 0, 0), (rectify, 0, 1), (hn_out, 3), (square, 0, 0), (wk_out, 1, 0, 1), (rectify, 0, 2), (rectify, 0, 3), (wk_out, 2, 0, 0), (square, 0, 1), (wv_out, 1, 0)]
-        tensor += [(first_product, 1, 0), (first_product, 1, 1), (wv_on_tensor, 1, QUARTER), (wk_on_tensor, 2, 0, 1), (first_product, 1, 2), (first_product, 1, 3), (wk_on_tensor, 3, 0, 0)] + slice0[:NT - 2]
-        scalar += [(rectify, 1, 0), (rectify, 1, 1), (wv_out, 1, QUARTER), (square, 1, 0), (wk_out, 2, 0, 1), (rectify, 1, 2), (rectify, 1, 3), (wk_out, 3, 0, 0), (square, 1, 1)]
+            (widen_on_vector, 1, 0, HALF, 2, 4), (quantize_wk, 0, 1, 2), (normalize, 3), (quantize_hn, 2), (wk_on_vector, 1, 1), (quantize_wv, 0, *U), (quantize_hn, 3),
+            (wk_on_vector, 2, 1), (widen_on_vector, 2, 0, HALF, 1, 2), (quantize_wk, 1, 0, 2), (widen_on_vector, 2, 0, HALF, 2, 4)]
+        tensor += [(first_product, 0, 0), (first_product, 0, 1), (turn_hn, 3), (wk_on_tensor, 1, 0, 1), (wk_on_tensor, 2, 0, 0), (first_product, 0, 2), (first_product, 0, 3), (wk_on_tensor, 2, 0, 1)]
+        scalar += [(rectify, 0, 0), (rectify, 0, 1), (hn_out, 3), (square, 0, 0), (wk_out, 1, 0, 1), (wk_out, 2, 0, 0), (rectify, 0, 2), (rectify, 0, 3), (widen_on_scalar, 2, 0, HALF, 0, 1), (square, 0, 1), (wk_out, 2, 0, 1)]
+        tensor += [(first_product, 1, 0), (first_product, 1, 1), (wv_on_tensor, 1, 0), (wk_on_tensor, 3, 0, 0), (first_product, 1, 2), (first_product, 1, 3), (wv_on_tensor, 1, QUARTER), (wk_on_tensor, 3, 0, 1)] + slice0[:FIRST]
+        scalar += [(rectify, 1, 0), (rectify, 1, 1), (wv_out, 1, 0), (square, 1, 0), (wk_out, 3, 0, 0), (rectify, 1, 2), (rectify, 1, 3), (wv_out, 1, QUARTER), (square, 1, 1), (wk_out, 3, 0, 1)]
 
         def paced(g):
-            return NT * g - 2 - g // LAG
+            return NT * (g - 1) + FIRST - (g - 1) // LAG
 
         for g in range(2, G):
-            slot = [wk_half(g + 1, 1) if g + 1 < G else wv_quarter(g, 0), wk_half(g + 2, 0) if g + 2 < G else wv_quarter(g, QUARTER)]
-            if g == 6:
-                slot[1] = both(wv_quarter(g, 0), slot[1])
+            slot = [wk_half(g + 2, b) if g + 2 < G else wv_quarter(g, QUARTER * b) for b in range(2)]
             for a in range(2):
                 tensor += [(first_product, g, 2 * a), (first_product, g, 2 * a + 1)] + slot[a][0]
                 scalar += [(rectify, g, 2 * a), (rectify, g, 2 * a + 1)] + slot[a][1] + [(square, g, a)]
             tensor += slice0[paced(g - 1):paced(g)]
-        vector += [(wk_on_vector, 2, 1), (widen_on_vector, 2, 0, HALF, 2, 4), (quantize_k, 0, 0, 2)] + lower(2)[1] + lower(3)[0] + lower(1)[2] + [(quantize_wk, 2, 0, 2)] + lower(2)[2]
-        for g in range(2, 5):
-            vector += [(wk_on_vector, g + 1, 1), (quantize_k, g - 1, 0, 2)] + lower(g + 1)[1] + [(quantize_wk, g + 1, 0, 2)] + lower(g + 1)[2]
-            vector += lower(g + 2)[0] if g < 4 else [(widen_on_vector, 6, 0, D, 0, 2)]
-        vector += [(wk_on_vector, 6, 1), (quantize_k, 4, 0, 2), (widen_on_vector, 6, 0, D, 2, 4), (quantize_wk, 6, 0, 2), (wv_on_vector, 6, *U)]
-        vector += [(wk_on_vector, 7, 1), (quantize_k, 5, 0, 2), (widen_on_vector, 7, 0, D, 0, 2), (quantize_wk, 7, 0, 2), (widen_on_vector, 7, 0, D, 2, 4)]
-        vector += [(widen_on_vector, 1, *U, 0, 4), (quantize_wv, 6, 0, D), (quantize_k, 6, 0, 2), (wv_on_vector, 7, *U), (widen_on_vector, 3, *R, 0, 4), (wv_on_vector, 1, *U), (wv_on_vector, 3, *R)]
-        vector += [(quantize_wv, 7, 0, D), (quantize_wv, 1, *U), (quantize_k, 7, 0, 2), (quantize_wv, 3, *R)]
-        for g, run in ((4, R), (5, R), (3, L), (2, U), (5, L), (4, L)):
+        vector += [(wk_on_vector, 3, 1)] + lower(2)[1] + [(quantize_k, 0, 0, 2), (quantize_wk, 2, 0, 2)] + lower(2)[2] + lower(3)[0] + [(widen_on_vector, 4, 0, HALF, 0, 1)] + lower(3)[1] + lower(1)[2]
+        vector += [(quantize_k, 1, 0, 2), (quantize_wk, 3, 0, 2)]
+        vector += [(wk_on_vector, 4, 1), (widen_on_vector, 4, 0, HALF, 1, 4)] + lower(3)[2] + lower(4)[1] + [(quantize_wk, 4, 0, 2), (quantize_k, 2, 0, 2)]
+        vector += [(wk_on_vector, 5, 1)] + lower(5)[0] + lower(4)[2] + lower(5)[1] + [(quantize_wk, 5, 0, 2), (quantize_k, 3, 0, 2)]
+        vector += [(wk_on_vector, 6, 1), (widen_on_vector, 6, 0, D, 0, 2)] + lower(5)[2] + [(widen_on_vector, 6, 0, D, 2, 4), (quantize_wk, 6, 0, 2), (quantize_k, 4, 0, 2)]
+        vector += [(wk_on_vector, 7, 1), (wv_on_vector, 6, *U), (widen_on_vector, 7, 0, D, 0, 4), (quantize_wk, 7, 0, 2), (quantize_k, 5, 0, 2)]
+        vector += [(widen_on_vector, 1, *U, 0, 4), (wv_on_vector, 7, *U), (wv_on_vector, 1, *U), (widen_on_vector, 3, *R, 0, 4), (quantize_wv, 6, 0, D), (quantize_k, 6, 0, 2), (wv_on_vector, 3, *R), (quantize_wv, 1, *U)]
+        vector += [(widen_on_vector, 4, *R, 0, 4), (quantize_wv, 7, 0, D), (wv_on_vector, 4, *R), (quantize_k, 7, 0, 2), (quantize_wv, 3, *R), (quantize_wv, 4, *R)]
+        for g, run in ((5, R), (3, L), (2, U), (5, L), (4, L)):
             scalar += by_plane(widen_on_scalar, g, *run)
         scalar += [(wv_on_scalar, 5, *L)]
-        tensor += slice0[paced(G - 1):-NT] + products(2, (0, 6, 1)) + slice0[-NT:] + products(2, (7, 3, 4)) + products(1, (0, 6))
-        tensor += products(2, (5,)) + products(1, (7, 1, 3)) + products(2, (2,)) + products(1, (2,))
+        tensor += slice0[paced(G - 1):-NT] + products(2, (0, 6, 1)) + slice0[-NT:] + products(2, (7, 3)) + products(1, (0, 6))
+        tensor += products(2, (4, 5)) + products(1, (7, 1, 3)) + products(2, (2,)) + products(1, (2,))
         tensor += [(second_product, 1, g, i, i + 2) for i in (0, 2) for g in (4, 5)]
         vector += [
-            (wv_on_vector, 4, *R), (finish, 0, 0, 1), (quantize_wv, 4, *R), (wv_on_vector, 5, *R), (finish, 0, 1, 2), (quantize_wv, 5, *R), (wv_on_vector, 3, *L), (finish, 0, 2, 3),
-            (quantize_wv, 3, *L), (wv_on_vector, 2, *U), (finish, 0, 3, 4), (quantize_wv, 2, *U),
-            (wv_on_vector, 4, *L), (finish, 2, 0, 2), (quantize_wv, 4, *L), (quantize_wv, 5, *L),
-            (finish, 2, 2, 4), ] + [(finish, 1, i, i + 1) for i in range(NT)]
+            (wv_on_vector, 5, *R), (finish, 0, 0, 1), (wv_on_vector, 3, *L), (quantize_wv, 5, *R), (finish, 0, 1, 2),
+            (quantize_wv, 3, *L), (wv_on_vector, 2, *U), (finish, 0, 2, 3), (quantize_wv, 2, *U),
+            (wv_on_vector, 4, *L), (finish, 0, 3, 4), (quantize_wv, 4, *L), (quantize_wv, 5, *L),
+            (finish, 2, 0, 2), (finish, 2, 2, 4)] + [(finish, 1, i, i + 1) for i in range(NT)]
 
 
         queues = [sync, tensor, scalar, vector, gpsimd]
@@ -475,6 +481,13 @@ def tile_block_pc_kernel(tc, h_attn, norm2_w, ffn_wk, ffn_wv_bytes, ffn_wv_scale
                 users.setdefault(key, []).append(job)
         at = [0] * len(queues)
         written, made = set(), set()
+
+        def room(tag, wanted):
+            busy = [any(user not in written for user in users[key]) for key in taken.get(tag, [])]
+            if tag in BANKS:
+                return not any(busy[:max(0, len(busy) + wanted - DEPTH[tag])])
+            return sum(busy) + wanted <= DEPTH[tag]
+
         while len(written) < len(jobs):
             before = len(written)
             for e in range(len(queues)):
@@ -486,8 +499,7 @@ def tile_block_pc_kernel(tc, h_attn, norm2_w, ffn_wk, ffn_wv_bytes, ffn_wv_scale
                 for key in keys:
                     if key not in held and key not in fresh.setdefault(key[0], []):
                         fresh[key[0]].append(key)
-                old = [key for tag in fresh for key in taken.get(tag, [])[:max(0, len(taken.get(tag, [])) + len(fresh[tag]) - DEPTH[tag])]]
-                if all(name in made for name in reads) and all(user in written for key in old for user in users[key]):
+                if all(name in made for name in reads) and all(room(tag, len(fresh[tag])) for tag in fresh):
                     job[0](*job[1:])
                     written.add(job)
                     for name in makes:

@@ -270,10 +270,10 @@ def tile_block_pc_kernel(tc, h_attn, norm2_w, ffn_wk, ffn_wv_bytes, ffn_wv_scale
                 )
 
         def result_key(sl, first):
-            return ("relu", "result") if sl == 1 else ("result", sl, first)
+            return ("relu", "result", sl) if sl > 0 else ("result", sl, first)
 
         def result(sl, first, last):
-            if sl == 1:
+            if sl > 0:
                 return buffer(result_key(sl, first), [P, NT, SLICES[sl][1]], F32)[:, first:last, :]
             return buffer(result_key(sl, first), [P, last - first, SLICES[sl][1]], F32)[:]
 
@@ -428,7 +428,7 @@ def tile_block_pc_kernel(tc, h_attn, norm2_w, ffn_wk, ffn_wv_bytes, ffn_wv_scale
                 (load_wk, 1, 1, 0, 2)]
         for g in range(2, G):
             sync += [(load_wk, g, 0, 0, 2), (load_wv, g, 0, PACK), (load_wk, g, 1, 0, 2)]
-        sync += [(store, 0, i, i + 1) for i in range(NT)] + [(store, 2, 0, 2), (store, 2, 2, 4)] + [(store, 1, i, i + 1) for i in range(NT)]
+        sync += [(store, 0, i, i + 1) for i in range(NT)] + [(store, sl, i, i + 1) for sl in (2, 1) for i in range(NT)]
         gpsimd = []
         tensor = [(spread_gain,), (wv_on_tensor, 0, HALF), (wv_on_tensor, 0, 768), (turn_hn, 0), (wk_on_tensor, 0, 1, 0), (turn_hn, 1), (wk_on_tensor, 0, 1, 1),
                   (turn_hn, 2), (wk_on_tensor, 1, 0, 0)]
@@ -437,7 +437,7 @@ def tile_block_pc_kernel(tc, h_attn, norm2_w, ffn_wk, ffn_wv_bytes, ffn_wv_scale
         vector = [(widen_on_vector, 0, 0, D, 0, 1), (widen_on_vector, 0, 0, QUARTER, 1, 2), (widen_on_vector, 0, 0, D, 2, 3), (widen_on_vector, 0, 0, HALF, 3, 4), (widen_on_vector, 0, HALF, QUARTER, 3, 4),
             (wv_on_vector, 0, 0, HALF), (normalize, 0), (quantize_wv, 0, 0, HALF), (normalize, 1), (wk_on_vector, 0, 0), (normalize, 2), (quantize_hn, 0), (quantize_wk, 0, 0, 1), (quantize_hn, 1),
             (widen_on_vector, 1, 0, HALF, 2, 4), (quantize_wk, 0, 1, 2), (normalize, 3), (quantize_hn, 2), (wk_on_vector, 1, 1), (quantize_wv, 0, *U), (quantize_hn, 3),
-            (wk_on_vector, 2, 1), (widen_on_vector, 2, 0, HALF, 1, 2), (quantize_wk, 1, 0, 2), (widen_on_vector, 2, 0, HALF, 2, 4)]
+            (widen_on_vector, 2, 0, HALF, 1, 4), (quantize_wk, 1, 0, 2)]
         tensor += [(first_product, 0, 0), (first_product, 0, 1), (turn_hn, 3), (wk_on_tensor, 1, 0, 1), (wk_on_tensor, 2, 0, 0), (first_product, 0, 2), (first_product, 0, 3), (wk_on_tensor, 2, 0, 1)]
         scalar += [(rectify, 0, 0), (rectify, 0, 1), (hn_out, 3), (square, 0, 0), (wk_out, 1, 0, 1), (wk_out, 2, 0, 0), (rectify, 0, 2), (rectify, 0, 3), (widen_on_scalar, 2, 0, HALF, 0, 1), (square, 0, 1), (wk_out, 2, 0, 1)]
         tensor += [(first_product, 1, 0), (first_product, 1, 1), (wv_on_tensor, 1, 0), (wk_on_tensor, 3, 0, 0), (first_product, 1, 2), (first_product, 1, 3), (wv_on_tensor, 1, QUARTER), (wk_on_tensor, 3, 0, 1)] + slice0[:FIRST]
@@ -452,7 +452,7 @@ def tile_block_pc_kernel(tc, h_attn, norm2_w, ffn_wk, ffn_wv_bytes, ffn_wv_scale
                 tensor += [(first_product, g, 2 * a), (first_product, g, 2 * a + 1)] + slot[a][0]
                 scalar += [(rectify, g, 2 * a), (rectify, g, 2 * a + 1)] + slot[a][1] + [(square, g, a)]
             tensor += slice0[paced(g - 1):paced(g)]
-        vector += [(wk_on_vector, 3, 1)] + lower(2)[1] + [(quantize_k, 0, 0, 2), (quantize_wk, 2, 0, 2)] + lower(2)[2] + lower(3)[0] + [(widen_on_vector, 4, 0, HALF, 0, 1)] + lower(3)[1] + lower(1)[2]
+        vector += [(wk_on_vector, 2, 1)] + lower(2)[1] + [(quantize_k, 0, 0, 2), (quantize_wk, 2, 0, 2)] + lower(2)[2] + [(wk_on_vector, 3, 1)] + lower(3)[0] + [(widen_on_vector, 4, 0, HALF, 0, 1)] + lower(3)[1] + lower(1)[2]
         vector += [(quantize_k, 1, 0, 2), (quantize_wk, 3, 0, 2)]
         vector += [(wk_on_vector, 4, 1), (widen_on_vector, 4, 0, HALF, 1, 4)] + lower(3)[2] + lower(4)[1] + [(quantize_wk, 4, 0, 2), (quantize_k, 2, 0, 2)]
         vector += [(wk_on_vector, 5, 1)] + lower(5)[0] + lower(4)[2] + lower(5)[1] + [(quantize_wk, 5, 0, 2), (quantize_k, 3, 0, 2)]
@@ -470,7 +470,7 @@ def tile_block_pc_kernel(tc, h_attn, norm2_w, ffn_wk, ffn_wv_bytes, ffn_wv_scale
             (wv_on_vector, 5, *R), (finish, 0, 0, 1), (wv_on_vector, 3, *L), (quantize_wv, 5, *R), (finish, 0, 1, 2),
             (quantize_wv, 3, *L), (wv_on_vector, 2, *U), (finish, 0, 2, 3), (quantize_wv, 2, *U),
             (wv_on_vector, 4, *L), (finish, 0, 3, 4), (quantize_wv, 4, *L), (quantize_wv, 5, *L),
-            (finish, 2, 0, 2), (finish, 2, 2, 4)] + [(finish, 1, i, i + 1) for i in range(NT)]
+        ] + [(finish, sl, i, i + 1) for sl in (2, 1) for i in range(NT)]
 
 
         queues = [sync, tensor, scalar, vector, gpsimd]

@@ -32,11 +32,11 @@ WHOLE = [(0, D)]
 HALVES = [(0, HALF), (HALF, HALF)]
 BY_SLICE = list(SLICES)
 WIDENED = {g: WHOLE if g in (0, 6, 7) else HALVES if g in (1, 2) else BY_SLICE for g in range(G)}
-QUANTIZED = {g: HALVES if g == 0 else WIDENED[g] for g in range(G)}
+QUANTIZED = {g: HALVES if g in (0, 6, 7) else WIDENED[g] for g in range(G)}
 LAG = 2
 BANKS = ("acc", "work")
-DEPTH = {"acc": 4, "work": 4, "wk_raw": 5, "grouped_wide": 3, "wk_codes": 3, "wk_scales": 3, "wv_bytes": 7, "planes_wide": 2, "planes": 4,
-         "wv_grouped": 3, "relu": 2, "k_grouped": 3, "result": 5}
+DEPTH = {"acc": 4, "work": 4, "wk_raw": 5, "grouped_wide": 2, "wk_codes": 3, "wk_scales": 3, "wv_bytes": 7, "planes_wide": 2, "planes": 4,
+         "wv_grouped": 5, "relu": 2, "k_grouped": 3, "result": 5}
 FIRST = 0
 
 
@@ -136,11 +136,10 @@ def tile_block_pc_kernel(tc, h_attn, norm2_w, ffn_wk, ffn_wv_bytes, ffn_wv_scale
             )
 
         def wk_on_vector(g, q):
-            for u in range(2):
-                nc.vector.tensor_copy(
-                    out=wk_grouped(g, q).rearrange("p (u e m j) -> p u m j e", u=2, e=2, j=PACK)[:, u, :, :, :],
-                    in_=buffer(("wk_raw", g, q))[:].rearrange("p j (m u e) -> p u m j e", u=2, e=2)[:, u, :, :, :],
-                )
+            nc.vector.tensor_copy(
+                out=wk_grouped(g, q).rearrange("p (t m i j) -> p m t j i", t=PACK, i=RUN, j=PACK),
+                in_=buffer(("wk_raw", g, q))[:].rearrange("p j (m i t) -> p m t j i", i=RUN, t=PACK),
+            )
 
         def wk_operand(g):
             return (buffer(("wk_codes", g), [P, Q * K_PASS], U32), buffer(("wk_scales", g), [P, Q * K_PASS], U8))
@@ -437,7 +436,7 @@ def tile_block_pc_kernel(tc, h_attn, norm2_w, ffn_wk, ffn_wv_bytes, ffn_wv_scale
         vector = [(widen_on_vector, 0, 0, D, 0, 1), (widen_on_vector, 0, 0, QUARTER, 1, 2), (widen_on_vector, 0, 0, D, 2, 3), (widen_on_vector, 0, 0, HALF, 3, 4), (widen_on_vector, 0, HALF, QUARTER, 3, 4),
             (wv_on_vector, 0, 0, HALF), (normalize, 0), (quantize_wv, 0, 0, HALF), (normalize, 1), (wk_on_vector, 0, 0), (normalize, 2), (quantize_hn, 0), (quantize_wk, 0, 0, 1), (quantize_hn, 1),
             (widen_on_vector, 1, 0, HALF, 2, 4), (quantize_wk, 0, 1, 2), (normalize, 3), (quantize_hn, 2), (wk_on_vector, 1, 1), (quantize_wv, 0, *U), (quantize_hn, 3),
-            (widen_on_vector, 2, 0, HALF, 1, 4), (quantize_wk, 1, 0, 2)]
+            (widen_on_vector, 2, 0, HALF, 1, 4), (quantize_wk, 1, 1, 2), (quantize_wk, 1, 0, 1)]
         tensor += [(first_product, 0, 0), (first_product, 0, 1), (turn_hn, 3), (wk_on_tensor, 1, 0, 1), (wk_on_tensor, 2, 0, 0), (first_product, 0, 2), (first_product, 0, 3), (wk_on_tensor, 2, 0, 1)]
         scalar += [(rectify, 0, 0), (rectify, 0, 1), (hn_out, 3), (square, 0, 0), (wk_out, 1, 0, 1), (wk_out, 2, 0, 0), (rectify, 0, 2), (rectify, 0, 3), (widen_on_scalar, 2, 0, HALF, 0, 1), (square, 0, 1), (wk_out, 2, 0, 1)]
         tensor += [(first_product, 1, 0), (first_product, 1, 1), (wv_on_tensor, 1, 0), (wk_on_tensor, 3, 0, 0), (first_product, 1, 2), (first_product, 1, 3), (wv_on_tensor, 1, QUARTER), (wk_on_tensor, 3, 0, 1)] + slice0[:FIRST]
@@ -452,25 +451,30 @@ def tile_block_pc_kernel(tc, h_attn, norm2_w, ffn_wk, ffn_wv_bytes, ffn_wv_scale
                 tensor += [(first_product, g, 2 * a), (first_product, g, 2 * a + 1)] + slot[a][0]
                 scalar += [(rectify, g, 2 * a), (rectify, g, 2 * a + 1)] + slot[a][1] + [(square, g, a)]
             tensor += slice0[paced(g - 1):paced(g)]
-        vector += [(wk_on_vector, 2, 1)] + lower(2)[1] + [(quantize_k, 0, 0, 2), (quantize_wk, 2, 0, 2)] + lower(2)[2] + [(wk_on_vector, 3, 1)] + lower(3)[0] + [(widen_on_vector, 4, 0, HALF, 0, 1)] + lower(3)[1] + lower(1)[2]
-        vector += [(quantize_k, 1, 0, 2), (quantize_wk, 3, 0, 2)]
-        vector += [(wk_on_vector, 4, 1), (widen_on_vector, 4, 0, HALF, 1, 4)] + lower(3)[2] + lower(4)[1] + [(quantize_wk, 4, 0, 2), (quantize_k, 2, 0, 2)]
-        vector += [(wk_on_vector, 5, 1)] + lower(5)[0] + lower(4)[2] + lower(5)[1] + [(quantize_wk, 5, 0, 2), (quantize_k, 3, 0, 2)]
-        vector += [(wk_on_vector, 6, 1), (widen_on_vector, 6, 0, D, 0, 2)] + lower(5)[2] + [(widen_on_vector, 6, 0, D, 2, 4), (quantize_wk, 6, 0, 2), (quantize_k, 4, 0, 2)]
-        vector += [(wk_on_vector, 7, 1), (wv_on_vector, 6, *U), (widen_on_vector, 7, 0, D, 0, 4), (quantize_wk, 7, 0, 2), (quantize_k, 5, 0, 2)]
-        vector += [(widen_on_vector, 1, *U, 0, 4), (wv_on_vector, 7, *U), (wv_on_vector, 1, *U), (widen_on_vector, 3, *R, 0, 4), (quantize_wv, 6, 0, D), (quantize_k, 6, 0, 2), (wv_on_vector, 3, *R), (quantize_wv, 1, *U)]
-        vector += [(widen_on_vector, 4, *R, 0, 4), (quantize_wv, 7, 0, D), (wv_on_vector, 4, *R), (quantize_k, 7, 0, 2), (quantize_wv, 3, *R), (quantize_wv, 4, *R)]
+
+        def wk_step(g):
+            return [(wk_on_vector, g, 1)], [(quantize_wk, g, 1, 2)], [(quantize_wk, g, 0, 1)]
+
+        vector += wk_step(2)[0] + [(widen_on_vector, 3, 0, HALF, 0, 1)] + wk_step(2)[1] + lower(2)[1] + [(quantize_k, 0, 0, 2)] + wk_step(2)[2] + lower(2)[2]
+        vector += wk_step(3)[0] + [(widen_on_vector, 3, 0, HALF, 1, 4)] + wk_step(3)[1] + lower(3)[1] + lower(1)[2] + [(quantize_k, 1, 0, 2)] + wk_step(3)[2]
+        for g in (4, 5):
+            vector += wk_step(g)[0] + lower(g)[0] + lower(g - 1)[2] + lower(g)[1] + wk_step(g)[1] + wk_step(g)[2] + [(quantize_k, g - 2, 0, 2)]
+        vector += wk_step(6)[0] + [(widen_on_vector, 6, 0, D, 0, 2)] + lower(5)[2] + [(widen_on_vector, 6, 0, D, 2, 4)] + wk_step(6)[1] + wk_step(6)[2] + [(quantize_k, 4, 0, 2)]
+        vector += wk_step(7)[0] + [(wv_on_vector, 6, *U), (widen_on_vector, 7, 0, D, 0, 4), (quantize_wv, 6, *U)] + wk_step(7)[1] + wk_step(7)[2] + [(quantize_k, 5, 0, 2)]
+        vector += [(widen_on_vector, 1, *U, 0, 4), (wv_on_vector, 7, *U), (wv_on_vector, 1, *U), (quantize_wv, 7, *U), (quantize_wv, 6, 0, HALF), (quantize_k, 6, 0, 2)]
+        vector += [(widen_on_vector, 3, *R, 0, 4), (quantize_wv, 1, *U), (wv_on_vector, 3, *R), (widen_on_vector, 4, *R, 2, 4), (quantize_wv, 7, 0, HALF), (quantize_k, 7, 0, 2), (quantize_wv, 3, *R)]
+        scalar += by_plane(widen_on_scalar, 4, *R, 0, 2)
         for g, run in ((5, R), (3, L), (2, U), (5, L), (4, L)):
             scalar += by_plane(widen_on_scalar, g, *run)
         scalar += [(wv_on_scalar, 5, *L)]
-        tensor += slice0[paced(G - 1):-NT] + products(2, (0, 6, 1)) + slice0[-NT:] + products(2, (7, 3)) + products(1, (0, 6))
+        tensor += slice0[paced(G - 1):-NT] + products(2, (0, 6)) + slice0[-NT:] + products(2, (7, 1, 3)) + products(1, (0, 6))
         tensor += products(2, (4, 5)) + products(1, (7, 1, 3)) + products(2, (2,)) + products(1, (2,))
         tensor += [(second_product, 1, g, i, i + 2) for i in (0, 2) for g in (4, 5)]
         vector += [
-            (wv_on_vector, 5, *R), (finish, 0, 0, 1), (wv_on_vector, 3, *L), (quantize_wv, 5, *R), (finish, 0, 1, 2),
+            (wv_on_vector, 4, *R), (finish, 0, 0, 1), (wv_on_vector, 5, *R), (quantize_wv, 4, *R), (wv_on_vector, 3, *L), (quantize_wv, 5, *R), (finish, 0, 1, 2),
             (quantize_wv, 3, *L), (wv_on_vector, 2, *U), (finish, 0, 2, 3), (quantize_wv, 2, *U),
-            (wv_on_vector, 4, *L), (finish, 0, 3, 4), (quantize_wv, 4, *L), (quantize_wv, 5, *L),
-        ] + [(finish, sl, i, i + 1) for sl in (2, 1) for i in range(NT)]
+            (wv_on_vector, 4, *L), (finish, 0, 3, 4), (quantize_wv, 4, *L), (finish, 2, 0, 1), (quantize_wv, 5, *L),
+        ] + [(finish, sl, i, i + 1) for sl in (2, 1) for i in range(NT)][1:]
 
 
         queues = [sync, tensor, scalar, vector, gpsimd]

@@ -32,7 +32,7 @@ WHOLE = [(0, D)]
 HALVES = [(0, HALF), (HALF, HALF)]
 BY_SLICE = list(SLICES)
 WIDENED = {g: WHOLE if g in (0, 6, 7) else HALVES if g in (1, 2) else BY_SLICE for g in range(G)}
-QUANTIZED = {g: HALVES if g in (0, 6, 7) else WIDENED[g] for g in range(G)}
+QUANTIZED = {g: [(0, QUARTER), (QUARTER, QUARTER), (HALF, HALF)] if g == 0 else HALVES if g in (6, 7) else WIDENED[g] for g in range(G)}
 LAG = 2
 BANKS = ("acc", "work")
 DEPTH = {"acc": 4, "work": 4, "wk_raw": 5, "grouped_wide": 2, "wk_codes": 3, "wk_scales": 3, "wv_bytes": 7, "planes_wide": 2, "planes": 4,
@@ -423,22 +423,23 @@ def tile_block_pc_kernel(tc, h_attn, norm2_w, ffn_wk, ffn_wv_bytes, ffn_wv_scale
 
         U = (HALF, HALF)
         sync = [(load_scale, 0, 2), (load_wv, 0, 0, 1), (load_wv, 0, 1, 2), (load_wv, 0, 2, 3), (load_h, 0), (load_gain,), (load_wv, 0, 3, 4),
-                (load_h, 1), (load_wv, 1, 0, 2), (load_wk, 0, 1, 0, 2), (load_h, 2), (load_wk, 0, 0, 0, 2), (load_h, 3), (load_wk, 1, 0, 0, 2), (load_wv, 1, 2, 4), (load_scale, 2, G),
-                (load_wk, 1, 1, 0, 2)]
+                (load_h, 1), (load_wk, 0, 1, 0, 1), (load_h, 2), (load_wk, 0, 1, 1, 2), (load_wv, 1, 0, 1), (load_h, 3), (load_wk, 0, 0, 0, 2), (load_wk, 1, 0, 0, 2), (load_wv, 1, 1, 4),
+                (load_wk, 1, 1, 0, 2), (load_scale, 2, G)]
         for g in range(2, G):
             sync += [(load_wk, g, 0, 0, 2), (load_wv, g, 0, PACK), (load_wk, g, 1, 0, 2)]
         sync += [(store, 0, i, i + 1) for i in range(NT)] + [(store, sl, i, i + 1) for sl in (2, 1) for i in range(NT)]
-        gpsimd = []
-        tensor = [(spread_gain,), (wv_on_tensor, 0, HALF), (wv_on_tensor, 0, 768), (turn_hn, 0), (wk_on_tensor, 0, 1, 0), (turn_hn, 1), (wk_on_tensor, 0, 1, 1),
-                  (turn_hn, 2), (wk_on_tensor, 1, 0, 0)]
-        scalar = [(widen_on_scalar, 0, QUARTER, 3 * QUARTER, 1, 2), (sum_squares, 0), (widen_on_scalar, 0, 768, QUARTER, 3, 4), (root, 0), (sum_squares, 1), (widen_on_scalar, 1, 0, QUARTER, 0, 1), (root, 1), (wv_out, 0, HALF), (sum_squares, 2), (wv_out, 0, 768), (root, 2),
-                  (hn_out, 0), (wk_out, 0, 1, 0), (hn_out, 1), (sum_squares, 3), (wk_out, 0, 1, 1), (root, 3), (hn_out, 2), (widen_on_scalar, 1, QUARTER, QUARTER, 0, 1), (wk_out, 1, 0, 0), (widen_on_scalar, 1, 0, HALF, 1, 2)]
-        vector = [(widen_on_vector, 0, 0, D, 0, 1), (widen_on_vector, 0, 0, QUARTER, 1, 2), (widen_on_vector, 0, 0, D, 2, 3), (widen_on_vector, 0, 0, HALF, 3, 4), (widen_on_vector, 0, HALF, QUARTER, 3, 4),
-            (wv_on_vector, 0, 0, HALF), (normalize, 0), (quantize_wv, 0, 0, HALF), (normalize, 1), (wk_on_vector, 0, 0), (normalize, 2), (quantize_hn, 0), (quantize_wk, 0, 0, 1), (quantize_hn, 1),
-            (widen_on_vector, 1, 0, HALF, 2, 4), (quantize_wk, 0, 1, 2), (normalize, 3), (quantize_hn, 2), (wk_on_vector, 1, 1), (quantize_wv, 0, *U), (quantize_hn, 3),
-            (widen_on_vector, 2, 0, HALF, 1, 4), (quantize_wk, 1, 1, 2), (quantize_wk, 1, 0, 1)]
-        tensor += [(first_product, 0, 0), (first_product, 0, 1), (turn_hn, 3), (wk_on_tensor, 1, 0, 1), (wk_on_tensor, 2, 0, 0), (first_product, 0, 2), (first_product, 0, 3), (wk_on_tensor, 2, 0, 1)]
-        scalar += [(rectify, 0, 0), (rectify, 0, 1), (hn_out, 3), (square, 0, 0), (wk_out, 1, 0, 1), (wk_out, 2, 0, 0), (rectify, 0, 2), (rectify, 0, 3), (widen_on_scalar, 2, 0, HALF, 0, 1), (square, 0, 1), (wk_out, 2, 0, 1)]
+        gpsimd = [(wv_on_gpsimd, 0, *U)]
+        tensor = [(spread_gain,), (wk_on_tensor, 0, 1, 0), (wk_on_tensor, 0, 1, 1), (turn_hn, 0), (wk_on_tensor, 0, 0, 0), (turn_hn, 1), (wk_on_tensor, 0, 0, 1),
+                  (turn_hn, 2), (turn_hn, 3), (wk_on_tensor, 1, 0, 0)]
+        scalar = [(widen_on_scalar, 0, QUARTER, 3 * QUARTER, 1, 2), (sum_squares, 0), (sum_squares, 1), (root, 0), (widen_on_scalar, 0, 768, QUARTER, 3, 4), (root, 1),
+                  (sum_squares, 2), (widen_on_scalar, 1, 0, QUARTER, 0, 1), (root, 2), (sum_squares, 3), (wk_out, 0, 1, 0), (root, 3), (wk_out, 0, 1, 1), (hn_out, 0), (wk_out, 0, 0, 0), (hn_out, 1),
+                  (widen_on_scalar, 1, QUARTER, QUARTER, 0, 1), (wk_out, 0, 0, 1), (hn_out, 2), (hn_out, 3), (widen_on_scalar, 1, 0, HALF, 1, 2), (wk_out, 1, 0, 0)]
+        vector = [(widen_on_vector, 0, 0, D, 0, 1), (widen_on_vector, 0, 0, QUARTER, 1, 2), (widen_on_vector, 0, 0, D, 2, 3), (widen_on_vector, 0, 0, QUARTER, 3, 4), (widen_on_vector, 0, QUARTER, HALF, 3, 4),
+            (wv_on_vector, 0, 0, QUARTER), (wv_on_vector, 0, QUARTER, QUARTER), (quantize_wv, 0, 0, QUARTER), (quantize_wv, 0, QUARTER, QUARTER)] + [(normalize, i) for i in range(NT)]
+        vector += [(quantize_wk, 0, 1, 2), (quantize_hn, 0), (quantize_wv, 0, *U), (quantize_hn, 1), (widen_on_vector, 1, 0, HALF, 2, 3), (quantize_wk, 0, 0, 1), (quantize_hn, 2), (quantize_hn, 3),
+                   (wk_on_vector, 1, 1), (widen_on_vector, 1, 0, HALF, 3, 4), (quantize_wk, 1, 1, 2), (widen_on_vector, 2, 0, HALF, 1, 4), (wk_on_vector, 2, 1), (quantize_wk, 1, 0, 1)]
+        tensor += [(first_product, 0, 0), (first_product, 0, 1), (wk_on_tensor, 1, 0, 1), (first_product, 0, 2), (first_product, 0, 3), (wk_on_tensor, 2, 0, 0), (wk_on_tensor, 2, 0, 1)]
+        scalar += [(rectify, 0, 0), (rectify, 0, 1), (widen_on_scalar, 2, 0, HALF, 0, 1), (wk_out, 1, 0, 1), (square, 0, 0), (rectify, 0, 2), (rectify, 0, 3), (wk_out, 2, 0, 0), (square, 0, 1), (wk_out, 2, 0, 1)]
         tensor += [(first_product, 1, 0), (first_product, 1, 1), (wv_on_tensor, 1, 0), (wk_on_tensor, 3, 0, 0), (first_product, 1, 2), (first_product, 1, 3), (wv_on_tensor, 1, QUARTER), (wk_on_tensor, 3, 0, 1)] + slice0[:FIRST]
         scalar += [(rectify, 1, 0), (rectify, 1, 1), (wv_out, 1, 0), (square, 1, 0), (wk_out, 3, 0, 0), (rectify, 1, 2), (rectify, 1, 3), (wv_out, 1, QUARTER), (square, 1, 1), (wk_out, 3, 0, 1)]
 
@@ -455,15 +456,14 @@ def tile_block_pc_kernel(tc, h_attn, norm2_w, ffn_wk, ffn_wv_bytes, ffn_wv_scale
         def wk_step(g):
             return [(wk_on_vector, g, 1)], [(quantize_wk, g, 1, 2)], [(quantize_wk, g, 0, 1)]
 
-        vector += wk_step(2)[0] + [(widen_on_vector, 3, 0, HALF, 0, 1)] + wk_step(2)[1] + lower(2)[1] + [(quantize_k, 0, 0, 2)] + wk_step(2)[2] + lower(2)[2]
-        vector += wk_step(3)[0] + [(widen_on_vector, 3, 0, HALF, 1, 4)] + wk_step(3)[1] + lower(3)[1] + lower(1)[2] + [(quantize_k, 1, 0, 2)] + wk_step(3)[2]
+        vector += lower(2)[1] + wk_step(2)[1] + lower(2)[2] + [(widen_on_vector, 3, 0, HALF, 0, 1), (quantize_k, 0, 0, 2)] + wk_step(2)[2]
+        vector += wk_step(3)[0] + [(widen_on_vector, 3, 0, HALF, 1, 4)] + wk_step(3)[1] + lower(3)[1] + lower(1)[2] + wk_step(4)[0] + [(quantize_k, 1, 0, 2)] + wk_step(3)[2]
         for g in (4, 5):
-            vector += wk_step(g)[0] + lower(g)[0] + lower(g - 1)[2] + lower(g)[1] + wk_step(g)[1] + wk_step(g)[2] + [(quantize_k, g - 2, 0, 2)]
+            vector += (wk_step(g)[0] if g == 5 else []) + lower(g)[0] + lower(g - 1)[2] + lower(g)[1] + wk_step(g)[1] + wk_step(g)[2] + [(quantize_k, g - 2, 0, 2)]
         vector += wk_step(6)[0] + [(widen_on_vector, 6, 0, D, 0, 2)] + lower(5)[2] + [(widen_on_vector, 6, 0, D, 2, 4)] + wk_step(6)[1] + wk_step(6)[2] + [(quantize_k, 4, 0, 2)]
         vector += wk_step(7)[0] + [(wv_on_vector, 6, *U), (widen_on_vector, 7, 0, D, 0, 4), (quantize_wv, 6, *U)] + wk_step(7)[1] + wk_step(7)[2] + [(quantize_k, 5, 0, 2)]
         vector += [(widen_on_vector, 1, *U, 0, 4), (wv_on_vector, 7, *U), (wv_on_vector, 1, *U), (quantize_wv, 7, *U), (quantize_wv, 6, 0, HALF), (quantize_k, 6, 0, 2)]
-        vector += [(widen_on_vector, 3, *R, 0, 4), (quantize_wv, 1, *U), (wv_on_vector, 3, *R), (widen_on_vector, 4, *R, 2, 4), (quantize_wv, 7, 0, HALF), (quantize_k, 7, 0, 2), (quantize_wv, 3, *R)]
-        scalar += by_plane(widen_on_scalar, 4, *R, 0, 2)
+        vector += [(widen_on_vector, 3, *R, 0, 4), (quantize_wv, 1, *U), (wv_on_vector, 3, *R), (widen_on_vector, 4, *R, 0, 4), (quantize_wv, 7, 0, HALF), (quantize_k, 7, 0, 2), (quantize_wv, 3, *R)]
         for g, run in ((5, R), (3, L), (2, U), (5, L), (4, L)):
             scalar += by_plane(widen_on_scalar, g, *run)
         scalar += [(wv_on_scalar, 5, *L)]

@@ -31,13 +31,14 @@ SLICES = ((0, HALF), (HALF, QUARTER), (HALF + QUARTER, QUARTER))
 WHOLE = [(0, D)]
 HALVES = [(0, HALF), (HALF, HALF)]
 BY_SLICE = list(SLICES)
-WIDENED = {g: WHOLE if g in (0, 6, 7) else HALVES if g in (1, 2) else BY_SLICE for g in range(G)}
+WIDENED = {g: WHOLE if g in (0, 6, 7) else HALVES if g in (1, 3) else BY_SLICE for g in range(G)}
 QUANTIZED = {g: [(0, QUARTER), (QUARTER, QUARTER), (HALF, HALF)] if g == 0 else HALVES if g in (6, 7) else WIDENED[g] for g in range(G)}
 LAG = 2
 BANKS = ("acc", "work")
-DEPTH = {"acc": 4, "work": 4, "wk_raw": 5, "grouped_wide": 2, "wk_codes": 3, "wk_scales": 3, "wv_bytes": 7, "planes_wide": 2, "planes": 4,
+DEPTH = {"acc": 4, "work": 4, "wk_raw": 4, "grouped_wide": 2, "wk_codes": 3, "wk_scales": 3, "wv_bytes": 7, "planes_wide": 2, "planes": 5,
          "wv_grouped": 5, "relu": 2, "k_grouped": 3, "result": 5}
 FIRST = 0
+SPARE = ()
 
 
 def tile_block_pc_kernel(tc, h_attn, norm2_w, ffn_wk, ffn_wv_bytes, ffn_wv_scale, out):
@@ -96,6 +97,9 @@ def tile_block_pc_kernel(tc, h_attn, norm2_w, ffn_wk, ffn_wv_bytes, ffn_wv_scale
         def acc_key(sl, i):
             return ("acc" if sl == 0 else "work", "sum", sl, i // (BANK // SLICES[sl][1]))
 
+        def wk_bank_key(g, q, b):
+            return ("acc" if (g, q, b) in SPARE else "work", "wk", g, q, b)
+
         def load_wk(g, q, b0, b1):
             raw = buffer(("wk_raw", g, q), [P, PACK, K_PASS], BF16)
             cols = slice(2 * P * b0, 2 * P * b1)
@@ -118,7 +122,7 @@ def tile_block_pc_kernel(tc, h_attn, norm2_w, ffn_wk, ffn_wv_bytes, ffn_wv_scale
             return buffer(("grouped_wide", g), [P, Q * K_PASS * PACK], BF16)[:, q * K_PASS * PACK:(q + 1) * K_PASS * PACK]
 
         def wk_on_tensor(g, q, b, first=0, last=2):
-            bank = buffer(("work", "wk", g, q, b), [P, PACK, 64, PACK], BF16)
+            bank = buffer(wk_bank_key(g, q, b), [P, PACK, 64, PACK], BF16)
             for part in range(first, last):
                 c0 = 2 * P * b + P * part
                 nc.tensor.matmul(
@@ -132,14 +136,21 @@ def tile_block_pc_kernel(tc, h_attn, norm2_w, ffn_wk, ffn_wv_bytes, ffn_wv_scale
         def wk_out(g, q, b):
             nc.scalar.copy(
                 out=wk_grouped(g, q).bitcast(F32).rearrange("p (t w) -> p t w", t=PACK)[:, :, P * b:P * b + P],
-                in_=buffer(("work", "wk", g, q, b))[:].rearrange("p t m j -> p t (m j)").bitcast(F32),
+                in_=buffer(wk_bank_key(g, q, b))[:].rearrange("p t m j -> p t (m j)").bitcast(F32),
             )
 
-        def wk_on_vector(g, q):
+        def wk_on_vector(g, q, b0=0, b1=2):
+            rows = slice(32 * b0, 32 * b1)
             nc.vector.tensor_copy(
-                out=wk_grouped(g, q).rearrange("p (t m i j) -> p m t j i", t=PACK, i=RUN, j=PACK),
-                in_=buffer(("wk_raw", g, q))[:].rearrange("p j (m i t) -> p m t j i", i=RUN, t=PACK),
+                out=wk_grouped(g, q).rearrange("p (t m i j) -> p m t j i", t=PACK, i=RUN, j=PACK)[:, rows, :, :, :],
+                in_=buffer(("wk_raw", g, q))[:].rearrange("p j (m i t) -> p m t j i", i=RUN, t=PACK)[:, rows, :, :, :],
             )
+
+        def wk_on_gpsimd(g, q, b):
+            nc.gpsimd.tensor_scalar(
+                out=wk_grouped(g, q).rearrange("p (t m j) -> p t m j", t=PACK, j=PACK)[:, :, 64 * b:64 * b + 64, :],
+                in0=buffer(("wk_raw", g, q))[:, :, 2 * P * b:2 * P * (b + 1)].rearrange("p j (m t) -> p t m j", t=PACK),
+                scalar1=1.0, scalar2=0.0, op0=ALU.mult, op1=ALU.add)
 
         def wk_operand(g):
             return (buffer(("wk_codes", g), [P, Q * K_PASS], U32), buffer(("wk_scales", g), [P, Q * K_PASS], U8))
@@ -319,11 +330,17 @@ def tile_block_pc_kernel(tc, h_attn, norm2_w, ffn_wk, ffn_wv_bytes, ffn_wv_scale
                 for q in range(Q):
                     nc.tensor.transpose(bank[:, q, v, :], words[:, q * P:(q + 1) * P], ident_f32[:])
 
+        def hn_views(i):
+            return (buffer(("result", "hn_grouped", i), [P, D], BF16)[:].bitcast(F32).rearrange("p (q n v) -> p q n v", q=Q, v=2),
+                    buffer(("work", "hn", i))[:].rearrange("p q v n -> p q n v"))
+
         def hn_out(i):
-            nc.scalar.copy(
-                out=buffer(("result", "hn_grouped", i), [P, D], BF16)[:].bitcast(F32).rearrange("p (q n v) -> p q n v", q=Q, v=2),
-                in_=buffer(("work", "hn", i))[:].rearrange("p q v n -> p q n v"),
-            )
+            words, bank = hn_views(i)
+            nc.scalar.copy(out=words, in_=bank)
+
+        def hn_out_on_vector(i):
+            words, bank = hn_views(i)
+            nc.vector.tensor_copy(out=words, in_=bank)
 
         def quantize_hn(i):
             for q in range(Q):
@@ -360,10 +377,11 @@ def tile_block_pc_kernel(tc, h_attn, norm2_w, ffn_wk, ffn_wv_bytes, ffn_wv_scale
             load_scale: lambda first, last: ([], [("scale", g) for g in range(first, last)], []),
             load_gain: lambda: ([], [("gain_row",)], []),
             load_h: lambda i: ([], [("h", i)], []),
-            wk_on_tensor: lambda g, q, b, first=0, last=2: ([("raw", g, q, b)], [("wk_bank", g, q, b, part) for part in range(first, last)], [("wk_raw", g, q), ("work", "wk", g, q, b)]),
-            wk_out: lambda g, q, b: ([("wk_bank", g, q, b, 0), ("wk_bank", g, q, b, 1)], [("wk", g, q, b)], [("grouped_wide", g), ("work", "wk", g, q, b)]),
-            wk_on_vector: lambda g, q: (
-                [("raw", g, q, 0), ("raw", g, q, 1)], [("wk", g, q, 0), ("wk", g, q, 1)], [("wk_raw", g, q), ("grouped_wide", g)]),
+            wk_on_tensor: lambda g, q, b, first=0, last=2: ([("raw", g, q, b)], [("wk_bank", g, q, b, part) for part in range(first, last)], [("wk_raw", g, q), wk_bank_key(g, q, b)]),
+            wk_out: lambda g, q, b: ([("wk_bank", g, q, b, 0), ("wk_bank", g, q, b, 1)], [("wk", g, q, b)], [("grouped_wide", g), wk_bank_key(g, q, b)]),
+            wk_on_gpsimd: lambda g, q, b: ([("raw", g, q, b)], [("wk", g, q, b)], [("wk_raw", g, q), ("grouped_wide", g)]),
+            wk_on_vector: lambda g, q, b0=0, b1=2: (
+                [("raw", g, q, b) for b in range(b0, b1)], [("wk", g, q, b) for b in range(b0, b1)], [("wk_raw", g, q), ("grouped_wide", g)]),
             quantize_wk: lambda g, q0, q1: (
                 [("wk", g, q, b) for q in range(q0, q1) for b in range(2)], [("wk_mx", g, q) for q in range(q0, q1)],
                 [("grouped_wide", g), ("wk_codes", g), ("wk_scales", g)]),
@@ -397,6 +415,7 @@ def tile_block_pc_kernel(tc, h_attn, norm2_w, ffn_wk, ffn_wv_bytes, ffn_wv_scale
             normalize: lambda i: ([("rstd", i), ("gain",)], [("hn", i)], [("acc", "gain"), ("result", "hn", i)]),
             turn_hn: lambda i: ([("hn", i)], [("hn_bank", i)], [("result", "hn", i), ("work", "hn", i)]),
             hn_out: lambda i: ([("hn_bank", i)], [("hn_grouped", i)], [("work", "hn", i), ("result", "hn_grouped", i)]),
+            hn_out_on_vector: lambda i: ([("hn_bank", i)], [("hn_grouped", i)], [("work", "hn", i), ("result", "hn_grouped", i)]),
             quantize_hn: lambda i: ([("hn_grouped", i)], [("hn_mx", i)], [("result", "hn_grouped", i)]),
         }
 
@@ -436,8 +455,8 @@ def tile_block_pc_kernel(tc, h_attn, norm2_w, ffn_wk, ffn_wv_bytes, ffn_wv_scale
                   (widen_on_scalar, 1, QUARTER, QUARTER, 0, 1), (wk_out, 0, 0, 1), (hn_out, 2), (hn_out, 3), (widen_on_scalar, 1, 0, HALF, 1, 2), (wk_out, 1, 0, 0)]
         vector = [(widen_on_vector, 0, 0, D, 0, 1), (widen_on_vector, 0, 0, QUARTER, 1, 2), (widen_on_vector, 0, 0, D, 2, 3), (widen_on_vector, 0, 0, QUARTER, 3, 4), (widen_on_vector, 0, QUARTER, HALF, 3, 4),
             (wv_on_vector, 0, 0, QUARTER), (wv_on_vector, 0, QUARTER, QUARTER), (quantize_wv, 0, 0, QUARTER), (quantize_wv, 0, QUARTER, QUARTER)] + [(normalize, i) for i in range(NT)]
-        vector += [(quantize_wk, 0, 1, 2), (quantize_hn, 0), (quantize_wv, 0, *U), (quantize_hn, 1), (widen_on_vector, 1, 0, HALF, 2, 3), (quantize_wk, 0, 0, 1), (quantize_hn, 2), (quantize_hn, 3),
-                   (wk_on_vector, 1, 1), (widen_on_vector, 1, 0, HALF, 3, 4), (quantize_wk, 1, 1, 2), (widen_on_vector, 2, 0, HALF, 1, 4), (wk_on_vector, 2, 1), (quantize_wk, 1, 0, 1)]
+        vector += [(quantize_wk, 0, 1, 2), (quantize_hn, 0), (quantize_wv, 0, *U), (quantize_hn, 1), (widen_on_vector, 1, 0, HALF, 2, 3), (quantize_wk, 0, 0, 1), (quantize_hn, 2),
+                   (wk_on_vector, 1, 1), (quantize_hn, 3), (widen_on_vector, 1, 0, HALF, 3, 4), (quantize_wk, 1, 1, 2), (widen_on_vector, 2, 0, HALF, 1, 4), (wk_on_vector, 2, 1), (quantize_wk, 1, 0, 1)]
         tensor += [(first_product, 0, 0), (first_product, 0, 1), (wk_on_tensor, 1, 0, 1), (first_product, 0, 2), (first_product, 0, 3), (wk_on_tensor, 2, 0, 0), (wk_on_tensor, 2, 0, 1)]
         scalar += [(rectify, 0, 0), (rectify, 0, 1), (widen_on_scalar, 2, 0, HALF, 0, 1), (wk_out, 1, 0, 1), (square, 0, 0), (rectify, 0, 2), (rectify, 0, 3), (wk_out, 2, 0, 0), (square, 0, 1), (wk_out, 2, 0, 1)]
         tensor += [(first_product, 1, 0), (first_product, 1, 1), (wv_on_tensor, 1, 0), (wk_on_tensor, 3, 0, 0), (first_product, 1, 2), (first_product, 1, 3), (wv_on_tensor, 1, QUARTER), (wk_on_tensor, 3, 0, 1)] + slice0[:FIRST]
@@ -457,23 +476,24 @@ def tile_block_pc_kernel(tc, h_attn, norm2_w, ffn_wk, ffn_wv_bytes, ffn_wv_scale
             return [(wk_on_vector, g, 1)], [(quantize_wk, g, 1, 2)], [(quantize_wk, g, 0, 1)]
 
         vector += lower(2)[1] + wk_step(2)[1] + lower(2)[2] + [(widen_on_vector, 3, 0, HALF, 0, 1), (quantize_k, 0, 0, 2)] + wk_step(2)[2]
-        vector += wk_step(3)[0] + [(widen_on_vector, 3, 0, HALF, 1, 4)] + wk_step(3)[1] + lower(3)[1] + lower(1)[2] + wk_step(4)[0] + [(quantize_k, 1, 0, 2)] + wk_step(3)[2]
+        vector += wk_step(3)[0] + [(widen_on_vector, 3, 0, HALF, 1, 4)] + wk_step(3)[1] + lower(3)[1] + wk_step(4)[0] + lower(1)[2] + [(quantize_k, 1, 0, 2)] + wk_step(3)[2]
         for g in (4, 5):
-            vector += (wk_step(g)[0] if g == 5 else []) + lower(g)[0] + lower(g - 1)[2] + lower(g)[1] + wk_step(g)[1] + wk_step(g)[2] + [(quantize_k, g - 2, 0, 2)]
-        vector += wk_step(6)[0] + [(widen_on_vector, 6, 0, D, 0, 2)] + lower(5)[2] + [(widen_on_vector, 6, 0, D, 2, 4)] + wk_step(6)[1] + wk_step(6)[2] + [(quantize_k, 4, 0, 2)]
-        vector += wk_step(7)[0] + [(wv_on_vector, 6, *U), (widen_on_vector, 7, 0, D, 0, 4), (quantize_wv, 6, *U)] + wk_step(7)[1] + wk_step(7)[2] + [(quantize_k, 5, 0, 2)]
+            vector += lower(g)[0] + lower(g - 1)[2] + lower(g)[1] + wk_step(g)[1] + wk_step(g)[2] + wk_step(g + 1)[0] + [(quantize_k, g - 2, 0, 2)]
+        vector += [(widen_on_vector, 6, 0, D, 0, 2)] + lower(5)[2] + [(widen_on_vector, 6, 0, D, 2, 4)] + wk_step(6)[1] + wk_step(6)[2] + wk_step(7)[0] + [(quantize_k, 4, 0, 2)]
+        vector += [(wv_on_vector, 6, *U), (widen_on_vector, 7, 0, D, 0, 4), (quantize_wv, 6, *U)] + wk_step(7)[1] + wk_step(7)[2] + [(quantize_k, 5, 0, 2)]
         vector += [(widen_on_vector, 1, *U, 0, 4), (wv_on_vector, 7, *U), (wv_on_vector, 1, *U), (quantize_wv, 7, *U), (quantize_wv, 6, 0, HALF), (quantize_k, 6, 0, 2)]
-        vector += [(widen_on_vector, 3, *R, 0, 4), (quantize_wv, 1, *U), (wv_on_vector, 3, *R), (widen_on_vector, 4, *R, 0, 4), (quantize_wv, 7, 0, HALF), (quantize_k, 7, 0, 2), (quantize_wv, 3, *R)]
-        for g, run in ((5, R), (3, L), (2, U), (5, L), (4, L)):
+        vector += [(widen_on_vector, 3, *U, 0, 4), (quantize_wv, 1, *U), (wv_on_vector, 3, *U), (quantize_wv, 7, 0, HALF), (widen_on_vector, 4, *R, 3, 4), (quantize_k, 7, 0, 2), (quantize_wv, 3, *U)]
+        scalar += by_plane(widen_on_scalar, 4, *R, 0, 3)
+        for g, run in ((5, R), (2, R), (2, L), (5, L), (4, L)):
             scalar += by_plane(widen_on_scalar, g, *run)
         scalar += [(wv_on_scalar, 5, *L)]
-        tensor += slice0[paced(G - 1):-NT] + products(2, (0, 6)) + slice0[-NT:] + products(2, (7, 1, 3)) + products(1, (0, 6))
-        tensor += products(2, (4, 5)) + products(1, (7, 1, 3)) + products(2, (2,)) + products(1, (2,))
+        tensor += slice0[paced(G - 1):-NT] + products(2, (0, 6)) + products(1, (0,)) + slice0[-NT:] + products(2, (7, 1, 3, 4)) + products(1, (6,))
+        tensor += products(2, (5,)) + products(1, (7,)) + products(2, (2,)) + products(1, (1, 3, 2))
         tensor += [(second_product, 1, g, i, i + 2) for i in (0, 2) for g in (4, 5)]
         vector += [
-            (wv_on_vector, 4, *R), (finish, 0, 0, 1), (wv_on_vector, 5, *R), (quantize_wv, 4, *R), (wv_on_vector, 3, *L), (quantize_wv, 5, *R), (finish, 0, 1, 2),
-            (quantize_wv, 3, *L), (wv_on_vector, 2, *U), (finish, 0, 2, 3), (quantize_wv, 2, *U),
-            (wv_on_vector, 4, *L), (finish, 0, 3, 4), (quantize_wv, 4, *L), (finish, 2, 0, 1), (quantize_wv, 5, *L),
+            (wv_on_vector, 4, *R), (finish, 0, 0, 1), (wv_on_vector, 5, *R), (quantize_wv, 4, *R), (wv_on_vector, 2, *R), (quantize_wv, 5, *R), (finish, 0, 1, 2), (quantize_wv, 2, *R),
+            (wv_on_vector, 2, *L), (finish, 0, 2, 3), (quantize_wv, 2, *L), (finish, 0, 3, 4),
+            (wv_on_vector, 4, *L), (finish, 2, 0, 1), (quantize_wv, 4, *L), (quantize_wv, 5, *L),
         ] + [(finish, sl, i, i + 1) for sl in (2, 1) for i in range(NT)][1:]
 
 

@@ -36,7 +36,7 @@ QUANTIZED = {g: [(0, QUARTER), (QUARTER, QUARTER), (HALF, HALF)] if g == 0 else 
 LAG = 2
 BANKS = ("acc", "work")
 DEPTH = {"acc": 4, "work": 4, "wk_raw": 4, "grouped_wide": 2, "wk_codes": 3, "wk_scales": 3, "wv_bytes": 7, "planes_wide": 2, "planes": 5,
-         "wv_grouped": 5, "relu": 2, "k_grouped": 3, "result": 5}
+         "wv_grouped": 6, "relu": 2, "k_grouped": 2, "result": 5}
 FIRST = 0
 SPARE = ()
 
@@ -459,8 +459,8 @@ def tile_block_pc_kernel(tc, h_attn, norm2_w, ffn_wk, ffn_wv_bytes, ffn_wv_scale
                    (wk_on_vector, 1, 1), (quantize_hn, 3), (widen_on_vector, 1, 0, HALF, 3, 4), (quantize_wk, 1, 1, 2), (widen_on_vector, 2, 0, HALF, 1, 4), (wk_on_vector, 2, 1), (quantize_wk, 1, 0, 1)]
         tensor += [(first_product, 0, 0), (first_product, 0, 1), (wk_on_tensor, 1, 0, 1), (first_product, 0, 2), (first_product, 0, 3), (wk_on_tensor, 2, 0, 0), (wk_on_tensor, 2, 0, 1)]
         scalar += [(rectify, 0, 0), (rectify, 0, 1), (widen_on_scalar, 2, 0, HALF, 0, 1), (wk_out, 1, 0, 1), (square, 0, 0), (rectify, 0, 2), (rectify, 0, 3), (wk_out, 2, 0, 0), (square, 0, 1), (wk_out, 2, 0, 1)]
-        tensor += [(first_product, 1, 0), (first_product, 1, 1), (wv_on_tensor, 1, 0), (wk_on_tensor, 3, 0, 0), (first_product, 1, 2), (first_product, 1, 3), (wv_on_tensor, 1, QUARTER), (wk_on_tensor, 3, 0, 1)] + slice0[:FIRST]
-        scalar += [(rectify, 1, 0), (rectify, 1, 1), (wv_out, 1, 0), (square, 1, 0), (wk_out, 3, 0, 0), (rectify, 1, 2), (rectify, 1, 3), (wv_out, 1, QUARTER), (square, 1, 1), (wk_out, 3, 0, 1)]
+        tensor += [(first_product, 1, 0), (first_product, 1, 1), (wv_on_tensor, 1, 0), (wk_on_tensor, 3, 0, 0), (first_product, 1, 2), (first_product, 1, 3), (wk_on_tensor, 3, 0, 1)] + slice0[:FIRST]
+        scalar += [(rectify, 1, 0), (rectify, 1, 1), (wv_out, 1, 0), (square, 1, 0), (wk_out, 3, 0, 0), (rectify, 1, 2), (rectify, 1, 3), (wk_out, 3, 0, 1), (square, 1, 1)]
 
         def paced(g):
             return NT * (g - 1) + FIRST - (g - 1) // LAG
@@ -476,25 +476,25 @@ def tile_block_pc_kernel(tc, h_attn, norm2_w, ffn_wk, ffn_wv_bytes, ffn_wv_scale
             return [(wk_on_vector, g, 1)], [(quantize_wk, g, 1, 2)], [(quantize_wk, g, 0, 1)]
 
         vector += lower(2)[1] + wk_step(2)[1] + lower(2)[2] + [(widen_on_vector, 3, 0, HALF, 0, 1), (quantize_k, 0, 0, 2)] + wk_step(2)[2]
-        vector += wk_step(3)[0] + [(widen_on_vector, 3, 0, HALF, 1, 4)] + wk_step(3)[1] + lower(3)[1] + wk_step(4)[0] + lower(1)[2] + [(quantize_k, 1, 0, 2)] + wk_step(3)[2]
+        vector += wk_step(3)[0] + [(widen_on_vector, 3, 0, HALF, 1, 4)] + wk_step(3)[1] + lower(3)[1] + [(wv_on_vector, 1, QUARTER, QUARTER)] + wk_step(4)[0] + lower(1)[2] + [(quantize_k, 1, 0, 2)] + wk_step(3)[2]
         for g in (4, 5):
             vector += lower(g)[0] + lower(g - 1)[2] + lower(g)[1] + wk_step(g)[1] + wk_step(g)[2] + wk_step(g + 1)[0] + [(quantize_k, g - 2, 0, 2)]
         vector += [(widen_on_vector, 6, 0, D, 0, 2)] + lower(5)[2] + [(widen_on_vector, 6, 0, D, 2, 4)] + wk_step(6)[1] + wk_step(6)[2] + wk_step(7)[0] + [(quantize_k, 4, 0, 2)]
         vector += [(wv_on_vector, 6, *U), (widen_on_vector, 7, 0, D, 0, 4), (quantize_wv, 6, *U)] + wk_step(7)[1] + wk_step(7)[2] + [(quantize_k, 5, 0, 2)]
         vector += [(widen_on_vector, 1, *U, 0, 4), (wv_on_vector, 7, *U), (wv_on_vector, 1, *U), (quantize_wv, 7, *U), (quantize_wv, 6, 0, HALF), (quantize_k, 6, 0, 2)]
-        vector += [(widen_on_vector, 3, *U, 0, 4), (quantize_wv, 1, *U), (wv_on_vector, 3, *U), (quantize_wv, 7, 0, HALF), (widen_on_vector, 4, *R, 3, 4), (quantize_k, 7, 0, 2), (quantize_wv, 3, *U)]
+        vector += [(widen_on_vector, 3, *U, 0, 4), (quantize_wv, 1, *U), (quantize_wv, 7, 0, HALF), (quantize_k, 7, 0, 2), (wv_on_vector, 3, *U)]
         scalar += by_plane(widen_on_scalar, 4, *R, 0, 3)
         for g, run in ((5, R), (2, R), (2, L), (5, L), (4, L)):
             scalar += by_plane(widen_on_scalar, g, *run)
         scalar += [(wv_on_scalar, 5, *L)]
-        tensor += slice0[paced(G - 1):-NT] + products(2, (0, 6)) + products(1, (0,)) + slice0[-NT:] + products(2, (7, 1, 3, 4)) + products(1, (6,))
-        tensor += products(2, (5,)) + products(1, (7,)) + products(2, (2,)) + products(1, (1, 3, 2))
+        gpsimd += [(wv_on_gpsimd, 4, *R)]
+        tensor += slice0[paced(G - 1):-NT] + products(2, (0, 6, 1)) + slice0[-NT:] + products(2, (7,)) + products(1, (0, 6, 7, 1)) + products(2, (3,))
+        tensor += products(1, (3,)) + products(2, (5, 4, 2)) + products(1, (2,))
         tensor += [(second_product, 1, g, i, i + 2) for i in (0, 2) for g in (4, 5)]
-        vector += [
-            (wv_on_vector, 4, *R), (finish, 0, 0, 1), (wv_on_vector, 5, *R), (quantize_wv, 4, *R), (wv_on_vector, 2, *R), (quantize_wv, 5, *R), (finish, 0, 1, 2), (quantize_wv, 2, *R),
-            (wv_on_vector, 2, *L), (finish, 0, 2, 3), (quantize_wv, 2, *L), (finish, 0, 3, 4),
-            (wv_on_vector, 4, *L), (finish, 2, 0, 1), (quantize_wv, 4, *L), (quantize_wv, 5, *L),
-        ] + [(finish, sl, i, i + 1) for sl in (2, 1) for i in range(NT)][1:]
+        vector += [(widen_on_vector, 4, *R, 3, 4)] + [(finish, 0, i, i + 1) for i in range(NT)] + [
+            (quantize_wv, 3, *U), (wv_on_vector, 5, *R), (wv_on_vector, 2, *R), (quantize_wv, 5, *R), (quantize_wv, 4, *R), (quantize_wv, 2, *R), (wv_on_vector, 2, *L),
+            (wv_on_vector, 4, *L), (quantize_wv, 2, *L), (quantize_wv, 4, *L), (quantize_wv, 5, *L),
+        ] + [(finish, sl, i, i + 1) for sl in (2, 1) for i in range(NT)]
 
 
         queues = [sync, tensor, scalar, vector, gpsimd]

@@ -482,17 +482,16 @@ def tile_block_pc_kernel(tc, h_attn, norm2_w, ffn_wk, ffn_wv_bytes, ffn_wv_scale
         vector += [(widen_on_vector, 6, 0, D, 0, 2)] + lower(5)[2] + [(widen_on_vector, 6, 0, D, 2, 4)] + wk_step(6)[1] + wk_step(6)[2] + wk_step(7)[0] + [(quantize_k, 4, 0, 2)]
         vector += [(wv_on_vector, 6, *U), (widen_on_vector, 7, 0, D, 0, 4), (quantize_wv, 6, *U)] + wk_step(7)[1] + wk_step(7)[2] + [(quantize_k, 5, 0, 2)]
         vector += [(widen_on_vector, 1, *U, 0, 4), (wv_on_vector, 7, *U), (wv_on_vector, 1, *U), (quantize_wv, 7, *U), (quantize_wv, 6, 0, HALF), (quantize_k, 6, 0, 2)]
-        vector += [(widen_on_vector, 3, *U, 0, 4), (quantize_wv, 1, *U), (quantize_wv, 7, 0, HALF), (quantize_k, 7, 0, 2), (wv_on_vector, 3, *U)]
+        vector += [(widen_on_vector, 3, *U, 0, 4), (quantize_wv, 1, *U), (quantize_wv, 7, 0, HALF), (wv_on_vector, 3, *R), (quantize_k, 7, 0, 2), (wv_on_vector, 3, *L)]
         scalar += by_plane(widen_on_scalar, 4, *R, 0, 3)
         for g, run in ((5, R), (2, R), (2, L), (5, L), (4, L)):
             scalar += by_plane(widen_on_scalar, g, *run)
         scalar += [(wv_on_scalar, 5, *L)]
         gpsimd += [(wv_on_gpsimd, 4, *R)]
-        tensor += slice0[paced(G - 1):-NT] + products(2, (0, 6, 1)) + slice0[-NT:] + products(2, (7,)) + products(1, (0, 6, 7, 1)) + products(2, (3,))
-        tensor += products(1, (3,)) + products(2, (5, 4, 2)) + products(1, (2,))
+        tensor += slice0[paced(G - 1):-NT] + products(2, (0, 6, 1)) + slice0[-NT:] + products(2, (7, 3)) + products(1, (0, 6, 7, 1)) + products(2, (4,)) + products(1, (3,)) + products(2, (5, 2)) + products(1, (2,))
         tensor += [(second_product, 1, g, i, i + 2) for i in (0, 2) for g in (4, 5)]
-        vector += [(widen_on_vector, 4, *R, 3, 4)] + [(finish, 0, i, i + 1) for i in range(NT)] + [
-            (quantize_wv, 3, *U), (wv_on_vector, 5, *R), (wv_on_vector, 2, *R), (quantize_wv, 5, *R), (quantize_wv, 4, *R), (quantize_wv, 2, *R), (wv_on_vector, 2, *L),
+        vector += [(widen_on_vector, 4, *R, 3, 4), (quantize_wv, 3, *U)] + [(finish, 0, i, i + 1) for i in range(NT)] + [
+            (quantize_wv, 4, *R), (wv_on_vector, 5, *R), (wv_on_vector, 2, *R), (quantize_wv, 5, *R), (wv_on_vector, 2, *L), (quantize_wv, 2, *R),
             (wv_on_vector, 4, *L), (quantize_wv, 2, *L), (quantize_wv, 4, *L), (quantize_wv, 5, *L),
         ] + [(finish, sl, i, i + 1) for sl in (2, 1) for i in range(NT)]
 

@@ -486,13 +486,13 @@ def tile_block_pc_kernel(tc, h_attn, norm2_w, ffn_wk, ffn_wv_bytes, ffn_wv_scale
         scalar += by_plane(widen_on_scalar, 4, *R, 0, 3)
         for g, run in ((5, R), (2, R), (2, L), (5, L), (4, L)):
             scalar += by_plane(widen_on_scalar, g, *run)
-        scalar += [(wv_on_scalar, 5, *L)]
+        scalar += [(wv_on_scalar, 5, *L), (wv_on_scalar, 4, L[0], P)]
         gpsimd += [(wv_on_gpsimd, 4, *R)]
         tensor += slice0[paced(G - 1):-NT] + products(2, (0, 6, 1)) + slice0[-NT:] + products(2, (7, 3)) + products(1, (0, 6, 7, 1)) + products(2, (4,)) + products(1, (3,)) + products(2, (5, 2)) + products(1, (2,))
-        tensor += [(second_product, 1, g, i, i + 2) for i in (0, 2) for g in (4, 5)]
+        tensor += [(second_product, 1, g, i, i + 2) for i in (0, 2) for g in (5, 4)]
         vector += [(widen_on_vector, 4, *R, 3, 4), (quantize_wv, 3, *U)] + [(finish, 0, i, i + 1) for i in range(NT)] + [
-            (quantize_wv, 4, *R), (wv_on_vector, 5, *R), (wv_on_vector, 2, *R), (quantize_wv, 5, *R), (wv_on_vector, 2, *L), (quantize_wv, 2, *R),
-            (wv_on_vector, 4, *L), (quantize_wv, 2, *L), (quantize_wv, 4, *L), (quantize_wv, 5, *L),
+            (quantize_wv, 4, *R), (wv_on_vector, 5, *R), (wv_on_vector, 2, *R), (quantize_wv, 5, *R), (quantize_wv, 2, *R), (wv_on_vector, 2, *L),
+            (wv_on_vector, 4, L[0] + P, P), (quantize_wv, 2, *L), (quantize_wv, 5, *L), (quantize_wv, 4, *L),
         ] + [(finish, sl, i, i + 1) for sl in (2, 1) for i in range(NT)]
 
 

@@ -56,8 +56,8 @@ def tile_block_pc_kernel(tc, h_attn, norm2_w, ffn_wk, ffn_wv_bytes, ffn_wv_scale
         ctx.enter_context(tc.manual_schedule())
 
         h_sb = keep.tile([P, NT, D], BF16, align_bytes=64, name="h_sb")
-        h_codes = keep.tile([P, Q, S], U32, align_bytes=64, name="h_codes")
-        h_scales = keep.tile([P, Q, S], U8, align_bytes=64, name="h_scales")
+        h_codes = keep.tile([P, 2, Q, 2 * P], U32, align_bytes=64, name="h_codes")
+        h_scales = keep.tile([P, 2, Q, 2 * P], U8, align_bytes=64, name="h_scales")
         wv_scale = keep.tile([P, G, 2 * PACK], F32, align_bytes=64, name="wv_scale")
         wv_codes = keep.tile([P, G, D], U32, align_bytes=64, name="wv_codes")
         wv_scales = keep.tile([P, G, D], U8, align_bytes=64, name="wv_scales")
@@ -226,7 +226,6 @@ def tile_block_pc_kernel(tc, h_attn, norm2_w, ffn_wk, ffn_wv_bytes, ffn_wv_scale
 
         def first_product(g, i):
             a, u = divmod(i, 2)
-            tokens = slice(2 * P * a, 2 * P * (a + 1))
             bank = buffer(("work", "hidden", g, i), [P, 2, 2 * P], F32)
             codes, scales = wk_operand(g)
             for e in range(2):
@@ -236,8 +235,8 @@ def tile_block_pc_kernel(tc, h_attn, norm2_w, ffn_wk, ffn_wv_bytes, ffn_wv_scale
                         out=bank[:, e, :],
                         lhsT=codes[:, cols].bitcast(FP8X4),
                         lhsT_scale=scales[:, cols],
-                        rhs=h_codes[:, q, tokens].bitcast(FP8X4),
-                        rhs_scale=h_scales[:, q, tokens],
+                        rhs=h_codes[:, a, q, :].bitcast(FP8X4),
+                        rhs_scale=h_scales[:, a, q, :],
                         start=(q == 0),
                         stop=(q == Q - 1),
                     )
@@ -331,7 +330,7 @@ def tile_block_pc_kernel(tc, h_attn, norm2_w, ffn_wk, ffn_wv_bytes, ffn_wv_scale
                     nc.tensor.transpose(bank[:, q, v, :], words[:, q * P:(q + 1) * P], ident_f32[:])
 
         def hn_views(i):
-            return (buffer(("result", "hn_grouped", i), [P, D], BF16)[:].bitcast(F32).rearrange("p (q n v) -> p q n v", q=Q, v=2),
+            return (buffer(("planes", "hn_grouped", i // 2), [P, 2 * D], BF16)[:].bitcast(F32).rearrange("p (q i n v) -> p q i n v", q=Q, i=2, v=2)[:, :, i % 2, :, :],
                     buffer(("work", "hn", i))[:].rearrange("p q v n -> p q n v"))
 
         def hn_out(i):
@@ -342,13 +341,12 @@ def tile_block_pc_kernel(tc, h_attn, norm2_w, ffn_wk, ffn_wv_bytes, ffn_wv_scale
             words, bank = hn_views(i)
             nc.vector.tensor_copy(out=words, in_=bank)
 
-        def quantize_hn(i):
-            for q in range(Q):
-                nc.vector.quantize_mx(
-                    out=h_codes[:, q, i * P:(i + 1) * P].bitcast(FP8X4),
-                    scales=h_scales[:, q, i * P:(i + 1) * P],
-                    in_=buffer(("result", "hn_grouped", i))[:, q * K_PASS:(q + 1) * K_PASS],
-                )
+        def quantize_hn(a):
+            nc.vector.quantize_mx(
+                out=h_codes[:, a, :, :].rearrange("p q n -> p (q n)").bitcast(FP8X4),
+                scales=h_scales[:, a, :, :].rearrange("p q n -> p (q n)"),
+                in_=buffer(("planes", "hn_grouped", a))[:],
+            )
 
         nc.vector.memset(ones[:], 1.0)
         nc.vector.memset(gain_row[:], 0.0)
@@ -396,7 +394,7 @@ def tile_block_pc_kernel(tc, h_attn, norm2_w, ffn_wk, ffn_wv_bytes, ffn_wv_scale
                 [("wv_bank", g, c0)], cells("grouped", g, c0, QUARTER), [grouped_key(g, c0), ("work", "wv", g, c0)]),
             quantize_wv: lambda g, c0, w: (cells("grouped", g, c0, w), cells("wv_mx", g, c0, w), [grouped_key(g, c0)]),
             first_product: lambda g, i: (
-                [("wk_mx", g, q) for q in range(Q)] + [("hn_mx", i // 2 * 2), ("hn_mx", i // 2 * 2 + 1)], [("hidden", g, i)],
+                [("wk_mx", g, q) for q in range(Q)] + [("hn_mx", i // 2)], [("hidden", g, i)],
                 [("wk_codes", g), ("wk_scales", g), ("work", "hidden", g, i)]),
             rectify: lambda g, i: ([("hidden", g, i)], [("relu", g, i)], [("work", "hidden", g, i), ("relu", g, i // 2)]),
             square: lambda g, a: ([("relu", g, 2 * a), ("relu", g, 2 * a + 1)], [("k", g, a)], [("relu", g, a), ("k_grouped", g)]),
@@ -414,9 +412,8 @@ def tile_block_pc_kernel(tc, h_attn, norm2_w, ffn_wk, ffn_wv_bytes, ffn_wv_scale
             root: lambda i: ([("sum", i)], [("rstd", i)], []),
             normalize: lambda i: ([("rstd", i), ("gain",)], [("hn", i)], [("acc", "gain"), ("result", "hn", i)]),
             turn_hn: lambda i: ([("hn", i)], [("hn_bank", i)], [("result", "hn", i), ("work", "hn", i)]),
-            hn_out: lambda i: ([("hn_bank", i)], [("hn_grouped", i)], [("work", "hn", i), ("result", "hn_grouped", i)]),
-            hn_out_on_vector: lambda i: ([("hn_bank", i)], [("hn_grouped", i)], [("work", "hn", i), ("result", "hn_grouped", i)]),
-            quantize_hn: lambda i: ([("hn_grouped", i)], [("hn_mx", i)], [("result", "hn_grouped", i)]),
+            hn_out: lambda i: ([("hn_bank", i)], [("hn_grouped", i)], [("work", "hn", i), ("planes", "hn_grouped", i // 2)]),
+                        quantize_hn: lambda i: ([("hn_grouped", i)], [("hn_mx", i)], [("result", "hn_grouped", i)]),
         }
 
         def by_plane(job, g, c0, w, first=0, last=PACK):
@@ -455,8 +452,8 @@ def tile_block_pc_kernel(tc, h_attn, norm2_w, ffn_wk, ffn_wv_bytes, ffn_wv_scale
                   (widen_on_scalar, 1, QUARTER, QUARTER, 0, 1), (wk_out, 0, 0, 1), (hn_out, 2), (hn_out, 3), (widen_on_scalar, 1, 0, HALF, 1, 2), (wk_out, 1, 0, 0)]
         vector = [(widen_on_vector, 0, 0, D, 0, 1), (widen_on_vector, 0, 0, QUARTER, 1, 2), (widen_on_vector, 0, 0, D, 2, 3), (widen_on_vector, 0, 0, QUARTER, 3, 4), (widen_on_vector, 0, QUARTER, HALF, 3, 4),
             (wv_on_vector, 0, 0, QUARTER), (wv_on_vector, 0, QUARTER, QUARTER), (quantize_wv, 0, 0, QUARTER), (quantize_wv, 0, QUARTER, QUARTER)] + [(normalize, i) for i in range(NT)]
-        vector += [(quantize_wk, 0, 1, 2), (quantize_hn, 0), (quantize_wv, 0, *U), (quantize_hn, 1), (widen_on_vector, 1, 0, HALF, 2, 3), (quantize_wk, 0, 0, 1), (quantize_hn, 2),
-                   (wk_on_vector, 1, 1), (quantize_hn, 3), (widen_on_vector, 1, 0, HALF, 3, 4), (quantize_wk, 1, 1, 2), (widen_on_vector, 2, 0, HALF, 1, 4), (wk_on_vector, 2, 1), (quantize_wk, 1, 0, 1)]
+        vector += [(quantize_wk, 0, 1, 2), (quantize_wv, 0, *U), (widen_on_vector, 1, 0, HALF, 2, 3), (quantize_hn, 0), (quantize_wk, 0, 0, 1),
+                   (wk_on_vector, 1, 1), (quantize_hn, 1), (widen_on_vector, 1, 0, HALF, 3, 4), (quantize_wk, 1, 1, 2), (widen_on_vector, 2, 0, HALF, 1, 4), (wk_on_vector, 2, 1), (quantize_wk, 1, 0, 1)]
         tensor += [(first_product, 0, 0), (first_product, 0, 1), (wk_on_tensor, 1, 0, 1), (first_product, 0, 2), (first_product, 0, 3), (wk_on_tensor, 2, 0, 0), (wk_on_tensor, 2, 0, 1)]
         scalar += [(rectify, 0, 0), (rectify, 0, 1), (widen_on_scalar, 2, 0, HALF, 0, 1), (wk_out, 1, 0, 1), (square, 0, 0), (rectify, 0, 2), (rectify, 0, 3), (wk_out, 2, 0, 0), (square, 0, 1), (wk_out, 2, 0, 1)]
         tensor += [(first_product, 1, 0), (first_product, 1, 1), (wv_on_tensor, 1, 0), (wk_on_tensor, 3, 0, 0), (first_product, 1, 2), (first_product, 1, 3), (wk_on_tensor, 3, 0, 1)] + slice0[:FIRST]
@@ -478,9 +475,9 @@ def tile_block_pc_kernel(tc, h_attn, norm2_w, ffn_wk, ffn_wv_bytes, ffn_wv_scale
         vector += lower(2)[1] + wk_step(2)[1] + lower(2)[2] + [(widen_on_vector, 3, 0, HALF, 0, 1), (quantize_k, 0, 0, 2)] + wk_step(2)[2]
         vector += wk_step(3)[0] + [(widen_on_vector, 3, 0, HALF, 1, 4)] + wk_step(3)[1] + lower(3)[1] + [(wv_on_vector, 1, QUARTER, QUARTER)] + wk_step(4)[0] + lower(1)[2] + [(quantize_k, 1, 0, 2)] + wk_step(3)[2]
         for g in (4, 5):
-            vector += lower(g)[0] + lower(g - 1)[2] + lower(g)[1] + wk_step(g)[1] + wk_step(g)[2] + wk_step(g + 1)[0] + [(quantize_k, g - 2, 0, 2)]
-        vector += [(widen_on_vector, 6, 0, D, 0, 2)] + lower(5)[2] + [(widen_on_vector, 6, 0, D, 2, 4)] + wk_step(6)[1] + wk_step(6)[2] + wk_step(7)[0] + [(quantize_k, 4, 0, 2)]
-        vector += [(wv_on_vector, 6, *U), (widen_on_vector, 7, 0, D, 0, 4), (quantize_wv, 6, *U)] + wk_step(7)[1] + wk_step(7)[2] + [(quantize_k, 5, 0, 2)]
+            vector += lower(g)[0] + lower(g - 1)[2] + lower(g)[1] + [(quantize_wk, g, 0, 2)] + wk_step(g + 1)[0] + [(quantize_k, g - 2, 0, 2)]
+        vector += [(widen_on_vector, 6, 0, D, 0, 2)] + lower(5)[2] + [(widen_on_vector, 6, 0, D, 2, 4)] + [(quantize_wk, 6, 0, 2)] + wk_step(7)[0] + [(quantize_k, 4, 0, 2)]
+        vector += [(wv_on_vector, 6, *U), (widen_on_vector, 7, 0, D, 0, 4), (quantize_wv, 6, *U)] + [(quantize_wk, 7, 0, 2)] + [(quantize_k, 5, 0, 2)]
         vector += [(widen_on_vector, 1, *U, 0, 4), (wv_on_vector, 7, *U), (wv_on_vector, 1, *U), (quantize_wv, 7, *U), (quantize_wv, 6, 0, HALF), (quantize_k, 6, 0, 2)]
         vector += [(widen_on_vector, 3, *U, 0, 4), (quantize_wv, 1, *U), (quantize_wv, 7, 0, HALF), (wv_on_vector, 3, *R), (quantize_k, 7, 0, 2), (wv_on_vector, 3, *L)]
         scalar += by_plane(widen_on_scalar, 4, *R, 0, 3)

@@ -348,12 +348,14 @@ def tile_block_pc_kernel(tc, h_attn, norm2_w, ffn_wk, ffn_wv_bytes, ffn_wv_scale
                 in_=buffer(("planes", "hn_grouped", a))[:],
             )
 
+        warm = keep.tile([P, 2], F32, align_bytes=64, name="warm")
+        nc.vector.memset(warm[:, 0:1], 1.0)
+        nc.scalar.activation(out=warm[:, 1:2], in_=warm[:, 0:1], func=ACT.Abs_reciprocal_sqrt)
+        nc.vector.memset(ident_bf16[:], 0.0)
         nc.vector.memset(ones[:], 1.0)
         nc.vector.memset(gain_row[:], 0.0)
-        make_identity(nc, ident_bf16[:])
-        make_identity(nc, ident_f32[:])
-        warm = keep.tile([P, 1], F32, align_bytes=64, name="warm")
-        nc.scalar.activation(out=warm[:], in_=ones[:, 0:1], func=ACT.Abs_reciprocal_sqrt)
+        make_identity(nc, ident_bf16[:], nomemset=True)
+        nc.scalar.copy(out=ident_f32[:], in_=ident_bf16[:])
 
         def cells(name, g, c0, w, *rest):
             return [(name, g, c) + rest for c in range(c0 // P, (c0 + w) // P)]
@@ -413,7 +415,7 @@ def tile_block_pc_kernel(tc, h_attn, norm2_w, ffn_wk, ffn_wv_bytes, ffn_wv_scale
             normalize: lambda i: ([("rstd", i), ("gain",)], [("hn", i)], [("acc", "gain"), ("result", "hn", i)]),
             turn_hn: lambda i: ([("hn", i)], [("hn_bank", i)], [("result", "hn", i), ("work", "hn", i)]),
             hn_out: lambda i: ([("hn_bank", i)], [("hn_grouped", i)], [("work", "hn", i), ("planes", "hn_grouped", i // 2)]),
-                        quantize_hn: lambda i: ([("hn_grouped", i)], [("hn_mx", i)], [("result", "hn_grouped", i)]),
+            quantize_hn: lambda a: ([("hn_grouped", 2 * a), ("hn_grouped", 2 * a + 1)], [("hn_mx", a)], [("planes", "hn_grouped", a)]),
         }
 
         def by_plane(job, g, c0, w, first=0, last=PACK):

from contextlib import ExitStack

import concourse.mybir as mybir
from concourse.masks import make_identity

S, D, FF = 512, 1024, 4096
EPS = 1e-5
FLOPS = 2 * 2 * S * D * FF

F32 = mybir.dt.float32
BF16 = mybir.dt.bfloat16
U32 = mybir.dt.uint32
U8 = mybir.dt.uint8
FP8 = mybir.dt.float8_e4m3fn
FP8X4 = mybir.dt.float8_e4m3fn_x4
ALU = mybir.AluOpType
ACT = mybir.ActivationFunctionType

P = 128
PACK = 4
K_PASS = P * PACK
NT = S // P
G = FF // K_PASS
Q = D // K_PASS
HALF = D // 2
QUARTER = D // 4
BANK = 512
RUN = 2

SLICES = ((0, HALF), (HALF, QUARTER), (HALF + QUARTER, QUARTER))
WHOLE = [(0, D)]
HALVES = [(0, HALF), (HALF, HALF)]
BY_SLICE = list(SLICES)
WIDENED = {g: WHOLE if g in (0, 6, 7) else HALVES if g in (1, 3) else BY_SLICE for g in range(G)}
QUANTIZED = {g: [(0, QUARTER), (QUARTER, QUARTER), (HALF, HALF)] if g == 0 else HALVES if g in (6, 7) else WIDENED[g] for g in range(G)}
LAG = 2
BANKS = ("acc", "work")
DEPTH = {"acc": 4, "work": 4, "wk_raw": 4, "grouped_wide": 2, "wk_codes": 3, "wk_scales": 3, "wv_bytes": 7, "planes_wide": 2, "planes": 5,
         "wv_grouped": 6, "relu": 2, "k_grouped": 2, "result": 5}
FIRST = 0
SPARE = ()


def tile_block_pc_kernel(tc, h_attn, norm2_w, ffn_wk, ffn_wv_bytes, ffn_wv_scale, out):
    nc = tc.nc
    h_v = h_attn.rearrange("b (i p) d -> (b i) p d", p=P)
    out_v = out.rearrange("b (i p) d -> p (b i) d", p=P)
    wk_v = ffn_wk.rearrange("(q p j) (g c) -> g q p j c", q=Q, p=P, j=PACK, c=K_PASS)
    wv_v = ffn_wv_bytes.rearrange("(g p t) n -> g p t n", p=P, t=PACK)
    scale_v = ffn_wv_scale.rearrange("(g p t) o -> p g (t o)", p=P, t=PACK)

    with ExitStack() as ctx:
        keep = ctx.enter_context(tc.tile_pool(name="keep", bufs=1))
        stream = ctx.enter_context(tc.tile_pool(name="stream", bufs=1))
        psum = ctx.enter_context(tc.psum_pool(name="psum", bufs=1))
        ctx.enter_context(tc.manual_schedule())

        h_sb = keep.tile([P, NT, D], BF16, align_bytes=64, name="h_sb")
        h_codes = keep.tile([P, 2, Q, 2 * P], U32, align_bytes=64, name="h_codes")
        h_scales = keep.tile([P, 2, Q, 2 * P], U8, align_bytes=64, name="h_scales")
        wv_scale = keep.tile([P, G, 2 * PACK], F32, align_bytes=64, name="wv_scale")
        wv_codes = keep.tile([P, G, D], U32, align_bytes=64, name="wv_codes")
        wv_scales = keep.tile([P, G, D], U8, align_bytes=64, name="wv_scales")
        k_codes = keep.tile([P, G, S], U32, align_bytes=64, name="k_codes")
        k_scales = keep.tile([P, G, S], U8, align_bytes=64, name="k_scales")
        gain_row = keep.tile([P, D], BF16, align_bytes=64, name="gain_row")
        ones = keep.tile([P, P], BF16, align_bytes=64, name="ones")
        ident_bf16 = keep.tile([P, P], BF16, align_bytes=64, name="ident_bf16")
        ident_f32 = keep.tile([P, P], F32, align_bytes=64, name="ident_f32")
        sumsq = keep.tile([P, NT], F32, align_bytes=64, name="sumsq")
        rstd = keep.tile([P, NT], F32, align_bytes=64, name="rstd")

        held, taken = {}, {}

        def buffer(key, shape=None, dtype=None):
            if key not in held:
                tag = key[0]
                turn = len(taken.setdefault(tag, []))
                taken[tag].append(key)
                if tag in BANKS:
                    held[key] = psum.tile(shape, dtype, name="%s%d" % (tag, turn % DEPTH[tag]))
                else:
                    held[key] = stream.tile(shape, dtype, align_bytes=64, name=tag, bufs=DEPTH[tag])
            return held[key]

        def covering(runs, g, c):
            return [(c0, w) for c0, w in runs[g] if c0 <= c < c0 + w][0]

        def planes_key(g, c):
            c0, w = covering(WIDENED, g, c)
            return ("planes_wide" if w > HALF else "planes", g, c0, w)

        def grouped_key(g, c):
            c0, w = covering(QUANTIZED, g, c)
            return ("grouped_wide" if w > HALF else "wv_grouped", g, c0, w)

        def acc_key(sl, i):
            return ("acc" if sl == 0 else "work", "sum", sl, i // (BANK // SLICES[sl][1]))

        def wk_bank_key(g, q, b):
            return ("acc" if (g, q, b) in SPARE else "work", "wk", g, q, b)

        def load_wk(g, q, b0, b1):
            raw = buffer(("wk_raw", g, q), [P, PACK, K_PASS], BF16)
            cols = slice(2 * P * b0, 2 * P * b1)
            nc.sync.dma_start(out=raw[:, :, cols], in_=wk_v[g, q][:, :, cols])

        def load_wv(g, first, last):
            raw = buffer(("wv_bytes", g), [P, PACK, D], U8)
            nc.sync.dma_start(out=raw[:, first:last, :], in_=wv_v[g][:, first:last, :])

        def load_scale(first, last):
            nc.sync.dma_start(out=wv_scale[:, first:last, 0:PACK], in_=scale_v[:, first:last, :])

        def load_gain():
            nc.sync.dma_start(out=gain_row[0:1, :], in_=norm2_w.rearrange("(o d) -> o d", o=1))

        def load_h(i):
            nc.sync.dma_start(out=h_sb[:, i, :], in_=h_v[i])

        def wk_grouped(g, q):
            return buffer(("grouped_wide", g), [P, Q * K_PASS * PACK], BF16)[:, q * K_PASS * PACK:(q + 1) * K_PASS * PACK]

        def wk_on_tensor(g, q, b, first=0, last=2):
            bank = buffer(wk_bank_key(g, q, b), [P, PACK, 64, PACK], BF16)
            for part in range(first, last):
                c0 = 2 * P * b + P * part
                nc.tensor.matmul(
                    bank[:, :, 32 * part:32 * part + 32, :].rearrange("p t m j -> p j m t"),
                    lhsT=ident_bf16[:],
                    rhs=buffer(("wk_raw", g, q))[:, :, c0:c0 + P].rearrange("p j (m t) -> p j m t", t=PACK),
                    start=True,
                    stop=True,
                )

        def wk_out(g, q, b):
            nc.scalar.copy(
                out=wk_grouped(g, q).bitcast(F32).rearrange("p (t w) -> p t w", t=PACK)[:, :, P * b:P * b + P],
                in_=buffer(wk_bank_key(g, q, b))[:].rearrange("p t m j -> p t (m j)").bitcast(F32),
            )

        def wk_on_vector(g, q, b0=0, b1=2):
            rows = slice(32 * b0, 32 * b1)
            nc.vector.tensor_copy(
                out=wk_grouped(g, q).rearrange("p (t m i j) -> p m t j i", t=PACK, i=RUN, j=PACK)[:, rows, :, :, :],
                in_=buffer(("wk_raw", g, q))[:].rearrange("p j (m i t) -> p m t j i", i=RUN, t=PACK)[:, rows, :, :, :],
            )

        def wk_on_gpsimd(g, q, b):
            nc.gpsimd.tensor_scalar(
                out=wk_grouped(g, q).rearrange("p (t m j) -> p t m j", t=PACK, j=PACK)[:, :, 64 * b:64 * b + 64, :],
                in0=buffer(("wk_raw", g, q))[:, :, 2 * P * b:2 * P * (b + 1)].rearrange("p j (m t) -> p t m j", t=PACK),
                scalar1=1.0, scalar2=0.0, op0=ALU.mult, op1=ALU.add)

        def wk_operand(g):
            return (buffer(("wk_codes", g), [P, Q * K_PASS], U32), buffer(("wk_scales", g), [P, Q * K_PASS], U8))

        def quantize_wk(g, q0, q1):
            codes, scales = wk_operand(g)
            nc.vector.quantize_mx(
                out=codes[:, q0 * K_PASS:q1 * K_PASS].bitcast(FP8X4),
                scales=scales[:, q0 * K_PASS:q1 * K_PASS],
                in_=buffer(("grouped_wide", g))[:, q0 * K_PASS * PACK:q1 * K_PASS * PACK],
            )

        def planes(g, c0, w):
            key = planes_key(g, c0)
            return buffer(key, [P, PACK, key[3]], BF16)[:, :, c0 - key[2]:c0 - key[2] + w]

        def grouped(g, c0, w):
            key = grouped_key(g, c0)
            return buffer(key, [P, key[3] * PACK], BF16)[:, (c0 - key[2]) * PACK:(c0 - key[2] + w) * PACK]

        def fp8_plane(g, c0, w, t):
            return buffer(("wv_bytes", g))[:, t, c0:c0 + w].bitcast(FP8)

        def widen_on_vector(g, c0, w, first, last):
            for t in range(first, last):
                nc.vector.tensor_scalar(
                    out=planes(g, c0, w)[:, t, :], in0=fp8_plane(g, c0, w, t), scalar1=wv_scale[:, g, t:t + 1],
                    scalar2=None, op0=ALU.mult)

        def widen_on_scalar(g, c0, w, first, last):
            for t in range(first, last):
                nc.scalar.activation(
                    out=planes(g, c0, w)[:, t, :], in_=fp8_plane(g, c0, w, t), func=ACT.Copy, scale=wv_scale[:, g, t:t + 1])

        def interleaving_views(g, c0, w):
            return (grouped(g, c0, w).rearrange("p (c i t) -> p c t i", i=RUN, t=PACK),
                    planes(g, c0, w).rearrange("p t (c i) -> p c t i", i=RUN))

        def wv_on_vector(g, c0, w):
            together, apart = interleaving_views(g, c0, w)
            nc.vector.tensor_copy(out=together, in_=apart)

        def wv_on_scalar(g, c0, w):
            together, apart = interleaving_views(g, c0, w)
            nc.scalar.copy(out=together, in_=apart)

        def wv_on_gpsimd(g, c0, w):
            nc.gpsimd.tensor_scalar(
                out=grouped(g, c0, w).rearrange("p (n t) -> p n t", t=PACK),
                in0=planes(g, c0, w).rearrange("p t n -> p n t"),
                scalar1=1.0, scalar2=0.0, op0=ALU.mult, op1=ALU.add)

        def wv_on_tensor(g, c0):
            bank = buffer(("work", "wv", g, c0), [P, QUARTER, PACK], BF16)
            for part in range(2):
                nc.tensor.matmul(
                    bank[:, P * part:P * part + P, :].rearrange("p n t -> p t n"),
                    lhsT=ident_bf16[:],
                    rhs=planes(g, c0 + P * part, P),
                    start=True,
                    stop=True,
                )

        def wv_out(g, c0):
            nc.scalar.copy(
                out=grouped(g, c0, QUARTER).bitcast(F32),
                in_=buffer(("work", "wv", g, c0))[:].rearrange("p n t -> p (n t)").bitcast(F32),
            )

        def quantize_wv(g, c0, w):
            nc.vector.quantize_mx(
                out=wv_codes[:, g, c0:c0 + w].bitcast(FP8X4), scales=wv_scales[:, g, c0:c0 + w], in_=grouped(g, c0, w))

        def first_product(g, i):
            a, u = divmod(i, 2)
            bank = buffer(("work", "hidden", g, i), [P, 2, 2 * P], F32)
            codes, scales = wk_operand(g)
            for e in range(2):
                for q in range(Q):
                    cols = slice(q * K_PASS + (2 * u + e) * P, q * K_PASS + (2 * u + e + 1) * P)
                    nc.tensor.matmul_mx(
                        out=bank[:, e, :],
                        lhsT=codes[:, cols].bitcast(FP8X4),
                        lhsT_scale=scales[:, cols],
                        rhs=h_codes[:, a, q, :].bitcast(FP8X4),
                        rhs_scale=h_scales[:, a, q, :],
                        start=(q == 0),
                        stop=(q == Q - 1),
                    )

        def rectify(g, i):
            a, u = divmod(i, 2)
            nc.scalar.activation(
                out=buffer(("relu", g, a), [P, 2, 2 * P, 2], F32)[:, u, :, :],
                in_=buffer(("work", "hidden", g, i))[:].rearrange("p e n -> p n e"), func=ACT.Relu)

        def square(g, a):
            nc.scalar.activation(
                out=buffer(("k_grouped", g), [P, 2, 2 * P, 2, 2], BF16)[:, a, :, :, :],
                in_=buffer(("relu", g, a))[:].rearrange("p u n e -> p n u e"), func=ACT.Square)

        def quantize_k(g, a0, a1):
            tokens = slice(2 * P * a0, 2 * P * a1)
            nc.vector.quantize_mx(
                out=k_codes[:, g, tokens].bitcast(FP8X4),
                scales=k_scales[:, g, tokens],
                in_=buffer(("k_grouped", g))[:, a0:a1, :, :, :].rearrange("p a n u e -> p (a n u e)"),
            )

        passes = {}

        def second_product(sl, g, first, last):
            c0, w = SLICES[sl]
            share = BANK // w
            for i in range(first, last):
                key = acc_key(sl, i)
                passes[key] = passes.get(key, 0) + 1
                nc.tensor.matmul_mx(
                    out=buffer(key, [P, share, w], F32)[:, i % share, :],
                    lhsT=k_codes[:, g, i * P:(i + 1) * P].bitcast(FP8X4),
                    lhsT_scale=k_scales[:, g, i * P:(i + 1) * P],
                    rhs=wv_codes[:, g, c0:c0 + w].bitcast(FP8X4),
                    rhs_scale=wv_scales[:, g, c0:c0 + w],
                    start=(passes[key] == 1),
                    stop=(passes[key] == G * share),
                )

        def result_key(sl, first):
            return ("relu", "result", sl) if sl > 0 else ("result", sl, first)

        def result(sl, first, last):
            if sl > 0:
                return buffer(result_key(sl, first), [P, NT, SLICES[sl][1]], F32)[:, first:last, :]
            return buffer(result_key(sl, first), [P, last - first, SLICES[sl][1]], F32)[:]

        def finish(sl, first, last):
            c0, w = SLICES[sl]
            share = BANK // w
            nc.vector.tensor_tensor(
                out=result(sl, first, last),
                in0=buffer(acc_key(sl, first))[:, first % share:first % share + last - first, :],
                in1=h_sb[:, first:last, c0:c0 + w], op=ALU.add)

        def store(sl, first, last):
            c0, w = SLICES[sl]
            nc.sync.dma_start(out=out_v[:, first:last, c0:c0 + w], in_=result(sl, first, last))

        def spread_gain():
            bank = buffer(("acc", "gain"), [P, D], BF16)
            for q in range(Q):
                cols = slice(q * K_PASS, (q + 1) * K_PASS)
                nc.tensor.matmul(bank[:, cols], lhsT=ones[:], rhs=gain_row[:, cols], start=True, stop=True)

        def sum_squares(i):
            squares = buffer(("k_grouped", "squares", i), [P, D], BF16)
            nc.scalar.activation(out=squares[:], in_=h_sb[:, i, :], func=ACT.Square, accum_out=sumsq[:, i:i + 1])

        def root(i):
            nc.scalar.activation(
                out=rstd[:, i:i + 1], in_=sumsq[:, i:i + 1], func=ACT.Abs_reciprocal_sqrt, scale=1.0 / D, bias=EPS)

        def normalize(i):
            hn = buffer(("result", "hn", i), [P, 2, HALF], BF16)
            for v in range(2):
                nc.vector.scalar_tensor_tensor(
                    out=hn[:, v, :].rearrange("p (m e) -> p m e", e=2),
                    in0=h_sb[:, i, :].rearrange("p (m v e) -> p v m e", v=2, e=2)[:, v, :, :],
                    scalar=rstd[:, i:i + 1],
                    in1=buffer(("acc", "gain"))[:].rearrange("p (m v e) -> p v m e", v=2, e=2)[:, v, :, :],
                    op0=ALU.mult, op1=ALU.mult)

        def turn_hn(i):
            bank = buffer(("work", "hn", i), [P, Q, 2, P], F32)
            for v in range(2):
                words = buffer(("result", "hn", i))[:, v, :].bitcast(F32)
                for q in range(Q):
                    nc.tensor.transpose(bank[:, q, v, :], words[:, q * P:(q + 1) * P], ident_f32[:])

        def hn_views(i):
            return (buffer(("planes", "hn_grouped", i // 2), [P, 2 * D], BF16)[:].bitcast(F32).rearrange("p (q i n v) -> p q i n v", q=Q, i=2, v=2)[:, :, i % 2, :, :],
                    buffer(("work", "hn", i))[:].rearrange("p q v n -> p q n v"))

        def hn_out(i):
            words, bank = hn_views(i)
            nc.scalar.copy(out=words, in_=bank)

        def hn_out_on_vector(i):
            words, bank = hn_views(i)
            nc.vector.tensor_copy(out=words, in_=bank)

        def quantize_hn(a):
            nc.vector.quantize_mx(
                out=h_codes[:, a, :, :].rearrange("p q n -> p (q n)").bitcast(FP8X4),
                scales=h_scales[:, a, :, :].rearrange("p q n -> p (q n)"),
                in_=buffer(("planes", "hn_grouped", a))[:],
            )

        warm = keep.tile([P, 2], F32, align_bytes=64, name="warm")
        nc.vector.memset(warm[:, 0:1], 1.0)
        nc.scalar.activation(out=warm[:, 1:2], in_=warm[:, 0:1], func=ACT.Abs_reciprocal_sqrt)
        nc.vector.memset(ident_bf16[:], 0.0)
        nc.vector.memset(ones[:], 1.0)
        nc.vector.memset(gain_row[:], 0.0)
        make_identity(nc, ident_bf16[:], nomemset=True)
        nc.scalar.copy(out=ident_f32[:], in_=ident_bf16[:])

        def cells(name, g, c0, w, *rest):
            return [(name, g, c) + rest for c in range(c0 // P, (c0 + w) // P)]

        def all_planes(g, c0, w):
            return [cell for t in range(PACK) for cell in cells("plane", g, c0, w, t)]

        def widening(g, c0, w, first, last):
            rows = range(first, last)
            return ([("scale", g)] + [("byte", g, t) for t in rows], [cell for t in rows for cell in cells("plane", g, c0, w, t)],
                    [("wv_bytes", g), planes_key(g, c0)])

        def interleaving(g, c0, w):
            return all_planes(g, c0, w), cells("grouped", g, c0, w), [planes_key(g, c0), grouped_key(g, c0)]

        flow = {
            load_wk: lambda g, q, b0, b1: ([], [("raw", g, q, b) for b in range(b0, b1)], [("wk_raw", g, q)]),
            load_wv: lambda g, first, last: ([], [("byte", g, t) for t in range(first, last)], [("wv_bytes", g)]),
            load_scale: lambda first, last: ([], [("scale", g) for g in range(first, last)], []),
            load_gain: lambda: ([], [("gain_row",)], []),
            load_h: lambda i: ([], [("h", i)], []),
            wk_on_tensor: lambda g, q, b, first=0, last=2: ([("raw", g, q, b)], [("wk_bank", g, q, b, part) for part in range(first, last)], [("wk_raw", g, q), wk_bank_key(g, q, b)]),
            wk_out: lambda g, q, b: ([("wk_bank", g, q, b, 0), ("wk_bank", g, q, b, 1)], [("wk", g, q, b)], [("grouped_wide", g), wk_bank_key(g, q, b)]),
            wk_on_gpsimd: lambda g, q, b: ([("raw", g, q, b)], [("wk", g, q, b)], [("wk_raw", g, q), ("grouped_wide", g)]),
            wk_on_vector: lambda g, q, b0=0, b1=2: (
                [("raw", g, q, b) for b in range(b0, b1)], [("wk", g, q, b) for b in range(b0, b1)], [("wk_raw", g, q), ("grouped_wide", g)]),
            quantize_wk: lambda g, q0, q1: (
                [("wk", g, q, b) for q in range(q0, q1) for b in range(2)], [("wk_mx", g, q) for q in range(q0, q1)],
                [("grouped_wide", g), ("wk_codes", g), ("wk_scales", g)]),
            widen_on_vector: widening,
            widen_on_scalar: widening,
            wv_on_vector: interleaving,
            wv_on_scalar: interleaving,
            wv_on_gpsimd: interleaving,
            wv_on_tensor: lambda g, c0: (
                all_planes(g, c0, QUARTER), [("wv_bank", g, c0)], [planes_key(g, c0), ("work", "wv", g, c0)]),
            wv_out: lambda g, c0: (
                [("wv_bank", g, c0)], cells("grouped", g, c0, QUARTER), [grouped_key(g, c0), ("work", "wv", g, c0)]),
            quantize_wv: lambda g, c0, w: (cells("grouped", g, c0, w), cells("wv_mx", g, c0, w), [grouped_key(g, c0)]),
            first_product: lambda g, i: (
                [("wk_mx", g, q) for q in range(Q)] + [("hn_mx", i // 2)], [("hidden", g, i)],
                [("wk_codes", g), ("wk_scales", g), ("work", "hidden", g, i)]),
            rectify: lambda g, i: ([("hidden", g, i)], [("relu", g, i)], [("work", "hidden", g, i), ("relu", g, i // 2)]),
            square: lambda g, a: ([("relu", g, 2 * a), ("relu", g, 2 * a + 1)], [("k", g, a)], [("relu", g, a), ("k_grouped", g)]),
            quantize_k: lambda g, a0, a1: (
                [("k", g, a) for a in range(a0, a1)], [("k_mx", g, a) for a in range(a0, a1)], [("k_grouped", g)]),
            second_product: lambda sl, g, first, last: (
                cells("wv_mx", g, *SLICES[sl]) + [("k_mx", g, i // 2) for i in range(first, last)],
                [("part",) + acc_key(sl, i) + (g, i) for i in range(first, last)], [acc_key(sl, i) for i in range(first, last)]),
            finish: lambda sl, first, last: (
                [("part",) + acc_key(sl, i) + (g, i) for g in range(G) for i in range(NT) if acc_key(sl, i) == acc_key(sl, first)],
                [("out", sl, first)], [acc_key(sl, first), result_key(sl, first)]),
            store: lambda sl, first, last: ([("out", sl, first)], [], [result_key(sl, first)]),
            spread_gain: lambda: ([("gain_row",)], [("gain",)], [("acc", "gain")]),
            sum_squares: lambda i: ([("h", i)], [("sum", i)], [("k_grouped", "squares", i)]),
            root: lambda i: ([("sum", i)], [("rstd", i)], []),
            normalize: lambda i: ([("rstd", i), ("gain",)], [("hn", i)], [("acc", "gain"), ("result", "hn", i)]),
            turn_hn: lambda i: ([("hn", i)], [("hn_bank", i)], [("result", "hn", i), ("work", "hn", i)]),
            hn_out: lambda i: ([("hn_bank", i)], [("hn_grouped", i)], [("work", "hn", i), ("planes", "hn_grouped", i // 2)]),
            quantize_hn: lambda a: ([("hn_grouped", 2 * a), ("hn_grouped", 2 * a + 1)], [("hn_mx", a)], [("planes", "hn_grouped", a)]),
        }

        def by_plane(job, g, c0, w, first=0, last=PACK):
            return [(job, g, c0, w, t, t + 1) for t in range(first, last)]

        def products(sl, groups):
            return [(second_product, sl, g, 0, NT) for g in groups]

        def wk_half(g, b, q=0):
            return [(wk_on_tensor, g, q, b)], [(wk_out, g, q, b)]

        def wv_quarter(g, c0):
            return [(wv_on_tensor, g, c0)], [(wv_out, g, c0)]

        def both(x, y):
            return x[0] + y[0], x[1] + y[1]

        def lower(g):
            return [(widen_on_vector, g, 0, HALF, 0, PACK)], [(wv_on_vector, g, 0, HALF)], [(quantize_wv, g, 0, HALF)]

        slice0 = [(second_product, 0, g, i, i + 1) for g in range(G) for i in range(NT)]
        R, L = SLICES[2], SLICES[1]

        U = (HALF, HALF)
        sync = [(load_scale, 0, 2), (load_wv, 0, 0, 1), (load_wv, 0, 1, 2), (load_wv, 0, 2, 3), (load_h, 0), (load_gain,), (load_wv, 0, 3, 4),
                (load_h, 1), (load_wk, 0, 1, 0, 1), (load_h, 2), (load_wk, 0, 1, 1, 2), (load_wv, 1, 0, 1), (load_h, 3), (load_wk, 0, 0, 0, 2), (load_wk, 1, 0, 0, 2), (load_wv, 1, 1, 4),
                (load_wk, 1, 1, 0, 2), (load_scale, 2, G)]
        for g in range(2, G):
            sync += [(load_wk, g, 0, 0, 2), (load_wv, g, 0, PACK), (load_wk, g, 1, 0, 2)]
        sync += [(store, 0, i, i + 1) for i in range(NT)] + [(store, sl, i, i + 1) for sl in (2, 1) for i in range(NT)]
        gpsimd = [(wv_on_gpsimd, 0, *U)]
        tensor = [(spread_gain,), (wk_on_tensor, 0, 1, 0), (wk_on_tensor, 0, 1, 1), (turn_hn, 0), (wk_on_tensor, 0, 0, 0), (turn_hn, 1), (wk_on_tensor, 0, 0, 1),
                  (turn_hn, 2), (turn_hn, 3), (wk_on_tensor, 1, 0, 0)]
        scalar = [(widen_on_scalar, 0, QUARTER, 3 * QUARTER, 1, 2), (sum_squares, 0), (sum_squares, 1), (root, 0), (widen_on_scalar, 0, 768, QUARTER, 3, 4), (root, 1),
                  (sum_squares, 2), (widen_on_scalar, 1, 0, QUARTER, 0, 1), (root, 2), (sum_squares, 3), (wk_out, 0, 1, 0), (root, 3), (wk_out, 0, 1, 1), (hn_out, 0), (wk_out, 0, 0, 0), (hn_out, 1),
                  (widen_on_scalar, 1, QUARTER, QUARTER, 0, 1), (wk_out, 0, 0, 1), (hn_out, 2), (hn_out, 3), (widen_on_scalar, 1, 0, HALF, 1, 2), (wk_out, 1, 0, 0)]
        vector = [(widen_on_vector, 0, 0, D, 0, 1), (widen_on_vector, 0, 0, QUARTER, 1, 2), (widen_on_vector, 0, 0, D, 2, 3), (widen_on_vector, 0, 0, QUARTER, 3, 4), (widen_on_vector, 0, QUARTER, HALF, 3, 4),
            (wv_on_vector, 0, 0, QUARTER), (wv_on_vector, 0, QUARTER, QUARTER), (quantize_wv, 0, 0, QUARTER), (quantize_wv, 0, QUARTER, QUARTER)] + [(normalize, i) for i in range(NT)]
        vector += [(quantize_wk, 0, 1, 2), (quantize_wv, 0, *U), (widen_on_vector, 1, 0, HALF, 2, 3), (quantize_hn, 0), (quantize_wk, 0, 0, 1),
                   (wk_on_vector, 1, 1), (quantize_hn, 1), (widen_on_vector, 1, 0, HALF, 3, 4), (quantize_wk, 1, 1, 2), (widen_on_vector, 2, 0, HALF, 1, 4), (wk_on_vector, 2, 1), (quantize_wk, 1, 0, 1)]
        tensor += [(first_product, 0, 0), (first_product, 0, 1), (wk_on_tensor, 1, 0, 1), (first_product, 0, 2), (first_product, 0, 3), (wk_on_tensor, 2, 0, 0), (wk_on_tensor, 2, 0, 1)]
        scalar += [(rectify, 0, 0), (rectify, 0, 1), (widen_on_scalar, 2, 0, HALF, 0, 1), (wk_out, 1, 0, 1), (square, 0, 0), (rectify, 0, 2), (rectify, 0, 3), (wk_out, 2, 0, 0), (square, 0, 1), (wk_out, 2, 0, 1)]
        tensor += [(first_product, 1, 0), (first_product, 1, 1), (wv_on_tensor, 1, 0), (wk_on_tensor, 3, 0, 0), (first_product, 1, 2), (first_product, 1, 3), (wk_on_tensor, 3, 0, 1)] + slice0[:FIRST]
        scalar += [(rectify, 1, 0), (rectify, 1, 1), (wv_out, 1, 0), (square, 1, 0), (wk_out, 3, 0, 0), (rectify, 1, 2), (rectify, 1, 3), (wk_out, 3, 0, 1), (square, 1, 1)]

        def paced(g):
            return NT * (g - 1) + FIRST - (g - 1) // LAG

        for g in range(2, G):
            slot = [wk_half(g + 2, b) if g + 2 < G else wv_quarter(g, QUARTER * b) for b in range(2)]
            for a in range(2):
                tensor += [(first_product, g, 2 * a), (first_product, g, 2 * a + 1)] + slot[a][0]
                scalar += [(rectify, g, 2 * a), (rectify, g, 2 * a + 1)] + slot[a][1] + [(square, g, a)]
            tensor += slice0[paced(g - 1):paced(g)]

        def wk_step(g):
            return [(wk_on_vector, g, 1)], [(quantize_wk, g, 1, 2)], [(quantize_wk, g, 0, 1)]

        vector += lower(2)[1] + wk_step(2)[1] + lower(2)[2] + [(widen_on_vector, 3, 0, HALF, 0, 1), (quantize_k, 0, 0, 2)] + wk_step(2)[2]
        vector += wk_step(3)[0] + [(widen_on_vector, 3, 0, HALF, 1, 4)] + wk_step(3)[1] + lower(3)[1] + [(wv_on_vector, 1, QUARTER, QUARTER)] + wk_step(4)[0] + lower(1)[2] + [(quantize_k, 1, 0, 2)] + wk_step(3)[2]
        for g in (4, 5):
            vector += lower(g)[0] + lower(g - 1)[2] + lower(g)[1] + [(quantize_wk, g, 0, 2)] + wk_step(g + 1)[0] + [(quantize_k, g - 2, 0, 2)]
        vector += [(widen_on_vector, 6, 0, D, 0, 2)] + lower(5)[2] + [(widen_on_vector, 6, 0, D, 2, 4)] + [(quantize_wk, 6, 0, 2)] + wk_step(7)[0] + [(quantize_k, 4, 0, 2)]
        vector += [(wv_on_vector, 6, *U), (widen_on_vector, 7, 0, D, 0, 4), (quantize_wv, 6, *U)] + [(quantize_wk, 7, 0, 2)] + [(quantize_k, 5, 0, 2)]
        vector += [(widen_on_vector, 1, *U, 0, 4), (wv_on_vector, 7, *U), (wv_on_vector, 1, *U), (quantize_wv, 7, *U), (quantize_wv, 6, 0, HALF), (quantize_k, 6, 0, 2)]
        vector += [(widen_on_vector, 3, *U, 0, 4), (quantize_wv, 1, *U), (quantize_wv, 7, 0, HALF), (wv_on_vector, 3, *R), (quantize_k, 7, 0, 2), (wv_on_vector, 3, *L)]
        scalar += by_plane(widen_on_scalar, 4, *R, 0, 3)
        for g, run in ((5, R), (2, R), (2, L), (5, L), (4, L)):
            scalar += by_plane(widen_on_scalar, g, *run)
        scalar += [(wv_on_scalar, 5, *L), (wv_on_scalar, 4, L[0], P)]
        gpsimd += [(wv_on_gpsimd, 4, *R)]
        tensor += slice0[paced(G - 1):-NT] + products(2, (0, 6, 1)) + slice0[-NT:] + products(2, (7, 3)) + products(1, (0, 6, 7, 1)) + products(2, (4,)) + products(1, (3,)) + products(2, (5, 2)) + products(1, (2,))
        tensor += [(second_product, 1, g, i, i + 2) for i in (0, 2) for g in (5, 4)]
        vector += [(widen_on_vector, 4, *R, 3, 4), (quantize_wv, 3, *U)] + [(finish, 0, i, i + 1) for i in range(NT)] + [
            (quantize_wv, 4, *R), (wv_on_vector, 5, *R), (wv_on_vector, 2, *R), (quantize_wv, 5, *R), (quantize_wv, 2, *R), (wv_on_vector, 2, *L),
            (wv_on_vector, 4, L[0] + P, P), (quantize_wv, 2, *L), (quantize_wv, 5, *L), (quantize_wv, 4, *L),
        ] + [(finish, sl, i, i + 1) for sl in (2, 1) for i in range(NT)]


        queues = [sync, tensor, scalar, vector, gpsimd]
        jobs = [job for queue in queues for job in queue]
        users = {}
        for job in jobs:
            for key in flow[job[0]](*job[1:])[2]:
                users.setdefault(key, []).append(job)
        at = [0] * len(queues)
        written, made = set(), set()

        def room(tag, wanted):
            busy = [any(user not in written for user in users[key]) for key in taken.get(tag, [])]
            if tag in BANKS:
                return not any(busy[:max(0, len(busy) + wanted - DEPTH[tag])])
            return sum(busy) + wanted <= DEPTH[tag]

        while len(written) < len(jobs):
            before = len(written)
            for e in range(len(queues)):
                if at[e] == len(queues[e]):
                    continue
                job = queues[e][at[e]]
                reads, makes, keys = flow[job[0]](*job[1:])
                fresh = {}
                for key in keys:
                    if key not in held and key not in fresh.setdefault(key[0], []):
                        fresh[key[0]].append(key)
                if all(name in made for name in reads) and all(room(tag, len(fresh[tag])) for tag in fresh):
                    job[0](*job[1:])
                    written.add(job)
                    for name in makes:
                        made.add(name)
                    at[e] += 1
            assert len(written) > before, "the lists wait for each other: %s" % [queues[e][at[e]:at[e] + 1] for e in range(len(queues))]
